import numpy as np
import ml_dtypes


def mxq(x, axis, fmt="e4m3"):
    dtype, down = {"e4m3": (ml_dtypes.float8_e4m3fn, 7), "e5m2": (ml_dtypes.float8_e5m2, 14)}[fmt]
    v = np.moveaxis(np.asarray(x, np.float32).astype(ml_dtypes.bfloat16).astype(np.float64), axis, -1)
    blocks = v.reshape(v.shape[:-1] + (-1, 32))
    amax = np.abs(blocks).max(-1, keepdims=True)
    byte = np.maximum(np.where(amax > 0, np.frexp(amax)[1] - 1 + 127, 0) - down, 1)
    scale = np.exp2(byte - 127.0)
    codes = (blocks / scale).astype(np.float32).astype(dtype).astype(np.float64)
    return np.moveaxis((codes * scale).reshape(v.shape), -1, axis)


WIDE = False


def mx_kscale(k):
    if not WIDE:
        return np.ones(k)
    levels = np.array([10, -10, 5, -5, 0])
    if k % 512:
        return np.exp2(np.random.permutation(np.resize(levels, k // 32))).repeat(32)
    a = np.empty((k // 512, 16))
    for p in range(k // 512):
        a[p, :8] = np.random.permutation(np.resize(levels, 8))
        for g in range(8):
            far = levels[np.abs(levels - a[p, g]) >= 10]
            a[p, g + 8] = far[np.random.randint(len(far))]
    return np.exp2(a.ravel()).repeat(32)


BF16 = ml_dtypes.bfloat16


def bf(x):
    return np.asarray(x, np.float32).astype(BF16)


def f64(x):
    return np.asarray(x).astype(np.float64)


B, S, D, H = 4, 128, 2048, 16
HD = D // H
THETA = 10000.0


def rope_tables():
    pos = np.arange(S, dtype=np.float64)
    inv_freq = THETA ** (-(np.arange(0, HD, 2, dtype=np.float64) / HD))
    freqs = pos[:, None] * inv_freq[None, :]
    return np.cos(freqs), np.sin(freqs)


def rope(t, cos, sin):
    t1 = t[..., 0::2]
    t2 = t[..., 1::2]
    r1 = t1 * cos - t2 * sin
    r2 = t1 * sin + t2 * cos
    return np.stack([r1, r2], axis=-1).reshape(t.shape)


def draw0():
    s = mx_kscale(D)
    return {"x": bf(np.random.standard_normal((B, S, D)) * s),
            "w_qk": bf(np.random.standard_normal((2 * D, D)) / np.sqrt(D) / s[None, :])}


def core(x, w_qk):
    qk = mxq(f64(x), 2, "e4m3") @ mxq(f64(w_qk), 1, "e4m3").T
    qk = qk.reshape(B, S, 2, H, HD).transpose(2, 3, 0, 1, 4)
    cos, sin = rope_tables()
    return rope(qk[0], cos, sin), rope(qk[1], cos, sin)


def e4m3fn_bytes(y):
    return np.clip(np.asarray(y, np.float64), -448.0, 448.0).astype(np.float32).astype(ml_dtypes.float8_e4m3fn).view(np.uint8)


def e4m3fn_values(b):
    return np.asarray(b, np.uint8).view(ml_dtypes.float8_e4m3fn).astype(np.float64)


def setup_inputs():
    d = draw0()
    x0 = np.asarray(d['w_qk']).astype(np.float64)
    s = (np.max(np.abs(x0), axis=(0,), keepdims=True) / 448.0).astype(np.float32)
    out = {}
    for k, v in d.items():
        if k == 'w_qk':
            out['w_qk_bytes'] = e4m3fn_bytes(x0 / s.astype(np.float64))
            out['w_qk_scale'] = s
        else:
            out[k] = v
    return out


def reference(x, w_qk_bytes, w_qk_scale):
    return core(x, e4m3fn_values(w_qk_bytes) * w_qk_scale.astype(np.float64))

@@ -1,0 +1,381 @@
+import math
+from contextlib import ExitStack
+
+import concourse.mybir as mybir
+from concourse.masks import make_identity
+
+F32 = mybir.dt.float32
+BF16 = mybir.dt.bfloat16
+U32 = mybir.dt.uint32
+U8 = mybir.dt.uint8
+I32 = mybir.dt.int32
+FP8 = mybir.dt.float8_e4m3fn
+FP8X4 = mybir.dt.float8_e4m3fn_x4
+ALU = mybir.AluOpType
+ACT = mybir.ActivationFunctionType
+
+B, S, D, H = 4, 128, 2048, 16
+HD = D // H
+FLOPS = 2 * B * S * D * 2 * D
+
+P = 128
+G = 4
+NPAIR = 16
+W2 = 256
+NBANK = NPAIR * G
+LAG = 4
+AHEAD = 5
+SCALAR_BANKS = (16, 24, 32, 40, 48, 56, 60, 62)
+SLEAD = 3
+BOTH_V = (7, 14)
+BOTH_G = ()
+DELAY = 2
+QDUMMY = (384, 384)
+PREWARM = 0
+LASTSPLIT = 1
+FILL = ()
+TAB_UNIT = 2
+CAST2_FIRST = 1
+CAST_G = 2
+CAST_LEAD = 3
+LOADS = (("x", 0), ("w", 1), ("x", 1))
+NEXTW = 2
+PQ_BUFS = 4
+GRP_BUFS = 4
+TS_BUFS = 6
+HEADDUMMY = 0
+
+V3, V2G1, SG3 = 0, 1, 2
+
+
+def rope_mode(p, h):
+    if p == NPAIR - 1:
+        return V3
+    if (h == 0 and p not in BOTH_V) or p in BOTH_G:
+        return SG3
+    return V2G1
+
+
+def tile_multiheadselfattention_pa_kernel(tc, x, w_qk_bytes, w_qk_scale, out_0, out_1):
+    nc = tc.nc
+    with ExitStack() as ctx:
+        const = ctx.enter_context(tc.tile_pool(name="const", bufs=1))
+        bytes_pool = ctx.enter_context(tc.tile_pool(name="bytes", bufs=NPAIR))
+        wide = ctx.enter_context(tc.tile_pool(name="wide", bufs=4))
+        work = ctx.enter_context(tc.tile_pool(name="work", bufs=4))
+        psum_t = ctx.enter_context(tc.psum_pool(name="psum_t", bufs=AHEAD))
+        psum_o = ctx.enter_context(tc.psum_pool(name="psum_o", bufs=3))
+        ctx.enter_context(tc.manual_schedule())
+
+        wby = []
+        xb = []
+
+        def load_w(i):
+            t = bytes_pool.tile([P, 2, D], U8, name="wby%d" % i, tag="wby")
+            nc.sync.dma_start(out=t[:], in_=w_qk_bytes[W2 * i:W2 * (i + 1), :].rearrange("(r p) k -> p r k", p=P))
+            wby.append(t)
+
+        def load_x(j):
+            t = const.tile([P, 2, D], BF16, name="xb%d" % j)
+            nc.sync.dma_start(out=t[:], in_=x[2 * j:2 * j + 2].rearrange("b s k -> s b k"))
+            xb.append(t)
+
+        load_w(0)
+        s_t = const.tile([P, G, 4], F32, name="s_t")
+        nc.sync.dma_start(out=s_t[:], in_=w_qk_scale.rearrange("o (g p t) -> p (o g) t", p=P, t=4))
+        for what, i in LOADS:
+            if what == "x":
+                load_x(i)
+            else:
+                load_w(i)
+        for i in range(NEXTW, NPAIR):
+            load_w(i)
+
+        dmy = const.tile([P, 512], BF16, name="dmy")
+        nc.gpsimd.memset(dmy[:], 0.0)
+        ident = const.tile([P, P], F32, name="ident")
+        make_identity(nc, ident[:])
+        pos_i = const.tile([P, 1], I32, name="pos_i")
+        nc.gpsimd.iota(out=pos_i[:], pattern=[[0, 1]], base=0, channel_multiplier=1)
+        pos_f = const.tile([P, 1], F32, name="pos_f")
+        nc.vector.tensor_copy(out=pos_f[:], in_=pos_i[:])
+        th = const.tile([P, HD // 2], F32, name="th")
+        nc.gpsimd.memset(th[:, 0:1], 1.0)
+        ratio = 10000.0 ** (-2.0 / HD)
+        for w in (1, 2, 4, 8, 16, 32):
+            nc.gpsimd.tensor_scalar(out=th[:, w:2 * w], in0=th[:, 0:w], scalar1=ratio ** w, scalar2=None, op0=ALU.mult)
+        turns = const.tile([P, HD // 2], F32, name="turns")
+        nc.gpsimd.tensor_scalar(out=turns[:], in0=th[:], scalar1=pos_f[:, 0:1], scalar2=1.0 / (2.0 * math.pi),
+                                op0=ALU.mult, op1=ALU.mult)
+        yy = const.tile([P, 2, HD // 2, 2], F32, name="yy")
+        for e in range(2):
+            nc.gpsimd.tensor_scalar(out=yy[:, 0, :, e], in0=turns[:], scalar1=0.25, scalar2=None, op0=ALU.add)
+            nc.gpsimd.tensor_copy(out=yy[:, 1, :, e], in_=turns[:])
+        yflat = yy[:].rearrange("p a j e -> p (a j e)")
+        whole = const.tile([P, 2 * HD], I32, name="whole")
+        frac = const.tile([P, 2 * HD], F32, name="frac")
+        over = const.tile([P, 2 * HD], F32, name="over")
+        frac2 = const.tile([P, 2, HD // 2, 2], F32, name="frac2")
+        cos4 = const.tile([P, 4, HD], F32, name="cos4")
+        sin4 = const.tile([P, 4, HD], F32, name="sin4")
+
+        def tables_vector():
+            nc.vector.tensor_copy(out=whole[:], in_=yflat)
+            nc.vector.tensor_tensor(out=frac[:], in0=yflat, in1=whole[:], op=ALU.subtract)
+
+        def tables_rest():
+            nc.gpsimd.tensor_scalar(out=over[:], in0=frac[:], scalar1=0.5, scalar2=None, op0=ALU.is_gt)
+            nc.gpsimd.tensor_tensor(out=frac2[:].rearrange("p a j e -> p (a j e)"), in0=frac[:], in1=over[:],
+                                    op=ALU.subtract)
+            nc.gpsimd.tensor_scalar(out=frac2[:, 1, :, 0], in0=frac2[:, 1, :, 0], scalar1=-1.0, scalar2=None,
+                                    op0=ALU.mult)
+            for a, dst in ((0, cos4), (1, sin4)):
+                nc.scalar.activation(out=dst[:],
+                                     in_=frac2[:, a].rearrange("p j e -> p (j e)").unsqueeze(1).to_broadcast([P, 4, HD]),
+                                     func=ACT.Sin, scale=2.0 * math.pi)
+
+        wb = {}
+        grp = {}
+        codes = {}
+        tps = {}
+
+        def dummy(bank, n):
+            nc.tensor.matmul(bank[:].rearrange("p a n -> p (a n)")[:, 0:n], lhsT=dmy[:, 0:P], rhs=dmy[:, 0:n],
+                             start=True, stop=True)
+
+        def cast(i, eng):
+            t = wide.tile([P, 2, D], BF16, name="wb%d" % i, tag="wb")
+            if eng == "v":
+                for r in range(2):
+                    nc.vector.tensor_copy(out=t[:, r, 0:D // 2], in_=wby[i][:, r, 0:D // 2].bitcast(FP8))
+                    nc.scalar.copy(out=t[:, r, D // 2:D], in_=wby[i][:, r, D // 2:D].bitcast(FP8))
+            else:
+                for r in range(2):
+                    nc.scalar.copy(out=t[:, r, :], in_=wby[i][:, r, :].bitcast(FP8))
+            wb[i] = t
+
+        def transposes(pool, tag, src, g, warm):
+            tp = pool.tile([P, 2, W2], F32, name=tag, tag=tag)
+            for n in range(warm):
+                dummy(tp, 512)
+            words = src[:].bitcast(F32)
+            for r in range(2):
+                for u in range(2):
+                    nc.tensor.transpose(tp[:, u, P * r:P * (r + 1)], words[:, r, 256 * g + u:256 * (g + 1):2], ident[:])
+            return tp
+
+        def t_bank(k, warm):
+            tps[k] = transposes(psum_t, "tp", wb[k // G], k % G, warm)
+
+        def new_group(key):
+            grp[key] = work.tile([P, G, W2, 4], BF16, name="grp", tag="grp", align_bytes=64, bufs=GRP_BUFS)
+
+        def scalar_out(k):
+            i, g = k // G, k % G
+            if i not in grp:
+                new_group(i)
+            pl = work.tile([P, 4, W2], BF16, name="pl", tag="pl", bufs=2)
+            src = tps[k][:].bitcast(BF16).rearrange("p u (n e) -> p u n e", e=2)
+            for t in range(4):
+                nc.scalar.activation(out=pl[:, t, :], in_=src[:, t // 2, :, t % 2], func=ACT.Copy,
+                                     scale=s_t[:, g, t:t + 1])
+            nc.scalar.copy(out=grp[i][:, g], in_=pl[:].rearrange("p t n -> p n t"))
+
+        def scale_out(k):
+            i, g = k // G, k % G
+            if i not in grp:
+                new_group(i)
+            nc.vector.tensor_tensor(
+                out=grp[i][:, g].rearrange("p n (u e) -> p n u e", e=2),
+                in0=tps[k][:].bitcast(BF16).rearrange("p u (n e) -> p n u e", e=2),
+                in1=s_t[:, g, :].rearrange("p (u e) -> p u e", e=2).unsqueeze(1).to_broadcast([P, W2, 2, 2]),
+                op=ALU.mult)
+
+        def copy_out(key, g, tp):
+            nc.vector.tensor_copy(
+                out=grp[key][:, g].rearrange("p n t -> p (n t)").bitcast(F32).rearrange("p (n u) -> p n u", u=2),
+                in_=tp[:].rearrange("p u n -> p n u"))
+
+        def quantize(key, pool, tagc, tags):
+            c = pool.tile([P, G, W2], U32, name=tagc, tag=tagc, align_bytes=64)
+            s = pool.tile([P, G, W2], U8, name=tags, tag=tags, align_bytes=64)
+            nc.vector.quantize_mx(out=c[:].rearrange("p g n -> p (g n)").bitcast(FP8X4),
+                                  scales=s[:].rearrange("p g n -> p (g n)"),
+                                  in_=grp[key][:].rearrange("p g n t -> p (g n t)"))
+            codes[key] = (c, s)
+
+        acc = {}
+        tsrc = {}
+        prod = {}
+        res = {}
+
+        def mm_group(m):
+            p, b = m // B, m % B
+            h, bb = b // 2, b % 2
+            if bb == 0:
+                acc[(p, h)] = psum_o.tile([P, 2, W2], F32, name="ot", tag="ot")
+                tsrc[(p, h)] = acc[(p, h)][:].rearrange("p b n -> p (b n)")
+            ot = acc[(p, h)]
+            if b == 0 and p < NPAIR - 1:
+                for n in QDUMMY:
+                    dummy(ot, n)
+            wc, ws = codes[p]
+            xc, xs = codes["x%d" % h]
+            for g in range(G):
+                nc.tensor.matmul_mx(out=ot[:, bb, :],
+                                    lhsT=xc[:, g, P * bb:P * (bb + 1)].bitcast(FP8X4),
+                                    lhsT_scale=xs[:, g, P * bb:P * (bb + 1)],
+                                    rhs=wc[:, g, :].bitcast(FP8X4),
+                                    rhs_scale=ws[:, g, :],
+                                    start=(g == 0), stop=(g == G - 1))
+
+        def rope_copy(p, h):
+            ts = work.tile([P, 2 * W2], F32, name="ts", tag="ts", bufs=TS_BUFS)
+            nc.scalar.copy(out=ts[:], in_=tsrc[(p, h)])
+            tsrc[(p, h)] = ts[:]
+
+        def rope_cos(eng, p, h):
+            pp = work.tile([P, 2 * W2], F32, name="pp", tag="pp", bufs=PQ_BUFS)
+            eng.tensor_tensor(out=pp[:], in0=tsrc[(p, h)], in1=cos4[:].rearrange("p a d -> p (a d)"), op=ALU.mult)
+            prod[(p, h, 0)] = pp
+
+        def rope_sin(eng, p, h):
+            qq = work.tile([P, 2 * W2], F32, name="qq", tag="qq", bufs=PQ_BUFS)
+            eng.tensor_tensor(out=qq[:].rearrange("p (m e) -> p m e", e=2),
+                              in0=tsrc[(p, h)].rearrange("p (m e) -> p m e", e=2)[:, :, ::-1],
+                              in1=sin4[:].rearrange("p a (j e) -> p (a j) e", e=2), op=ALU.mult)
+            prod[(p, h, 1)] = qq
+
+        def rope_add(eng, p, h):
+            if p not in res:
+                res[p] = work.tile([P, 2, B, HD], F32, name="rr", tag="rr")
+                first = True
+            else:
+                first = False
+            eng.tensor_tensor(out=res[p][:, :, 2 * h:2 * h + 2, :].rearrange("p h b d -> p b h d"),
+                              in0=prod[(p, h, 0)][:].rearrange("p (b h d) -> p b h d", b=2, h=2),
+                              in1=prod[(p, h, 1)][:].rearrange("p (b h d) -> p b h d", b=2, h=2), op=ALU.add)
+            dst = out_0 if p < NPAIR // 2 else out_1
+            h0 = 2 * (p % (NPAIR // 2))
+            if p >= NPAIR - LASTSPLIT:
+                for hh in range(2):
+                    nc.sync.dma_start(out=dst[h0 + hh, 2 * h:2 * h + 2].rearrange("b s d -> s b d"),
+                                      in_=res[p][:, hh, 2 * h:2 * h + 2, :])
+            elif not first:
+                nc.sync.dma_start(out=dst[h0:h0 + 2].rearrange("h b s d -> s (h b) d"),
+                                  in_=res[p][:].rearrange("p h b d -> p (h b) d"))
+
+        pending = []
+        taken = [0]
+
+        def waiting():
+            return len(pending) - taken[0]
+
+        def vector_piece():
+            what, p, h = pending[taken[0]]
+            taken[0] += 1
+            if what == 0:
+                rope_cos(nc.vector, p, h)
+            elif what == 1:
+                rope_sin(nc.vector, p, h)
+                if rope_mode(p, h) == V2G1:
+                    rope_add(nc.gpsimd, p, h)
+            else:
+                rope_add(nc.vector, p, h)
+
+        def by_scalar(k):
+            return k in SCALAR_BANKS
+
+        xts = {}
+        t_done = [0]
+
+        def x_bank(k):
+            xts[k] = transposes(psum_t, "tp", xb[k // G], k % G, 0)
+
+        def t_upto(last):
+            for k in range(t_done[0], min(last, NBANK - 1) + 1):
+                t_bank(k, 0)
+            t_done[0] = max(t_done[0], min(last, NBANK - 1) + 1)
+
+        plan = {}
+        for p in range(NPAIR):
+            for b in range(B):
+                plan.setdefault(G * p + LAG + b, []).append((p, b))
+        plan[LAG + 2].remove((0, 2))
+        plan[LAG + 3].remove((0, 3))
+        plan[2 * G].append((0, 2))
+        plan[2 * G + 1].append((0, 3))
+
+        cast(0, "v")
+        cast(1, "s")
+        t_upto(0)
+        x_bank(0)
+        t_upto(1)
+        x_bank(1)
+        t_upto(2)
+
+        ready = []
+        for k in range(NBANK + LAG):
+            i, g = k // G, k % G
+            if by_scalar(k + SLEAD):
+                scalar_out(k + SLEAD)
+            if k < NBANK and not by_scalar(k):
+                scale_out(k)
+            if g == 0 and 1 <= i <= NPAIR:
+                quantize(i - 1, work, "wc", "ws")
+            if k == 0 and CAST2_FIRST:
+                cast(2, "s")
+            if k == TAB_UNIT:
+                tables_vector()
+                tables_rest()
+                if not CAST2_FIRST:
+                    cast(2, "s")
+            if k == G:
+                quantize("x0", const, "xc0", "xs0")
+            if k == 2 * G:
+                quantize("x1", const, "xc1", "xs1")
+            if k < 2 * G:
+                if g == 0:
+                    new_group("x%d" % i)
+                copy_out("x%d" % i, g, xts[k])
+            for item in ready:
+                if item[0] + DELAY <= k or k >= NBANK:
+                    pending.extend(item[1])
+            ready = [item for item in ready if not (item[0] + DELAY <= k or k >= NBANK)]
+            if k >= NBANK:
+                for n in range(waiting()):
+                    vector_piece()
+            elif (g != 0 or by_scalar(k)) and waiting() > 0:
+                vector_piece()
+                if waiting() > 3:
+                    vector_piece()
+            if k + 2 < 2 * G:
+                x_bank(k + 2)
+                t_upto(k + 3)
+            elif k + 2 == 2 * G:
+                t_upto(k + AHEAD - 1)
+            else:
+                t_upto(k + AHEAD)
+            if k in FILL:
+                for n in range(2):
+                    dummy(tps[t_done[0] - 1], 512)
+            for p, b in plan.get(k, []):
+                mm_group(B * p + b)
+                if b % 2 == 1:
+                    h = b // 2
+                    mode = rope_mode(p, h)
+                    if mode == SG3:
+                        rope_copy(p, h)
+                        rope_cos(nc.gpsimd, p, h)
+                        rope_sin(nc.gpsimd, p, h)
+                        rope_add(nc.gpsimd, p, h)
+                    elif mode == V2G1:
+                        ready.append((k, [(0, p, h), (1, p, h)]))
+                    else:
+                        ready.append((k, [(0, p, h), (1, p, h), (2, p, h)]))
+            if g == CAST_G and 3 <= i + CAST_LEAD < NPAIR:
+                cast(i + CAST_LEAD, "s")
+        for item in ready:
+            pending.extend(item[1])
+        for n in range(waiting()):
+            vector_piece()

@@ -265,6 +265,12 @@ def tile_multiheadselfattention_pa_kernel(tc, x, w_qk_bytes, w_qk_scale, out_0, 
                 nc.sync.dma_start(out=dst[h0:h0 + 2].rearrange("h b s d -> s (h b) d"),
                                   in_=res[p][:].rearrange("p h b d -> p (h b) d"))
 
+        junk = const.tile([P, 1], U32, name="junk")
+        gq = []
+
+        def fence(key):
+            nc.gpsimd.tensor_copy(out=junk[:], in_=codes[key][0][:, 0, 0:1])
+
         pending = []
         taken = [0]
 
@@ -334,6 +340,13 @@ def tile_multiheadselfattention_pa_kernel(tc, x, w_qk_bytes, w_qk_scale, out_0, 
                 quantize("x0", const, "xc0", "xs0")
             if k == 2 * G:
                 quantize("x1", const, "xc1", "xs1")
+            if g == 0 and 1 <= i <= NPAIR:
+                fence("x0" if k == G else "x1" if k == 2 * G else i - 1)
+                for p, h in gq:
+                    rope_cos(nc.gpsimd, p, h)
+                    rope_sin(nc.gpsimd, p, h)
+                    rope_add(nc.gpsimd, p, h)
+                gq.clear()
             if k < 2 * G:
                 if g == 0:
                     new_group("x%d" % i)
@@ -366,9 +379,7 @@ def tile_multiheadselfattention_pa_kernel(tc, x, w_qk_bytes, w_qk_scale, out_0, 
                     mode = rope_mode(p, h)
                     if mode == SG3:
                         rope_copy(p, h)
-                        rope_cos(nc.gpsimd, p, h)
-                        rope_sin(nc.gpsimd, p, h)
-                        rope_add(nc.gpsimd, p, h)
+                        gq.append((p, h))
                     elif mode == V2G1:
                         ready.append((k, [(0, p, h), (1, p, h)]))
                     else:

@@ -27,7 +27,8 @@ LAG = 4
 AHEAD = 5
 SCALAR_BANKS = (16, 24, 32, 40, 48, 56, 60, 62)
 SLEAD = 3
-BOTH_V = (7, 14)
+BOTH_V = (14,)
+ADD_V = (3, 5, 7, 9, 11, 13)
 BOTH_G = ()
 DELAY = 2
 QDUMMY = (384, 384)
@@ -49,7 +50,7 @@ V3, V2G1, SG3 = 0, 1, 2
 
 
 def rope_mode(p, h):
-    if p == NPAIR - 1:
+    if p == NPAIR - 1 or (h == 1 and p in ADD_V):
         return V3
     if (h == 0 and p not in BOTH_V) or p in BOTH_G:
         return SG3
@@ -327,6 +328,8 @@ def tile_multiheadselfattention_pa_kernel(tc, x, w_qk_bytes, w_qk_scale, out_0, 
                 scalar_out(k + SLEAD)
             if k < NBANK and not by_scalar(k):
                 scale_out(k)
+            if g == 0 and waiting() > 0 and pending[taken[0]][0] == 2:
+                vector_piece()
             if g == 0 and 1 <= i <= NPAIR:
                 quantize(i - 1, work, "wc", "ws")
             if k == 0 and CAST2_FIRST:
@@ -358,9 +361,9 @@ def tile_multiheadselfattention_pa_kernel(tc, x, w_qk_bytes, w_qk_scale, out_0, 
             if k >= NBANK:
                 for n in range(waiting()):
                     vector_piece()
-            elif (g != 0 or by_scalar(k)) and waiting() > 0:
+            elif (g != 0 or by_scalar(k)) and waiting() > 0 and pending[taken[0]][0] != 2:
                 vector_piece()
-                if waiting() > 3:
+                if waiting() > 3 and pending[taken[0]][0] != 2:
                     vector_piece()
             if k + 2 < 2 * G:
                 x_bank(k + 2)

@@ -117,8 +117,7 @@ def tile_multiheadselfattention_pa_kernel(tc, x, w_qk_bytes, w_qk_scale, out_0, 
         frac = const.tile([P, 2 * HD], F32, name="frac")
         over = const.tile([P, 2 * HD], F32, name="over")
         frac2 = const.tile([P, 2, HD // 2, 2], F32, name="frac2")
-        cos4 = const.tile([P, 4, HD], F32, name="cos4")
-        sin4 = const.tile([P, 4, HD], F32, name="sin4")
+        tab = const.tile([P, 2, 4, HD], F32, name="tab")
 
         def tables_vector():
             nc.vector.tensor_copy(out=whole[:], in_=yflat)
@@ -128,10 +127,10 @@ def tile_multiheadselfattention_pa_kernel(tc, x, w_qk_bytes, w_qk_scale, out_0, 
             nc.gpsimd.tensor_scalar(out=over[:], in0=frac[:], scalar1=0.5, scalar2=None, op0=ALU.is_gt)
             nc.gpsimd.tensor_tensor(out=frac2[:].rearrange("p a j e -> p (a j e)"), in0=frac[:], in1=over[:],
                                     op=ALU.subtract)
-            nc.gpsimd.tensor_scalar(out=frac2[:, 1, :, 0], in0=frac2[:, 1, :, 0], scalar1=-1.0, scalar2=None,
+            nc.gpsimd.tensor_scalar(out=frac2[:, 1, :, 1], in0=frac2[:, 1, :, 1], scalar1=-1.0, scalar2=None,
                                     op0=ALU.mult)
-            for a, dst in ((0, cos4), (1, sin4)):
-                nc.scalar.activation(out=dst[:],
+            for a in range(2):
+                nc.scalar.activation(out=tab[:, a],
                                      in_=frac2[:, a].rearrange("p j e -> p (j e)").unsqueeze(1).to_broadcast([P, 4, HD]),
                                      func=ACT.Sin, scale=2.0 * math.pi)
 
@@ -235,36 +234,30 @@ def tile_multiheadselfattention_pa_kernel(tc, x, w_qk_bytes, w_qk_scale, out_0, 
             nc.scalar.copy(out=ts[:], in_=tsrc[(p, h)])
             tsrc[(p, h)] = ts[:]
 
-        def rope_cos(eng, p, h):
-            pp = work.tile([P, 2 * W2], F32, name="pp", tag="pp", bufs=PQ_BUFS)
-            eng.tensor_tensor(out=pp[:], in0=tsrc[(p, h)], in1=cos4[:].rearrange("p a d -> p (a d)"), op=ALU.mult)
-            prod[(p, h, 0)] = pp
-
-        def rope_sin(eng, p, h):
-            qq = work.tile([P, 2 * W2], F32, name="qq", tag="qq", bufs=PQ_BUFS)
-            eng.tensor_tensor(out=qq[:].rearrange("p (m e) -> p m e", e=2),
-                              in0=tsrc[(p, h)].rearrange("p (m e) -> p m e", e=2)[:, :, ::-1],
-                              in1=sin4[:].rearrange("p a (j e) -> p (a j) e", e=2), op=ALU.mult)
-            prod[(p, h, 1)] = qq
+        def rope_products(eng, p, h):
+            pq = work.tile([P, 2, 2 * W2], F32, name="pq", tag="pq", bufs=PQ_BUFS)
+            eng.tensor_tensor(out=pq[:], in0=tsrc[(p, h)].unsqueeze(1).to_broadcast([P, 2, 2 * W2]),
+                              in1=tab[:].rearrange("p a r d -> p a (r d)"), op=ALU.mult)
+            prod[(p, h)] = pq
 
         def rope_add(eng, p, h):
             if p not in res:
-                res[p] = work.tile([P, 2, B, HD], F32, name="rr", tag="rr")
+                res[p] = work.tile([P, B, 2, HD], F32, name="rr", tag="rr")
                 first = True
             else:
                 first = False
-            eng.tensor_tensor(out=res[p][:, :, 2 * h:2 * h + 2, :].rearrange("p h b d -> p b h d"),
-                              in0=prod[(p, h, 0)][:].rearrange("p (b h d) -> p b h d", b=2, h=2),
-                              in1=prod[(p, h, 1)][:].rearrange("p (b h d) -> p b h d", b=2, h=2), op=ALU.add)
+            eng.tensor_tensor(out=res[p][:, 2 * h:2 * h + 2].rearrange("p b h (j e) -> p (b h j) e", e=2),
+                              in0=prod[(p, h)][:, 0].rearrange("p (m e) -> p m e", e=2),
+                              in1=prod[(p, h)][:, 1].rearrange("p (m e) -> p m e", e=2)[:, :, ::-1], op=ALU.add)
             dst = out_0 if p < NPAIR // 2 else out_1
             h0 = 2 * (p % (NPAIR // 2))
             if p >= NPAIR - LASTSPLIT:
                 for hh in range(2):
                     nc.sync.dma_start(out=dst[h0 + hh, 2 * h:2 * h + 2].rearrange("b s d -> s b d"),
-                                      in_=res[p][:, hh, 2 * h:2 * h + 2, :])
+                                      in_=res[p][:, 2 * h:2 * h + 2, hh, :])
             elif not first:
-                nc.sync.dma_start(out=dst[h0:h0 + 2].rearrange("h b s d -> s (h b) d"),
-                                  in_=res[p][:].rearrange("p h b d -> p (h b) d"))
+                for hh in range(2):
+                    nc.sync.dma_start(out=dst[h0 + hh].rearrange("b s d -> s b d"), in_=res[p][:, :, hh, :])
 
         junk = const.tile([P, 1], U32, name="junk")
         gq = []
@@ -282,9 +275,7 @@ def tile_multiheadselfattention_pa_kernel(tc, x, w_qk_bytes, w_qk_scale, out_0, 
             what, p, h = pending[taken[0]]
             taken[0] += 1
             if what == 0:
-                rope_cos(nc.vector, p, h)
-            elif what == 1:
-                rope_sin(nc.vector, p, h)
+                rope_products(nc.vector, p, h)
                 if rope_mode(p, h) == V2G1:
                     rope_add(nc.gpsimd, p, h)
             else:
@@ -346,8 +337,7 @@ def tile_multiheadselfattention_pa_kernel(tc, x, w_qk_bytes, w_qk_scale, out_0, 
             if g == 0 and 1 <= i <= NPAIR:
                 fence("x0" if k == G else "x1" if k == 2 * G else i - 1)
                 for p, h in gq:
-                    rope_cos(nc.gpsimd, p, h)
-                    rope_sin(nc.gpsimd, p, h)
+                    rope_products(nc.gpsimd, p, h)
                     rope_add(nc.gpsimd, p, h)
                 gq.clear()
             if k < 2 * G:
@@ -363,7 +353,7 @@ def tile_multiheadselfattention_pa_kernel(tc, x, w_qk_bytes, w_qk_scale, out_0, 
                     vector_piece()
             elif (g != 0 or by_scalar(k)) and waiting() > 0 and pending[taken[0]][0] != 2:
                 vector_piece()
-                if waiting() > 3 and pending[taken[0]][0] != 2:
+                if waiting() > 1 and pending[taken[0]][0] != 2:
                     vector_piece()
             if k + 2 < 2 * G:
                 x_bank(k + 2)
@@ -384,9 +374,9 @@ def tile_multiheadselfattention_pa_kernel(tc, x, w_qk_bytes, w_qk_scale, out_0, 
                         rope_copy(p, h)
                         gq.append((p, h))
                     elif mode == V2G1:
-                        ready.append((k, [(0, p, h), (1, p, h)]))
+                        ready.append((k, [(0, p, h)]))
                     else:
-                        ready.append((k, [(0, p, h), (1, p, h), (2, p, h)]))
+                        ready.append((k, [(0, p, h), (2, p, h)]))
             if g == CAST_G and 3 <= i + CAST_LEAD < NPAIR:
                 cast(i + CAST_LEAD, "s")
         for item in ready:

@@ -22,6 +22,7 @@ P = 128
 G = 4
 NPAIR = 16
 W2 = 256
+KP = 512
 NBANK = NPAIR * G
 LAG = 4
 AHEAD = 5
@@ -43,7 +44,7 @@ LOADS = (("x", 0), ("w", 1), ("x", 1))
 NEXTW = 2
 PQ_BUFS = 4
 GRP_BUFS = 4
-TS_BUFS = 6
+TS_BUFS = 4
 HEADDUMMY = 0
 
 V3, V2G1, SG3 = 0, 1, 2
@@ -61,7 +62,7 @@ def tile_multiheadselfattention_pa_kernel(tc, x, w_qk_bytes, w_qk_scale, out_0, 
     nc = tc.nc
     with ExitStack() as ctx:
         const = ctx.enter_context(tc.tile_pool(name="const", bufs=1))
-        bytes_pool = ctx.enter_context(tc.tile_pool(name="bytes", bufs=NPAIR))
+        bytes_pool = ctx.enter_context(tc.tile_pool(name="bytes", bufs=NPAIR - 1))
         wide = ctx.enter_context(tc.tile_pool(name="wide", bufs=4))
         work = ctx.enter_context(tc.tile_pool(name="work", bufs=4))
         psum_t = ctx.enter_context(tc.psum_pool(name="psum_t", bufs=AHEAD))
@@ -81,17 +82,28 @@ def tile_multiheadselfattention_pa_kernel(tc, x, w_qk_bytes, w_qk_scale, out_0, 
             nc.sync.dma_start(out=t[:], in_=x[2 * j:2 * j + 2].rearrange("b s k -> s b k"))
             xb.append(t)
 
-        load_w(0)
+        wby0 = []
+        xb0 = []
         s_t = const.tile([P, G, 4], F32, name="s_t")
-        nc.sync.dma_start(out=s_t[:], in_=w_qk_scale.rearrange("o (g p t) -> p (o g) t", p=P, t=4))
-        for what, i in LOADS:
-            if what == "x":
-                load_x(i)
-            else:
-                load_w(i)
-        for i in range(NEXTW, NPAIR):
+        for g in range(G):
+            t = const.tile([P, 2, KP], U8, name="wby0_%d" % g)
+            nc.sync.dma_start(out=t[:], in_=w_qk_bytes[0:W2, KP * g:KP * (g + 1)].rearrange("(r p) k -> p r k", p=P))
+            wby0.append(t)
+            if g == 0:
+                nc.sync.dma_start(out=s_t[:], in_=w_qk_scale.rearrange("o (g p t) -> p (o g) t", p=P, t=4))
+            t = const.tile([P, 2, KP], BF16, name="xb0_%d" % g)
+            nc.sync.dma_start(out=t[:], in_=x[0:2, :, KP * g:KP * (g + 1)].rearrange("b s k -> s b k"))
+            xb0.append(t)
+        wby.append(None)
+        xb.append(None)
+        load_w(1)
+        load_x(1)
+        for i in range(2, NPAIR):
             load_w(i)
 
+        warm = const.tile([P, 2], F32, name="warm")
+        nc.gpsimd.memset(warm[:, 0:1], 0.0)
+        nc.scalar.activation(out=warm[:, 1:2], in_=warm[:, 0:1], func=ACT.Sin)
         dmy = const.tile([P, 512], BF16, name="dmy")
         nc.gpsimd.memset(dmy[:], 0.0)
         ident = const.tile([P, P], F32, name="ident")
@@ -143,15 +155,21 @@ def tile_multiheadselfattention_pa_kernel(tc, x, w_qk_bytes, w_qk_scale, out_0, 
             nc.tensor.matmul(bank[:].rearrange("p a n -> p (a n)")[:, 0:n], lhsT=dmy[:, 0:P], rhs=dmy[:, 0:n],
                              start=True, stop=True)
 
+        wb0 = {}
+
+        def cast0(g, eng):
+            t = const.tile([P, 2, KP], BF16, name="wb0_%d" % g)
+            src = wby0[g][:].rearrange("p r k -> p (r k)").bitcast(FP8)
+            if eng == "v":
+                nc.vector.tensor_copy(out=t[:].rearrange("p r k -> p (r k)"), in_=src)
+            else:
+                nc.scalar.copy(out=t[:].rearrange("p r k -> p (r k)"), in_=src)
+            wb0[g] = t
+
         def cast(i, eng):
             t = wide.tile([P, 2, D], BF16, name="wb%d" % i, tag="wb")
-            if eng == "v":
-                for r in range(2):
-                    nc.vector.tensor_copy(out=t[:, r, 0:D // 2], in_=wby[i][:, r, 0:D // 2].bitcast(FP8))
-                    nc.scalar.copy(out=t[:, r, D // 2:D], in_=wby[i][:, r, D // 2:D].bitcast(FP8))
-            else:
-                for r in range(2):
-                    nc.scalar.copy(out=t[:, r, :], in_=wby[i][:, r, :].bitcast(FP8))
+            for r in range(2):
+                nc.scalar.copy(out=t[:, r, :], in_=wby[i][:, r, :].bitcast(FP8))
             wb[i] = t
 
         def transposes(pool, tag, src, g, warm):
@@ -165,7 +183,10 @@ def tile_multiheadselfattention_pa_kernel(tc, x, w_qk_bytes, w_qk_scale, out_0, 
             return tp
 
         def t_bank(k, warm):
-            tps[k] = transposes(psum_t, "tp", wb[k // G], k % G, warm)
+            if k < G:
+                tps[k] = transposes(psum_t, "tp", wb0[k], 0, warm)
+            else:
+                tps[k] = transposes(psum_t, "tp", wb[k // G], k % G, warm)
 
         def new_group(key):
             grp[key] = work.tile([P, G, W2, 4], BF16, name="grp", tag="grp", align_bytes=64, bufs=GRP_BUFS)
@@ -288,7 +309,10 @@ def tile_multiheadselfattention_pa_kernel(tc, x, w_qk_bytes, w_qk_scale, out_0, 
         t_done = [0]
 
         def x_bank(k):
-            xts[k] = transposes(psum_t, "tp", xb[k // G], k % G, 0)
+            if k < G:
+                xts[k] = transposes(psum_t, "tp", xb0[k], 0, 0)
+            else:
+                xts[k] = transposes(psum_t, "tp", xb[k // G], k % G, 0)
 
         def t_upto(last):
             for k in range(t_done[0], min(last, NBANK - 1) + 1):
@@ -304,13 +328,14 @@ def tile_multiheadselfattention_pa_kernel(tc, x, w_qk_bytes, w_qk_scale, out_0, 
         plan[2 * G].append((0, 2))
         plan[2 * G + 1].append((0, 3))
 
-        cast(0, "v")
+        cast0(0, "v")
+        cast0(1, "s")
+        cast0(3, "s")
         cast(1, "s")
         t_upto(0)
         x_bank(0)
         t_upto(1)
         x_bank(1)
-        t_upto(2)
 
         ready = []
         for k in range(NBANK + LAG):
@@ -323,6 +348,9 @@ def tile_multiheadselfattention_pa_kernel(tc, x, w_qk_bytes, w_qk_scale, out_0, 
                 vector_piece()
             if g == 0 and 1 <= i <= NPAIR:
                 quantize(i - 1, work, "wc", "ws")
+            if k == 0:
+                cast0(2, "v")
+                t_upto(2)
             if k == 0 and CAST2_FIRST:
                 cast(2, "s")
             if k == TAB_UNIT:

@@ -26,10 +26,10 @@ KP = 512
 NBANK = NPAIR * G
 LAG = 4
 AHEAD = 5
-SCALAR_BANKS = (16, 24, 32, 40, 48, 56, 60, 62)
+SCALAR_BANKS = (16, 24, 32, 40, 48, 56, 60, 62, 63)
 SLEAD = 3
-BOTH_V = (14,)
-ADD_V = (3, 5, 7, 9, 11, 13)
+BOTH_V = (13, 14)
+ADD_V = (1, 3, 5, 7, 9, 11, 12, 13)
 BOTH_G = ()
 DELAY = 2
 QDUMMY = (384, 384)

@@ -32,7 +32,7 @@ BOTH_V = (13, 14)
 ADD_V = (1, 3, 5, 7, 9, 11, 12, 13)
 BOTH_G = ()
 DELAY = 2
-QDUMMY = (384, 384)
+QDUMMY = ()
 PREWARM = 0
 LASTSPLIT = 1
 FILL = ()

@@ -19,395 +19,370 @@ HD = D // H
 FLOPS = 2 * B * S * D * 2 * D
 
 P = 128
-G = 4
-NPAIR = 16
-W2 = 256
-KP = 512
-NBANK = NPAIR * G
-LAG = 4
-AHEAD = 5
-SCALAR_BANKS = (16, 24, 32, 40, 48, 56, 60, 62, 63)
-SLEAD = 3
-BOTH_V = (13, 14)
-ADD_V = (1, 3, 5, 7, 9, 11, 12, 13)
-BOTH_G = ()
-DELAY = 2
-QDUMMY = ()
-PREWARM = 0
-LASTSPLIT = 1
-FILL = ()
-TAB_UNIT = 2
-CAST2_FIRST = 1
-CAST_G = 2
-CAST_LEAD = 3
-LOADS = (("x", 0), ("w", 1), ("x", 1))
-NEXTW = 2
-PQ_BUFS = 4
-GRP_BUFS = 4
-TS_BUFS = 4
-HEADDUMMY = 0
+PACK = 4
+K_PASS = P * PACK
+PASSES = D // K_PASS
+PAIR_ROWS = 2 * HD
+PAIRS = 2 * D // PAIR_ROWS
+BANKS = PAIRS * PASSES
+X_BANKS = 2 * PASSES
 
-V3, V2G1, SG3 = 0, 1, 2
+TRANSPOSE_BANKS = 5
+SUM_BANKS = 3
+CAST_AHEAD = 3
+SCALAR_AHEAD = 3
+PRODUCT_LAG = 2
+
+BY_VECTOR = 0
+SUM_ON_GPSIMD = 1
+BY_GPSIMD = 2
 
 
-def rope_mode(p, h):
-    if p == NPAIR - 1 or (h == 1 and p in ADD_V):
-        return V3
-    if (h == 0 and p not in BOTH_V) or p in BOTH_G:
-        return SG3
-    return V2G1
+def by_scalar(k):
+    pair, g = divmod(k, PASSES)
+    if pair >= PAIRS:
+        return False
+    if pair == PAIRS - 1:
+        return g != 1
+    return g == 0 and pair >= 4 and pair % 2 == 0
+
+
+def rope_way(pair, half):
+    if pair == PAIRS - 1:
+        return BY_VECTOR
+    if half == 1 and any(by_scalar(k) for k in range(PASSES * (pair + 2) + 1, PASSES * (pair + 3) + 1)):
+        return BY_VECTOR
+    if half == 0 and pair < PAIRS - 3:
+        return BY_GPSIMD
+    return SUM_ON_GPSIMD
 
 
 def tile_multiheadselfattention_pa_kernel(tc, x, w_qk_bytes, w_qk_scale, out_0, out_1):
     nc = tc.nc
     with ExitStack() as ctx:
         const = ctx.enter_context(tc.tile_pool(name="const", bufs=1))
-        bytes_pool = ctx.enter_context(tc.tile_pool(name="bytes", bufs=NPAIR - 1))
-        wide = ctx.enter_context(tc.tile_pool(name="wide", bufs=4))
+        bytes_pool = ctx.enter_context(tc.tile_pool(name="bytes", bufs=PAIRS - 1))
+        wide = ctx.enter_context(tc.tile_pool(name="wide", bufs=CAST_AHEAD + 1))
         work = ctx.enter_context(tc.tile_pool(name="work", bufs=4))
-        psum_t = ctx.enter_context(tc.psum_pool(name="psum_t", bufs=AHEAD))
-        psum_o = ctx.enter_context(tc.psum_pool(name="psum_o", bufs=3))
+        psum_t = ctx.enter_context(tc.psum_pool(name="psum_t", bufs=TRANSPOSE_BANKS))
+        psum_o = ctx.enter_context(tc.psum_pool(name="psum_o", bufs=SUM_BANKS))
         ctx.enter_context(tc.manual_schedule())
 
-        wby = []
-        xb = []
-
-        def load_w(i):
-            t = bytes_pool.tile([P, 2, D], U8, name="wby%d" % i, tag="wby")
-            nc.sync.dma_start(out=t[:], in_=w_qk_bytes[W2 * i:W2 * (i + 1), :].rearrange("(r p) k -> p r k", p=P))
-            wby.append(t)
-
-        def load_x(j):
-            t = const.tile([P, 2, D], BF16, name="xb%d" % j)
-            nc.sync.dma_start(out=t[:], in_=x[2 * j:2 * j + 2].rearrange("b s k -> s b k"))
-            xb.append(t)
-
-        wby0 = []
-        xb0 = []
-        s_t = const.tile([P, G, 4], F32, name="s_t")
-        for g in range(G):
-            t = const.tile([P, 2, KP], U8, name="wby0_%d" % g)
-            nc.sync.dma_start(out=t[:], in_=w_qk_bytes[0:W2, KP * g:KP * (g + 1)].rearrange("(r p) k -> p r k", p=P))
-            wby0.append(t)
+        first_bytes = []
+        first_x = []
+        scale = const.tile([P, PASSES, PACK], F32, name="scale")
+        for g in range(PASSES):
+            k_cols = slice(K_PASS * g, K_PASS * (g + 1))
+            t = const.tile([P, 2, K_PASS], U8, name="first_bytes%d" % g)
+            nc.sync.dma_start(out=t[:], in_=w_qk_bytes[0:PAIR_ROWS, k_cols].rearrange("(r p) k -> p r k", p=P))
+            first_bytes.append(t)
             if g == 0:
-                nc.sync.dma_start(out=s_t[:], in_=w_qk_scale.rearrange("o (g p t) -> p (o g) t", p=P, t=4))
-            t = const.tile([P, 2, KP], BF16, name="xb0_%d" % g)
-            nc.sync.dma_start(out=t[:], in_=x[0:2, :, KP * g:KP * (g + 1)].rearrange("b s k -> s b k"))
-            xb0.append(t)
-        wby.append(None)
-        xb.append(None)
-        load_w(1)
-        load_x(1)
-        for i in range(2, NPAIR):
-            load_w(i)
+                nc.sync.dma_start(out=scale[:], in_=w_qk_scale.rearrange("o (g p t) -> p (o g) t", p=P, t=PACK))
+            t = const.tile([P, 2, K_PASS], BF16, name="first_x%d" % g)
+            nc.sync.dma_start(out=t[:], in_=x[0:2, :, k_cols].rearrange("b s k -> s b k"))
+            first_x.append(t)
+
+        pair_bytes = {}
+
+        def load_pair(i):
+            t = bytes_pool.tile([P, 2, D], U8, name="pair_bytes%d" % i, tag="pair_bytes")
+            nc.sync.dma_start(out=t[:],
+                              in_=w_qk_bytes[PAIR_ROWS * i:PAIR_ROWS * (i + 1), :].rearrange("(r p) k -> p r k", p=P))
+            pair_bytes[i] = t
+
+        load_pair(1)
+        second_x = const.tile([P, 2, D], BF16, name="second_x")
+        nc.sync.dma_start(out=second_x[:], in_=x[2:4].rearrange("b s k -> s b k"))
+        for i in range(2, PAIRS):
+            load_pair(i)
 
         warm = const.tile([P, 2], F32, name="warm")
         nc.gpsimd.memset(warm[:, 0:1], 0.0)
         nc.scalar.activation(out=warm[:, 1:2], in_=warm[:, 0:1], func=ACT.Sin)
-        dmy = const.tile([P, 512], BF16, name="dmy")
-        nc.gpsimd.memset(dmy[:], 0.0)
         ident = const.tile([P, P], F32, name="ident")
         make_identity(nc, ident[:])
+
         pos_i = const.tile([P, 1], I32, name="pos_i")
         nc.gpsimd.iota(out=pos_i[:], pattern=[[0, 1]], base=0, channel_multiplier=1)
         pos_f = const.tile([P, 1], F32, name="pos_f")
         nc.vector.tensor_copy(out=pos_f[:], in_=pos_i[:])
-        th = const.tile([P, HD // 2], F32, name="th")
-        nc.gpsimd.memset(th[:, 0:1], 1.0)
+        power = const.tile([P, HD // 2], F32, name="power")
+        nc.gpsimd.memset(power[:, 0:1], 1.0)
         ratio = 10000.0 ** (-2.0 / HD)
         for w in (1, 2, 4, 8, 16, 32):
-            nc.gpsimd.tensor_scalar(out=th[:, w:2 * w], in0=th[:, 0:w], scalar1=ratio ** w, scalar2=None, op0=ALU.mult)
+            nc.gpsimd.tensor_scalar(out=power[:, w:2 * w], in0=power[:, 0:w], scalar1=ratio ** w, scalar2=None,
+                                    op0=ALU.mult)
         turns = const.tile([P, HD // 2], F32, name="turns")
-        nc.gpsimd.tensor_scalar(out=turns[:], in0=th[:], scalar1=pos_f[:, 0:1], scalar2=1.0 / (2.0 * math.pi),
+        nc.gpsimd.tensor_scalar(out=turns[:], in0=power[:], scalar1=pos_f[:, 0:1], scalar2=1.0 / (2.0 * math.pi),
                                 op0=ALU.mult, op1=ALU.mult)
-        yy = const.tile([P, 2, HD // 2, 2], F32, name="yy")
+        arg = const.tile([P, 2, HD // 2, 2], F32, name="arg")
         for e in range(2):
-            nc.gpsimd.tensor_scalar(out=yy[:, 0, :, e], in0=turns[:], scalar1=0.25, scalar2=None, op0=ALU.add)
-            nc.gpsimd.tensor_copy(out=yy[:, 1, :, e], in_=turns[:])
-        yflat = yy[:].rearrange("p a j e -> p (a j e)")
+            nc.gpsimd.tensor_scalar(out=arg[:, 0, :, e], in0=turns[:], scalar1=0.25, scalar2=None, op0=ALU.add)
+            nc.gpsimd.tensor_copy(out=arg[:, 1, :, e], in_=turns[:])
+        arg_flat = arg[:].rearrange("p a j e -> p (a j e)")
         whole = const.tile([P, 2 * HD], I32, name="whole")
         frac = const.tile([P, 2 * HD], F32, name="frac")
         over = const.tile([P, 2 * HD], F32, name="over")
-        frac2 = const.tile([P, 2, HD // 2, 2], F32, name="frac2")
-        tab = const.tile([P, 2, 4, HD], F32, name="tab")
+        near = const.tile([P, 2, HD // 2, 2], F32, name="near")
+        table = const.tile([P, 2, 4, HD], F32, name="table")
 
-        def tables_vector():
-            nc.vector.tensor_copy(out=whole[:], in_=yflat)
-            nc.vector.tensor_tensor(out=frac[:], in0=yflat, in1=whole[:], op=ALU.subtract)
-
-        def tables_rest():
+        def make_table():
+            nc.vector.tensor_copy(out=whole[:], in_=arg_flat)
+            nc.vector.tensor_tensor(out=frac[:], in0=arg_flat, in1=whole[:], op=ALU.subtract)
             nc.gpsimd.tensor_scalar(out=over[:], in0=frac[:], scalar1=0.5, scalar2=None, op0=ALU.is_gt)
-            nc.gpsimd.tensor_tensor(out=frac2[:].rearrange("p a j e -> p (a j e)"), in0=frac[:], in1=over[:],
+            nc.gpsimd.tensor_tensor(out=near[:].rearrange("p a j e -> p (a j e)"), in0=frac[:], in1=over[:],
                                     op=ALU.subtract)
-            nc.gpsimd.tensor_scalar(out=frac2[:, 1, :, 1], in0=frac2[:, 1, :, 1], scalar1=-1.0, scalar2=None,
+            nc.gpsimd.tensor_scalar(out=near[:, 1, :, 1], in0=near[:, 1, :, 1], scalar1=-1.0, scalar2=None,
                                     op0=ALU.mult)
             for a in range(2):
-                nc.scalar.activation(out=tab[:, a],
-                                     in_=frac2[:, a].rearrange("p j e -> p (j e)").unsqueeze(1).to_broadcast([P, 4, HD]),
+                nc.scalar.activation(out=table[:, a],
+                                     in_=near[:, a].rearrange("p j e -> p (j e)").unsqueeze(1).to_broadcast([P, 4, HD]),
                                      func=ACT.Sin, scale=2.0 * math.pi)
 
-        wb = {}
-        grp = {}
+        first_wide = {}
+        pair_wide = {}
+        w_bank = {}
+        x_bank = {}
+        grouped = {}
         codes = {}
-        tps = {}
 
-        def dummy(bank, n):
-            nc.tensor.matmul(bank[:].rearrange("p a n -> p (a n)")[:, 0:n], lhsT=dmy[:, 0:P], rhs=dmy[:, 0:n],
-                             start=True, stop=True)
+        def cast_first(g, copy):
+            t = const.tile([P, 2, K_PASS], BF16, name="first_wide%d" % g)
+            copy(out=t[:].rearrange("p r k -> p (r k)"),
+                 in_=first_bytes[g][:].rearrange("p r k -> p (r k)").bitcast(FP8))
+            first_wide[g] = t
 
-        wb0 = {}
-
-        def cast0(g, eng):
-            t = const.tile([P, 2, KP], BF16, name="wb0_%d" % g)
-            src = wby0[g][:].rearrange("p r k -> p (r k)").bitcast(FP8)
-            if eng == "v":
-                nc.vector.tensor_copy(out=t[:].rearrange("p r k -> p (r k)"), in_=src)
-            else:
-                nc.scalar.copy(out=t[:].rearrange("p r k -> p (r k)"), in_=src)
-            wb0[g] = t
-
-        def cast(i, eng):
-            t = wide.tile([P, 2, D], BF16, name="wb%d" % i, tag="wb")
+        def cast_pair(i):
+            t = wide.tile([P, 2, D], BF16, name="pair_wide%d" % i, tag="pair_wide")
             for r in range(2):
-                nc.scalar.copy(out=t[:, r, :], in_=wby[i][:, r, :].bitcast(FP8))
-            wb[i] = t
+                nc.scalar.copy(out=t[:, r, :], in_=pair_bytes[i][:, r, :].bitcast(FP8))
+            pair_wide[i] = t
 
-        def transposes(pool, tag, src, g, warm):
-            tp = pool.tile([P, 2, W2], F32, name=tag, tag=tag)
-            for n in range(warm):
-                dummy(tp, 512)
+        def transposes(src, g):
+            bank = psum_t.tile([P, 2, PAIR_ROWS], F32, name="bank", tag="bank")
             words = src[:].bitcast(F32)
             for r in range(2):
                 for u in range(2):
-                    nc.tensor.transpose(tp[:, u, P * r:P * (r + 1)], words[:, r, 256 * g + u:256 * (g + 1):2], ident[:])
-            return tp
+                    nc.tensor.transpose(bank[:, u, P * r:P * (r + 1)],
+                                        words[:, r, K_PASS // 2 * g + u:K_PASS // 2 * (g + 1):2], ident[:])
+            return bank
 
-        def t_bank(k, warm):
-            if k < G:
-                tps[k] = transposes(psum_t, "tp", wb0[k], 0, warm)
+        w_banks_done = [0]
+
+        def transpose_weights_upto(last):
+            for k in range(w_banks_done[0], min(last, BANKS - 1) + 1):
+                if k < PASSES:
+                    w_bank[k] = transposes(first_wide[k], 0)
+                else:
+                    w_bank[k] = transposes(pair_wide[k // PASSES], k % PASSES)
+            w_banks_done[0] = max(w_banks_done[0], min(last, BANKS - 1) + 1)
+
+        def transpose_x(k):
+            if k < PASSES:
+                x_bank[k] = transposes(first_x[k], 0)
             else:
-                tps[k] = transposes(psum_t, "tp", wb[k // G], k % G, warm)
+                x_bank[k] = transposes(second_x, k % PASSES)
 
-        def new_group(key):
-            grp[key] = work.tile([P, G, W2, 4], BF16, name="grp", tag="grp", align_bytes=64, bufs=GRP_BUFS)
+        def new_grouped(key):
+            grouped[key] = work.tile([P, PASSES, PAIR_ROWS, PACK], BF16, name="grouped", tag="grouped", align_bytes=64)
 
-        def scalar_out(k):
-            i, g = k // G, k % G
-            if i not in grp:
-                new_group(i)
-            pl = work.tile([P, 4, W2], BF16, name="pl", tag="pl", bufs=2)
-            src = tps[k][:].bitcast(BF16).rearrange("p u (n e) -> p u n e", e=2)
-            for t in range(4):
-                nc.scalar.activation(out=pl[:, t, :], in_=src[:, t // 2, :, t % 2], func=ACT.Copy,
-                                     scale=s_t[:, g, t:t + 1])
-            nc.scalar.copy(out=grp[i][:, g], in_=pl[:].rearrange("p t n -> p n t"))
-
-        def scale_out(k):
-            i, g = k // G, k % G
-            if i not in grp:
-                new_group(i)
+        def vector_scale(k):
+            i, g = divmod(k, PASSES)
+            if i not in grouped:
+                new_grouped(i)
             nc.vector.tensor_tensor(
-                out=grp[i][:, g].rearrange("p n (u e) -> p n u e", e=2),
-                in0=tps[k][:].bitcast(BF16).rearrange("p u (n e) -> p n u e", e=2),
-                in1=s_t[:, g, :].rearrange("p (u e) -> p u e", e=2).unsqueeze(1).to_broadcast([P, W2, 2, 2]),
+                out=grouped[i][:, g].rearrange("p n (u e) -> p n u e", e=2),
+                in0=w_bank[k][:].bitcast(BF16).rearrange("p u (n e) -> p n u e", e=2),
+                in1=scale[:, g, :].rearrange("p (u e) -> p u e", e=2).unsqueeze(1).to_broadcast([P, PAIR_ROWS, 2, 2]),
                 op=ALU.mult)
 
-        def copy_out(key, g, tp):
-            nc.vector.tensor_copy(
-                out=grp[key][:, g].rearrange("p n t -> p (n t)").bitcast(F32).rearrange("p (n u) -> p n u", u=2),
-                in_=tp[:].rearrange("p u n -> p n u"))
+        def scalar_scale(k):
+            i, g = divmod(k, PASSES)
+            if i not in grouped:
+                new_grouped(i)
+            planes = work.tile([P, PACK, PAIR_ROWS], BF16, name="planes", tag="planes", bufs=2)
+            src = w_bank[k][:].bitcast(BF16).rearrange("p u (n e) -> p u n e", e=2)
+            for t in range(PACK):
+                nc.scalar.activation(out=planes[:, t, :], in_=src[:, t // 2, :, t % 2], func=ACT.Copy,
+                                     scale=scale[:, g, t:t + 1])
+            nc.scalar.copy(out=grouped[i][:, g], in_=planes[:].rearrange("p t n -> p n t"))
 
-        def quantize(key, pool, tagc, tags):
-            c = pool.tile([P, G, W2], U32, name=tagc, tag=tagc, align_bytes=64)
-            s = pool.tile([P, G, W2], U8, name=tags, tag=tags, align_bytes=64)
+        def copy_x(k):
+            key, g = "x%d" % (k // PASSES), k % PASSES
+            if g == 0:
+                new_grouped(key)
+            nc.vector.tensor_copy(
+                out=grouped[key][:, g].rearrange("p n t -> p (n t)").bitcast(F32).rearrange("p (n u) -> p n u", u=2),
+                in_=x_bank[k][:].rearrange("p u n -> p n u"))
+
+        def quantize(key, pool, name):
+            c = pool.tile([P, PASSES, PAIR_ROWS], U32, name=name + "_codes", tag=name + "_codes", align_bytes=64)
+            s = pool.tile([P, PASSES, PAIR_ROWS], U8, name=name + "_scales", tag=name + "_scales", align_bytes=64)
             nc.vector.quantize_mx(out=c[:].rearrange("p g n -> p (g n)").bitcast(FP8X4),
                                   scales=s[:].rearrange("p g n -> p (g n)"),
-                                  in_=grp[key][:].rearrange("p g n t -> p (g n t)"))
+                                  in_=grouped[key][:].rearrange("p g n t -> p (g n t)"))
             codes[key] = (c, s)
 
-        acc = {}
-        tsrc = {}
-        prod = {}
-        res = {}
+        sums = {}
+        sum_tile = {}
+        products = {}
+        rotated = {}
 
-        def mm_group(m):
-            p, b = m // B, m % B
-            h, bb = b // 2, b % 2
+        def matmuls(pair, b):
+            half, bb = divmod(b, 2)
             if bb == 0:
-                acc[(p, h)] = psum_o.tile([P, 2, W2], F32, name="ot", tag="ot")
-                tsrc[(p, h)] = acc[(p, h)][:].rearrange("p b n -> p (b n)")
-            ot = acc[(p, h)]
-            if b == 0 and p < NPAIR - 1:
-                for n in QDUMMY:
-                    dummy(ot, n)
-            wc, ws = codes[p]
-            xc, xs = codes["x%d" % h]
-            for g in range(G):
-                nc.tensor.matmul_mx(out=ot[:, bb, :],
-                                    lhsT=xc[:, g, P * bb:P * (bb + 1)].bitcast(FP8X4),
-                                    lhsT_scale=xs[:, g, P * bb:P * (bb + 1)],
-                                    rhs=wc[:, g, :].bitcast(FP8X4),
-                                    rhs_scale=ws[:, g, :],
-                                    start=(g == 0), stop=(g == G - 1))
+                sum_tile[(pair, half)] = psum_o.tile([P, 2, PAIR_ROWS], F32, name="sum_bank", tag="sum_bank")
+                sums[(pair, half)] = sum_tile[(pair, half)][:].rearrange("p b n -> p (b n)")
+            w_codes, w_scales = codes[pair]
+            x_codes, x_scales = codes["x%d" % half]
+            for g in range(PASSES):
+                nc.tensor.matmul_mx(out=sum_tile[(pair, half)][:, bb, :],
+                                    lhsT=x_codes[:, g, P * bb:P * (bb + 1)].bitcast(FP8X4),
+                                    lhsT_scale=x_scales[:, g, P * bb:P * (bb + 1)],
+                                    rhs=w_codes[:, g, :].bitcast(FP8X4),
+                                    rhs_scale=w_scales[:, g, :],
+                                    start=(g == 0), stop=(g == PASSES - 1))
 
-        def rope_copy(p, h):
-            ts = work.tile([P, 2 * W2], F32, name="ts", tag="ts", bufs=TS_BUFS)
-            nc.scalar.copy(out=ts[:], in_=tsrc[(p, h)])
-            tsrc[(p, h)] = ts[:]
+        def copy_sums(pair, half):
+            t = work.tile([P, 2 * PAIR_ROWS], F32, name="sums_copy", tag="sums_copy")
+            nc.scalar.copy(out=t[:], in_=sums[(pair, half)])
+            sums[(pair, half)] = t[:]
 
-        def rope_products(eng, p, h):
-            pq = work.tile([P, 2, 2 * W2], F32, name="pq", tag="pq", bufs=PQ_BUFS)
-            eng.tensor_tensor(out=pq[:], in0=tsrc[(p, h)].unsqueeze(1).to_broadcast([P, 2, 2 * W2]),
-                              in1=tab[:].rearrange("p a r d -> p a (r d)"), op=ALU.mult)
-            prod[(p, h)] = pq
+        def rope_product(eng, pair, half):
+            t = work.tile([P, 2, 2 * PAIR_ROWS], F32, name="products", tag="products")
+            eng.tensor_tensor(out=t[:], in0=sums[(pair, half)].unsqueeze(1).to_broadcast([P, 2, 2 * PAIR_ROWS]),
+                              in1=table[:].rearrange("p a c d -> p a (c d)"), op=ALU.mult)
+            products[(pair, half)] = t
 
-        def rope_add(eng, p, h):
-            if p not in res:
-                res[p] = work.tile([P, B, 2, HD], F32, name="rr", tag="rr")
-                first = True
-            else:
-                first = False
-            eng.tensor_tensor(out=res[p][:, 2 * h:2 * h + 2].rearrange("p b h (j e) -> p (b h j) e", e=2),
-                              in0=prod[(p, h)][:, 0].rearrange("p (m e) -> p m e", e=2),
-                              in1=prod[(p, h)][:, 1].rearrange("p (m e) -> p m e", e=2)[:, :, ::-1], op=ALU.add)
-            dst = out_0 if p < NPAIR // 2 else out_1
-            h0 = 2 * (p % (NPAIR // 2))
-            if p >= NPAIR - LASTSPLIT:
-                for hh in range(2):
-                    nc.sync.dma_start(out=dst[h0 + hh, 2 * h:2 * h + 2].rearrange("b s d -> s b d"),
-                                      in_=res[p][:, 2 * h:2 * h + 2, hh, :])
-            elif not first:
-                for hh in range(2):
-                    nc.sync.dma_start(out=dst[h0 + hh].rearrange("b s d -> s b d"), in_=res[p][:, :, hh, :])
+        def rope_sum(eng, pair, half):
+            second = pair in rotated
+            if not second:
+                rotated[pair] = work.tile([P, B, 2, HD], F32, name="rotated", tag="rotated")
+            batches = slice(2 * half, 2 * half + 2)
+            eng.tensor_tensor(out=rotated[pair][:, batches].rearrange("p b h (j e) -> p (b h j) e", e=2),
+                              in0=products[(pair, half)][:, 0].rearrange("p (m e) -> p m e", e=2),
+                              in1=products[(pair, half)][:, 1].rearrange("p (m e) -> p m e", e=2)[:, :, ::-1],
+                              op=ALU.add)
+            dst = out_0 if pair < PAIRS // 2 else out_1
+            head = 2 * (pair % (PAIRS // 2))
+            for hh in range(2):
+                if pair == PAIRS - 1:
+                    nc.sync.dma_start(out=dst[head + hh, batches].rearrange("b s d -> s b d"),
+                                      in_=rotated[pair][:, batches, hh, :])
+                elif second:
+                    nc.sync.dma_start(out=dst[head + hh].rearrange("b s d -> s b d"), in_=rotated[pair][:, :, hh, :])
 
-        junk = const.tile([P, 1], U32, name="junk")
-        gq = []
+        for_gpsimd = []
+        fence_word = const.tile([P, 1], U32, name="fence_word")
 
-        def fence(key):
-            nc.gpsimd.tensor_copy(out=junk[:], in_=codes[key][0][:, 0, 0:1])
+        def gpsimd_burst(key):
+            nc.gpsimd.tensor_copy(out=fence_word[:], in_=codes[key][0][:, 0, 0:1])
+            for pair, half in for_gpsimd:
+                rope_product(nc.gpsimd, pair, half)
+                rope_sum(nc.gpsimd, pair, half)
+            for_gpsimd.clear()
 
-        pending = []
-        taken = [0]
+        PRODUCT, SUM = 0, 1
+        pieces = []
+        pieces_done = [0]
 
-        def waiting():
-            return len(pending) - taken[0]
+        def pieces_left():
+            return len(pieces) - pieces_done[0]
+
+        def next_is(what):
+            return pieces_left() > 0 and pieces[pieces_done[0]][0] == what
 
         def vector_piece():
-            what, p, h = pending[taken[0]]
-            taken[0] += 1
-            if what == 0:
-                rope_products(nc.vector, p, h)
-                if rope_mode(p, h) == V2G1:
-                    rope_add(nc.gpsimd, p, h)
+            what, pair, half = pieces[pieces_done[0]]
+            pieces_done[0] += 1
+            if what == PRODUCT:
+                rope_product(nc.vector, pair, half)
+                if rope_way(pair, half) == SUM_ON_GPSIMD:
+                    rope_sum(nc.gpsimd, pair, half)
             else:
-                rope_add(nc.vector, p, h)
+                rope_sum(nc.vector, pair, half)
 
-        def by_scalar(k):
-            return k in SCALAR_BANKS
-
-        xts = {}
-        t_done = [0]
-
-        def x_bank(k):
-            if k < G:
-                xts[k] = transposes(psum_t, "tp", xb0[k], 0, 0)
-            else:
-                xts[k] = transposes(psum_t, "tp", xb[k // G], k % G, 0)
-
-        def t_upto(last):
-            for k in range(t_done[0], min(last, NBANK - 1) + 1):
-                t_bank(k, 0)
-            t_done[0] = max(t_done[0], min(last, NBANK - 1) + 1)
-
-        plan = {}
-        for p in range(NPAIR):
+        groups = {}
+        for pair in range(PAIRS):
             for b in range(B):
-                plan.setdefault(G * p + LAG + b, []).append((p, b))
-        plan[LAG + 2].remove((0, 2))
-        plan[LAG + 3].remove((0, 3))
-        plan[2 * G].append((0, 2))
-        plan[2 * G + 1].append((0, 3))
+                if pair > 0 or b < 2:
+                    groups.setdefault(PASSES * (pair + 1) + b, []).append((pair, b))
+        for b in (2, 3):
+            groups[2 * PASSES + b - 2].append((0, b))
 
-        cast0(0, "v")
-        cast0(1, "s")
-        cast0(3, "s")
-        cast(1, "s")
-        t_upto(0)
-        x_bank(0)
-        t_upto(1)
-        x_bank(1)
+        cast_first(0, nc.vector.tensor_copy)
+        cast_first(1, nc.scalar.copy)
+        cast_first(3, nc.scalar.copy)
+        cast_pair(1)
+        transpose_weights_upto(0)
+        transpose_x(0)
+        transpose_weights_upto(1)
+        transpose_x(1)
 
-        ready = []
-        for k in range(NBANK + LAG):
-            i, g = k // G, k % G
-            if by_scalar(k + SLEAD):
-                scalar_out(k + SLEAD)
-            if k < NBANK and not by_scalar(k):
-                scale_out(k)
-            if g == 0 and waiting() > 0 and pending[taken[0]][0] == 2:
-                vector_piece()
-            if g == 0 and 1 <= i <= NPAIR:
-                quantize(i - 1, work, "wc", "ws")
+        fresh = []
+        for k in range(BANKS + PASSES):
+            i, g = divmod(k, PASSES)
+            draining = k >= BANKS
+
+            if by_scalar(k + SCALAR_AHEAD):
+                scalar_scale(k + SCALAR_AHEAD)
+
+            if not draining and not by_scalar(k):
+                vector_scale(k)
+            if g == 0:
+                if next_is(SUM):
+                    vector_piece()
+                if i >= 1:
+                    quantize(i - 1, work, "w")
             if k == 0:
-                cast0(2, "v")
-                t_upto(2)
-            if k == 0 and CAST2_FIRST:
-                cast(2, "s")
-            if k == TAB_UNIT:
-                tables_vector()
-                tables_rest()
-                if not CAST2_FIRST:
-                    cast(2, "s")
-            if k == G:
-                quantize("x0", const, "xc0", "xs0")
-            if k == 2 * G:
-                quantize("x1", const, "xc1", "xs1")
-            if g == 0 and 1 <= i <= NPAIR:
-                fence("x0" if k == G else "x1" if k == 2 * G else i - 1)
-                for p, h in gq:
-                    rope_products(nc.gpsimd, p, h)
-                    rope_add(nc.gpsimd, p, h)
-                gq.clear()
-            if k < 2 * G:
-                if g == 0:
-                    new_group("x%d" % i)
-                copy_out("x%d" % i, g, xts[k])
-            for item in ready:
-                if item[0] + DELAY <= k or k >= NBANK:
-                    pending.extend(item[1])
-            ready = [item for item in ready if not (item[0] + DELAY <= k or k >= NBANK)]
-            if k >= NBANK:
-                for n in range(waiting()):
+                cast_first(2, nc.vector.tensor_copy)
+                transpose_weights_upto(2)
+                cast_pair(2)
+            if k == 2:
+                make_table()
+            if g == 0 and 1 <= i <= 2:
+                quantize("x%d" % (i - 1), const, "x%d" % (i - 1))
+            if g == 0 and for_gpsimd:
+                gpsimd_burst("x1" if i == 2 else i - 1)
+            if k < X_BANKS:
+                copy_x(k)
+
+            for unit, its_pieces in fresh:
+                if unit + PRODUCT_LAG <= k or draining:
+                    pieces.extend(its_pieces)
+            fresh = [item for item in fresh if not (item[0] + PRODUCT_LAG <= k or draining)]
+            if draining:
+                for n in range(pieces_left()):
                     vector_piece()
-            elif (g != 0 or by_scalar(k)) and waiting() > 0 and pending[taken[0]][0] != 2:
+            elif (g != 0 or by_scalar(k)) and next_is(PRODUCT):
                 vector_piece()
-                if waiting() > 1 and pending[taken[0]][0] != 2:
+                if pieces_left() > 1 and next_is(PRODUCT):
                     vector_piece()
-            if k + 2 < 2 * G:
-                x_bank(k + 2)
-                t_upto(k + 3)
-            elif k + 2 == 2 * G:
-                t_upto(k + AHEAD - 1)
+
+            if k + 2 < X_BANKS:
+                transpose_x(k + 2)
+                transpose_weights_upto(k + 3)
+            elif k + 2 == X_BANKS:
+                transpose_weights_upto(k + TRANSPOSE_BANKS - 1)
             else:
-                t_upto(k + AHEAD)
-            if k in FILL:
-                for n in range(2):
-                    dummy(tps[t_done[0] - 1], 512)
-            for p, b in plan.get(k, []):
-                mm_group(B * p + b)
+                transpose_weights_upto(k + TRANSPOSE_BANKS)
+            for pair, b in groups.get(k, []):
+                matmuls(pair, b)
                 if b % 2 == 1:
-                    h = b // 2
-                    mode = rope_mode(p, h)
-                    if mode == SG3:
-                        rope_copy(p, h)
-                        gq.append((p, h))
-                    elif mode == V2G1:
-                        ready.append((k, [(0, p, h)]))
+                    half = b // 2
+                    way = rope_way(pair, half)
+                    if way == BY_GPSIMD:
+                        copy_sums(pair, half)
+                        for_gpsimd.append((pair, half))
+                    elif way == SUM_ON_GPSIMD:
+                        fresh.append((k, [(PRODUCT, pair, half)]))
                     else:
-                        ready.append((k, [(0, p, h), (2, p, h)]))
-            if g == CAST_G and 3 <= i + CAST_LEAD < NPAIR:
-                cast(i + CAST_LEAD, "s")
-        for item in ready:
-            pending.extend(item[1])
-        for n in range(waiting()):
+                        fresh.append((k, [(PRODUCT, pair, half), (SUM, pair, half)]))
+
+            if g == 2 and CAST_AHEAD <= i + CAST_AHEAD < PAIRS:
+                cast_pair(i + CAST_AHEAD)
+
+        for unit, its_pieces in fresh:
+            pieces.extend(its_pieces)
+        for n in range(pieces_left()):
             vector_piece()

@@ -205,7 +205,8 @@ def tile_multiheadselfattention_pa_kernel(tc, x, w_qk_bytes, w_qk_scale, out_0, 
             for t in range(PACK):
                 nc.scalar.activation(out=planes[:, t, :], in_=src[:, t // 2, :, t % 2], func=ACT.Copy,
                                      scale=scale[:, g, t:t + 1])
-            nc.scalar.copy(out=grouped[i][:, g], in_=planes[:].rearrange("p t n -> p n t"))
+            nc.scalar.copy(out=grouped[i][:, g].rearrange("p (c i) t -> p c t i", i=4),
+                           in_=planes[:].rearrange("p t (c i) -> p c t i", i=4))
 
         def copy_x(k):
             key, g = "x%d" % (k // PASSES), k % PASSES

@@ -29,60 +29,124 @@ X_BANKS = 2 * PASSES
 
 TRANSPOSE_BANKS = 5
 SUM_BANKS = 3
-CAST_AHEAD = 3
-SCALAR_AHEAD = 3
-PRODUCT_LAG = 2
 
 BY_VECTOR = 0
 SUM_ON_GPSIMD = 1
 BY_GPSIMD = 2
 
 
-def by_scalar(k):
-    pair, g = divmod(k, PASSES)
-    if pair >= PAIRS:
-        return False
-    if pair == PAIRS - 1:
-        return g != 1
-    return g == 0 and pair >= 4 and pair % 2 == 0
+BYTES_BUFS = 12
+HALF_CAST = (1, 2, 3)
+SCALE_FIRST = ()
+SCALED_BY_SCALAR = (24, 32, 40, 48, 56, 60, 62, 63)
+G_ALL, V_PRODUCT, V_PRODUCT_HALF_SUM, V_ALL = range(4)
+XS = (4, 5, 6, 7)
+WHOLE_CAST = 99
+MERGE = False
+S_FROM = 4
+HEAD_W = 9
+HEAD_T = [("w", 0), ("x", 0), ("w", 1), ("x", 1), ("w", 2), ("x", 2), ("w", 3), ("x", 3), ("w", 4), ("x", 4), ("w", 5), ("x", 5), ("w", 6), ("m", 0), ("w", 7), ("x", 6), ("m", 1), ("w", 8), ("x", 7)]
+HEAD_S = [("c", 1, 0), ("c", 1, 1), ("c", 1, 2), ("c", 1, 3), ("x", 4), ("c", 2, 0), ("c", 2, 1), ("x", 5), ("c", 2, 2), ("c", 2, 3), ("x", 6), ("x", 7), "sin", ("s", 0)]
 
 
-def rope_way(pair, half):
-    if pair == PAIRS - 1:
-        return BY_VECTOR
-    if half == 1 and any(by_scalar(k) for k in range(PASSES * (pair + 2) + 1, PASSES * (pair + 3) + 1)):
-        return BY_VECTOR
-    if half == 0 and pair < PAIRS - 3:
-        return BY_GPSIMD
-    return SUM_ON_GPSIMD
+def ahead(k):
+    return 5
 
+
+def cast_lead(p):
+    return 10
+
+
+def way(pair, half):
+    if half == 0:
+        return G_ALL if pair < 13 else V_PRODUCT
+    if any(k in SCALED_BY_SCALAR for k in range(PASSES * (pair + 2) + 1, PASSES * (pair + 3) + 1)):
+        return V_ALL
+    return V_PRODUCT
+GC = (3,)
 
 def tile_multiheadselfattention_pa_kernel(tc, x, w_qk_bytes, w_qk_scale, out_0, out_1):
     nc = tc.nc
     with ExitStack() as ctx:
         const = ctx.enter_context(tc.tile_pool(name="const", bufs=1))
-        bytes_pool = ctx.enter_context(tc.tile_pool(name="bytes", bufs=PAIRS - 1))
-        wide = ctx.enter_context(tc.tile_pool(name="wide", bufs=CAST_AHEAD + 1))
+        bytes_pool = ctx.enter_context(tc.tile_pool(name="bytes", bufs=12))
+        wide = ctx.enter_context(tc.tile_pool(name="wide", bufs=4))
         work = ctx.enter_context(tc.tile_pool(name="work", bufs=4))
         psum_t = ctx.enter_context(tc.psum_pool(name="psum_t", bufs=TRANSPOSE_BANKS))
         psum_o = ctx.enter_context(tc.psum_pool(name="psum_o", bufs=SUM_BANKS))
         ctx.enter_context(tc.manual_schedule())
 
+        programs = {"load": [], "S": [], "V": [], "T": [], "G": []}
+        done = set()
+        rings = {}
+
+        def ring_free(name, bufs, key):
+            r = rings.setdefault(name, [])
+            return key in r or len(r) < bufs or r[len(r) - bufs] in done
+
+        def ring_take(name, key):
+            if key not in rings[name]:
+                rings[name].append(key)
+
+        def item(engine, name, needs, run, ring=None):
+            programs[engine].append((name, needs, run, ring))
+
+        def emit_all():
+            at = {e: 0 for e in programs}
+            moved = True
+            while_guard = 0
+            for round_ in range(100000):
+                moved = False
+                for e in programs:
+                    for n in range(len(programs[e])):
+                        if at[e] >= len(programs[e]):
+                            break
+                        name, needs, run, ring = programs[e][at[e]]
+                        if not all(x in done for x in needs):
+                            break
+                        if ring is not None and not all(ring_free(rn, rb, rk) for rn, rb, rk in ring):
+                            break
+                        if ring is not None:
+                            for rn, rb, rk in ring:
+                                ring_take(rn, rk)
+                        run()
+                        done.add(name)
+                        at[e] += 1
+                        moved = True
+                if not moved:
+                    break
+            stuck = [(e, programs[e][at[e]][0], programs[e][at[e]][3], [x for x in programs[e][at[e]][1] if x not in done]) for e in programs if at[e] < len(programs[e])]
+            assert not stuck, stuck
+
         first_bytes = []
         first_x = []
         scale = const.tile([P, PASSES, PACK], F32, name="scale")
-        for g in range(PASSES):
+
+        def load_first_bytes(g):
             k_cols = slice(K_PASS * g, K_PASS * (g + 1))
             t = const.tile([P, 2, K_PASS], U8, name="first_bytes%d" % g)
             nc.sync.dma_start(out=t[:], in_=w_qk_bytes[0:PAIR_ROWS, k_cols].rearrange("(r p) k -> p r k", p=P))
             first_bytes.append(t)
-            if g == 0:
-                nc.sync.dma_start(out=scale[:], in_=w_qk_scale.rearrange("o (g p t) -> p (o g) t", p=P, t=PACK))
+
+        def load_first_x(g):
+            k_cols = slice(K_PASS * g, K_PASS * (g + 1))
             t = const.tile([P, 2, K_PASS], BF16, name="first_x%d" % g)
             nc.sync.dma_start(out=t[:], in_=x[0:2, :, k_cols].rearrange("b s k -> s b k"))
             first_x.append(t)
 
+        load_first_bytes(0)
+        load_first_bytes(1)
+        nc.sync.dma_start(out=scale[:], in_=w_qk_scale.rearrange("o (g p t) -> p (o g) t", p=P, t=PACK))
+        load_first_x(0)
+        load_first_bytes(2)
+        load_first_x(1)
+        load_first_bytes(3)
+        load_first_x(2)
+        load_first_x(3)
+
         pair_bytes = {}
+        second_x = const.tile([P, 2, D], BF16, name="second_x")
+        scale_rows = const.tile([P, D], F32, name="scale_rows") if SCALE_FIRST else None
 
         def load_pair(i):
             t = bytes_pool.tile([P, 2, D], U8, name="pair_bytes%d" % i, tag="pair_bytes")
@@ -90,11 +154,22 @@ def tile_multiheadselfattention_pa_kernel(tc, x, w_qk_bytes, w_qk_scale, out_0, 
                               in_=w_qk_bytes[PAIR_ROWS * i:PAIR_ROWS * (i + 1), :].rearrange("(r p) k -> p r k", p=P))
             pair_bytes[i] = t
 
-        load_pair(1)
-        second_x = const.tile([P, 2, D], BF16, name="second_x")
-        nc.sync.dma_start(out=second_x[:], in_=x[2:4].rearrange("b s k -> s b k"))
+        def load_scale_rows(h):
+            k_cols = slice(D // 2 * h, D // 2 * (h + 1))
+            nc.sync.dma_start(out=scale_rows[:, k_cols],
+                              in_=w_qk_scale[:, k_cols].rearrange("o k -> (o k)").partition_broadcast(P))
+
+        def load_second_x():
+            nc.sync.dma_start(out=second_x[:], in_=x[2:4].rearrange("b s k -> s b k"))
+
+        def add_load_pair(i):
+            item("load", ("bytes", i), [], lambda: load_pair(i), [("bytes", BYTES_BUFS, ("widened", i))])
+
+        add_load_pair(1)
+        item("load", ("second_x",), [], load_second_x)
         for i in range(2, PAIRS):
-            load_pair(i)
+            add_load_pair(i)
+
 
         warm = const.tile([P, 2], F32, name="warm")
         nc.gpsimd.memset(warm[:, 0:1], 0.0)
@@ -129,11 +204,15 @@ def tile_multiheadselfattention_pa_kernel(tc, x, w_qk_bytes, w_qk_scale, out_0, 
         def make_table():
             nc.vector.tensor_copy(out=whole[:], in_=arg_flat)
             nc.vector.tensor_tensor(out=frac[:], in0=arg_flat, in1=whole[:], op=ALU.subtract)
+
+        def make_table_gpsimd():
             nc.gpsimd.tensor_scalar(out=over[:], in0=frac[:], scalar1=0.5, scalar2=None, op0=ALU.is_gt)
             nc.gpsimd.tensor_tensor(out=near[:].rearrange("p a j e -> p (a j e)"), in0=frac[:], in1=over[:],
                                     op=ALU.subtract)
             nc.gpsimd.tensor_scalar(out=near[:, 1, :, 1], in0=near[:, 1, :, 1], scalar1=-1.0, scalar2=None,
                                     op0=ALU.mult)
+
+        def make_sin():
             for a in range(2):
                 nc.scalar.activation(out=table[:, a],
                                      in_=near[:, a].rearrange("p j e -> p (j e)").unsqueeze(1).to_broadcast([P, 4, HD]),
@@ -152,11 +231,40 @@ def tile_multiheadselfattention_pa_kernel(tc, x, w_qk_bytes, w_qk_scale, out_0, 
                  in_=first_bytes[g][:].rearrange("p r k -> p (r k)").bitcast(FP8))
             first_wide[g] = t
 
-        def cast_pair(i):
-            t = wide.tile([P, 2, D], BF16, name="pair_wide%d" % i, tag="pair_wide")
-            for r in range(2):
-                nc.scalar.copy(out=t[:, r, :], in_=pair_bytes[i][:, r, :].bitcast(FP8))
-            pair_wide[i] = t
+        def need_wide(i):
+            if i not in pair_wide:
+                pair_wide[i] = wide.tile([P, 2, D], BF16, name="pair_wide%d" % i, tag="pair_wide")
+
+        def widen_piece(i, r, k0, k1, engine):
+            need_wide(i)
+            if r == 2:
+                out = pair_wide[i][:].rearrange("p r k -> p (r k)")
+                in_ = pair_bytes[i][:].rearrange("p r k -> p (r k)").bitcast(FP8)
+            else:
+                out, in_ = pair_wide[i][:, r, k0:k1], pair_bytes[i][:, r, k0:k1].bitcast(FP8)
+            if engine == "G":
+                nc.gpsimd.tensor_copy(out=out, in_=in_)
+            elif engine == "V":
+                nc.vector.tensor_tensor(out=out, in0=in_, in1=scale_rows[:, k0:k1], op=ALU.mult)
+            else:
+                nc.scalar.copy(out=out, in_=in_)
+            widened_left[i] -= 1
+            if widened_left[i] == 0:
+                done.add(("widened", i))
+
+        widened_left = {}
+
+        def add_widen(engine, i, halves):
+            parts = [(h, r) for h in range(2) for r in range(2)] if halves else [(None, r) for r in ((0, 1) if i < WHOLE_CAST else (2,))]
+            widened_left[i] = len(parts)
+            out = []
+            for h, r in parts:
+                k0, k1 = (0, D) if h is None else (D // 2 * h, D // 2 * (h + 1))
+                first = (h in (None, 0)) and r in (0, 2)
+                out.append((engine, ("wide", i, h, r), [("bytes", i)] + ([("scale_rows", h)] if engine == "V" else []),
+                            lambda r=r, k0=k0, k1=k1: widen_piece(i, r, k0, k1, engine),
+                            [("wide", 4, ("transposed", i))] if first else None))
+            return out
 
         def transposes(src, g):
             bank = psum_t.tile([P, 2, PAIR_ROWS], F32, name="bank", tag="bank")
@@ -167,15 +275,27 @@ def tile_multiheadselfattention_pa_kernel(tc, x, w_qk_bytes, w_qk_scale, out_0, 
                                         words[:, r, K_PASS // 2 * g + u:K_PASS // 2 * (g + 1):2], ident[:])
             return bank
 
-        w_banks_done = [0]
+        transposed_left = {}
 
-        def transpose_weights_upto(last):
-            for k in range(w_banks_done[0], min(last, BANKS - 1) + 1):
-                if k < PASSES:
-                    w_bank[k] = transposes(first_wide[k], 0)
-                else:
-                    w_bank[k] = transposes(pair_wide[k // PASSES], k % PASSES)
-            w_banks_done[0] = max(w_banks_done[0], min(last, BANKS - 1) + 1)
+        def transpose_weights(k):
+            i = k // PASSES
+            if i == 0:
+                w_bank[k] = transposes(first_wide[k], 0)
+            else:
+                w_bank[k] = transposes(pair_wide[i], k % PASSES)
+            transposed_left[i] = transposed_left.get(i, PASSES) - 1
+            if transposed_left[i] == 0:
+                done.add(("transposed", i))
+
+        def add_transpose_w(k):
+            i, g = divmod(k, PASSES)
+            if i == 0:
+                needs = [("first_wide", g)]
+            elif i in HALF_CAST:
+                needs = [("wide", i, g // 2, r) for r in range(2)]
+            else:
+                needs = [("wide", i, None, r) for r in ((0, 1) if i < WHOLE_CAST else (2,))]
+            item("T", ("w", k), needs, lambda: transpose_weights(k), [("bank", TRANSPOSE_BANKS, ("emptied_w", k))])
 
         def transpose_x(k):
             if k < PASSES:
@@ -183,13 +303,17 @@ def tile_multiheadselfattention_pa_kernel(tc, x, w_qk_bytes, w_qk_scale, out_0, 
             else:
                 x_bank[k] = transposes(second_x, k % PASSES)
 
-        def new_grouped(key):
-            grouped[key] = work.tile([P, PASSES, PAIR_ROWS, PACK], BF16, name="grouped", tag="grouped", align_bytes=64)
+        def add_transpose_x(k):
+            item("T", ("x", k), [("second_x",)] if k >= PASSES else [], lambda: transpose_x(k),
+                 [("bank", TRANSPOSE_BANKS, ("emptied_x", k))])
+
+        def need_grouped(key):
+            if key not in grouped:
+                grouped[key] = work.tile([P, PASSES, PAIR_ROWS, PACK], BF16, name="grouped", tag="grouped", align_bytes=64)
 
         def vector_scale(k):
             i, g = divmod(k, PASSES)
-            if i not in grouped:
-                new_grouped(i)
+            need_grouped(i)
             nc.vector.tensor_tensor(
                 out=grouped[i][:, g].rearrange("p n (u e) -> p n u e", e=2),
                 in0=w_bank[k][:].bitcast(BF16).rearrange("p u (n e) -> p n u e", e=2),
@@ -198,8 +322,7 @@ def tile_multiheadselfattention_pa_kernel(tc, x, w_qk_bytes, w_qk_scale, out_0, 
 
         def scalar_scale(k):
             i, g = divmod(k, PASSES)
-            if i not in grouped:
-                new_grouped(i)
+            need_grouped(i)
             planes = work.tile([P, PACK, PAIR_ROWS], BF16, name="planes", tag="planes", bufs=2)
             src = w_bank[k][:].bitcast(BF16).rearrange("p u (n e) -> p u n e", e=2)
             for t in range(PACK):
@@ -208,182 +331,279 @@ def tile_multiheadselfattention_pa_kernel(tc, x, w_qk_bytes, w_qk_scale, out_0, 
             nc.scalar.copy(out=grouped[i][:, g].rearrange("p (c i) t -> p c t i", i=4),
                            in_=planes[:].rearrange("p t (c i) -> p c t i", i=4))
 
-        def copy_x(k):
-            key, g = "x%d" % (k // PASSES), k % PASSES
-            if g == 0:
-                new_grouped(key)
-            nc.vector.tensor_copy(
+        def copy_bank(copy, key, g, bank):
+            need_grouped(key)
+            copy(
                 out=grouped[key][:, g].rearrange("p n t -> p (n t)").bitcast(F32).rearrange("p (n u) -> p n u", u=2),
-                in_=x_bank[k][:].rearrange("p u n -> p n u"))
+                in_=bank[:].rearrange("p u n -> p n u"))
 
-        def quantize(key, pool, name):
-            c = pool.tile([P, PASSES, PAIR_ROWS], U32, name=name + "_codes", tag=name + "_codes", align_bytes=64)
-            s = pool.tile([P, PASSES, PAIR_ROWS], U8, name=name + "_scales", tag=name + "_scales", align_bytes=64)
-            nc.vector.quantize_mx(out=c[:].rearrange("p g n -> p (g n)").bitcast(FP8X4),
-                                  scales=s[:].rearrange("p g n -> p (g n)"),
-                                  in_=grouped[key][:].rearrange("p g n t -> p (g n t)"))
-            codes[key] = (c, s)
+        def add_empty_w(engine, k):
+            i, g = divmod(k, PASSES)
+            if engine == "V":
+                run = lambda: vector_scale(k)
+            elif i in SCALE_FIRST:
+                run = lambda: copy_bank(nc.scalar.copy, i, g, w_bank[k])
+            else:
+                run = lambda: scalar_scale(k)
+            item(engine, ("emptied_w", k), [("w", k)], run)
 
-        sums = {}
+        def add_copy_x(k, engine="S"):
+            copy = nc.scalar.copy if engine == "S" else nc.vector.tensor_copy
+            item(engine, ("emptied_x", k), [("x", k)], lambda: copy_bank(copy, "x%d" % (k // PASSES), k % PASSES, x_bank[k]))
+
+        def quantize(key, pool, name, g0, g1):
+            if key not in codes:
+                codes[key] = (pool.tile([P, PASSES, PAIR_ROWS], U32, name=name + "_codes", tag=name + "_codes", align_bytes=64),
+                              pool.tile([P, PASSES, PAIR_ROWS], U8, name=name + "_scales", tag=name + "_scales", align_bytes=64))
+            c, s = codes[key]
+            nc.vector.quantize_mx(out=c[:, g0:g1].rearrange("p g n -> p (g n)").bitcast(FP8X4),
+                                  scales=s[:, g0:g1].rearrange("p g n -> p (g n)"),
+                                  in_=grouped[key][:, g0:g1].rearrange("p g n t -> p (g n t)"))
+
+        def add_quantize(key, g0=0, g1=PASSES):
+            if isinstance(key, str):
+                needs = [("emptied_x", PASSES * int(key[1]) + g) for g in range(g0, g1)]
+                item("V", ("codes", key, g0), needs, lambda: quantize(key, const, key, g0, g1))
+            else:
+                needs = [("emptied_w", PASSES * key + g) for g in range(g0, g1)]
+                item("V", ("codes", key, g0), needs, lambda: quantize(key, work, "w", g0, g1))
+
         sum_tile = {}
+        sums = {}
         products = {}
         rotated = {}
 
-        def matmuls(pair, b):
-            half, bb = divmod(b, 2)
-            if bb == 0:
-                sum_tile[(pair, half)] = psum_o.tile([P, 2, PAIR_ROWS], F32, name="sum_bank", tag="sum_bank")
-                sums[(pair, half)] = sum_tile[(pair, half)][:].rearrange("p b n -> p (b n)")
+        def matmuls(key, b, g0, g1):
+            pair, b0, nb = key
+            if key not in sum_tile:
+                pool = psum_t if pair == PAIRS - 1 else psum_o
+                sum_tile[key] = pool.tile([P, 2, PAIR_ROWS], F32, name="bank" if pair == PAIRS - 1 else "sum_bank",
+                                          tag="bank" if pair == PAIRS - 1 else "sum_bank")
+                sums[key] = sum_tile[key][:, 0:nb].rearrange("p b n -> p (b n)")
             w_codes, w_scales = codes[pair]
-            x_codes, x_scales = codes["x%d" % half]
-            for g in range(PASSES):
-                nc.tensor.matmul_mx(out=sum_tile[(pair, half)][:, bb, :],
+            x_codes, x_scales = codes["x%d" % (b // 2)]
+            bb = b % 2
+            for g in range(g0, g1):
+                nc.tensor.matmul_mx(out=sum_tile[key][:, b - b0, :],
                                     lhsT=x_codes[:, g, P * bb:P * (bb + 1)].bitcast(FP8X4),
                                     lhsT_scale=x_scales[:, g, P * bb:P * (bb + 1)],
                                     rhs=w_codes[:, g, :].bitcast(FP8X4),
                                     rhs_scale=w_scales[:, g, :],
                                     start=(g == 0), stop=(g == PASSES - 1))
 
-        def copy_sums(pair, half):
+        def add_matmuls(key, b, g0=0, g1=PASSES):
+            pair, b0, nb = key
+            ring = None
+            if b == b0 and g0 == 0:
+                ring = [("bank", TRANSPOSE_BANKS, ("read", key))] if pair == PAIRS - 1 else [("sums", SUM_BANKS, ("read", key))]
+            needs = [("codes", "x%d" % (b // 2), 0), ("codes", pair, g0 if pair == PAIRS - 1 else 0)]
+            item("T", ("mx", key, b, g1), needs, lambda: matmuls(key, b, g0, g1), ring)
+
+        def summed(key):
+            return [("mx", key, b, PASSES) for b in range(key[1], key[1] + key[2])]
+
+        def copy_sums(key):
             t = work.tile([P, 2 * PAIR_ROWS], F32, name="sums_copy", tag="sums_copy")
-            nc.scalar.copy(out=t[:], in_=sums[(pair, half)])
-            sums[(pair, half)] = t[:]
+            nc.scalar.copy(out=t[:], in_=sums[key])
+            sums[key] = t[:]
 
-        def rope_product(eng, pair, half):
-            t = work.tile([P, 2, 2 * PAIR_ROWS], F32, name="products", tag="products")
-            eng.tensor_tensor(out=t[:], in0=sums[(pair, half)].unsqueeze(1).to_broadcast([P, 2, 2 * PAIR_ROWS]),
-                              in1=table[:].rearrange("p a c d -> p a (c d)"), op=ALU.mult)
-            products[(pair, half)] = t
+        def add_copy_sums(key):
+            item("S", ("read", key), summed(key), lambda: copy_sums(key), [("sums_copy", 4, ("product", key))])
 
-        def rope_sum(eng, pair, half):
-            second = pair in rotated
-            if not second:
+        def rope_product(eng, key):
+            pair, b0, nb = key
+            cols = nb * PAIR_ROWS
+            if pair not in products:
+                products[pair] = work.tile([P, 2, 2, 2 * PAIR_ROWS], F32, name="products", tag="products", bufs=3)
+            at = PAIR_ROWS * (b0 % 2)
+            eng.tensor_tensor(out=products[pair][:, b0 // 2, :, at:at + cols], in0=sums[key].unsqueeze(1).to_broadcast([P, 2, cols]),
+                              in1=table[:, :, 0:2 * key[2]].rearrange("p a c d -> p a (c d)"), op=ALU.mult)
+
+        def add_product(engine, key):
+            def run():
+                rope_product(nc.vector if engine == "V" else nc.gpsimd, key)
+                done.add(("product", key))
+                done.add(("read", key))
+            item(engine, ("product", key), summed(key) + [("table",)] + ([("read", key)] if engine == "G" else []), run,
+                 [("products", 3, ("added", key[0]))])
+
+        added = {}
+
+        def rope_sum(eng, key, b, nb):
+            pair, b0, n_ = key
+            if pair not in rotated:
                 rotated[pair] = work.tile([P, B, 2, HD], F32, name="rotated", tag="rotated")
-            batches = slice(2 * half, 2 * half + 2)
-            eng.tensor_tensor(out=rotated[pair][:, batches].rearrange("p b h (j e) -> p (b h j) e", e=2),
-                              in0=products[(pair, half)][:, 0].rearrange("p (m e) -> p m e", e=2),
-                              in1=products[(pair, half)][:, 1].rearrange("p (m e) -> p m e", e=2)[:, :, ::-1],
-                              op=ALU.add)
+            if nb == B:
+                eng.tensor_tensor(out=rotated[pair][:].rearrange("p (q b) h (j e) -> p q (b h j) e", q=2, e=2),
+                                  in0=products[pair][:, :, 0].rearrange("p q (m e) -> p q m e", e=2),
+                                  in1=products[pair][:, :, 1].rearrange("p q (m e) -> p q m e", e=2)[:, :, :, ::-1],
+                                  op=ALU.add)
+            else:
+                cols = slice(PAIR_ROWS * (b % 2), PAIR_ROWS * (b % 2 + nb))
+                eng.tensor_tensor(out=rotated[pair][:, b:b + nb].rearrange("p b h (j e) -> p (b h j) e", e=2),
+                                  in0=products[pair][:, b // 2, 0, cols].rearrange("p (m e) -> p m e", e=2),
+                                  in1=products[pair][:, b // 2, 1, cols].rearrange("p (m e) -> p m e", e=2)[:, :, ::-1],
+                                  op=ALU.add)
+            added[pair] = added.get(pair, 0) + nb
+            if added[pair] == B:
+                done.add(("added", pair))
             dst = out_0 if pair < PAIRS // 2 else out_1
             head = 2 * (pair % (PAIRS // 2))
-            for hh in range(2):
-                if pair == PAIRS - 1:
-                    nc.sync.dma_start(out=dst[head + hh, batches].rearrange("b s d -> s b d"),
-                                      in_=rotated[pair][:, batches, hh, :])
-                elif second:
+            if pair == PAIRS - 1:
+                for q in range(b, b + nb):
+                    nc.sync.dma_start(out=dst[head:head + 2, q].rearrange("h s d -> s h d"), in_=rotated[pair][:, q])
+            elif added[pair] == B:
+                for hh in range(2):
                     nc.sync.dma_start(out=dst[head + hh].rearrange("b s d -> s b d"), in_=rotated[pair][:, :, hh, :])
 
-        for_gpsimd = []
+        def add_sum(engine, key, b, nb):
+            item(engine, ("sum", key, b), [("product", key)] if nb < B else [("product", (key[0], 0, 2)), ("product", (key[0], 2, 2))], lambda: rope_sum(nc.vector if engine == "V" else nc.gpsimd, key, b, nb))
+
         fence_word = const.tile([P, 1], U32, name="fence_word")
 
-        def gpsimd_burst(key):
-            nc.gpsimd.tensor_copy(out=fence_word[:], in_=codes[key][0][:, 0, 0:1])
-            for pair, half in for_gpsimd:
-                rope_product(nc.gpsimd, pair, half)
-                rope_sum(nc.gpsimd, pair, half)
-            for_gpsimd.clear()
+        def add_fence(key):
+            item("G", ("fence", key), [("codes", key, 0)],
+                 lambda: nc.gpsimd.tensor_copy(out=fence_word[:], in_=codes[key][0][:, 0, 0:1]))
 
-        PRODUCT, SUM = 0, 1
-        pieces = []
-        pieces_done = [0]
+        def pair_key(pair, half):
+            return (pair, 2 * half, 2)
 
-        def pieces_left():
-            return len(pieces) - pieces_done[0]
+        item("V", ("first_wide", 0), [], lambda: cast_first(0, nc.vector.tensor_copy))
+        item("V", ("first_wide", 1), [], lambda: cast_first(1, nc.vector.tensor_copy))
+        add_empty_w("V", 0)
+        for k in range(4):
+            if k not in XS:
+                add_copy_x(k, "V")
+            add_empty_w("V", k + 1)
+            if k == 1:
+                item("V", ("table_a",), [], make_table)
+        add_quantize("x0")
+        add_quantize(0)
+        for k in range(4, 8):
+            if k not in XS:
+                add_copy_x(k, "V")
+            add_empty_w("V", k + 1)
+        add_quantize(1)
+        add_quantize("x1")
+        for k in (9, 10, 11):
+            add_empty_w("V", k)
+        add_product("V", pair_key(0, 1))
+        add_empty_w("V", 12)
+        add_quantize(2)
+        add_empty_w("V", 13)
+        add_product("V", pair_key(1, 1))
+        add_empty_w("V", 14)
+        add_empty_w("V", 15)
+        for i in range(4, PAIRS):
+            for g in range(PASSES):
+                k = PASSES * i + g
+                if k not in SCALED_BY_SCALAR:
+                    add_empty_w("V", k)
+                if g == 0:
+                    if i >= 4 and way(i - 3, 1) == V_ALL:
+                        add_sum("V", pair_key(i - 3, 1), 2, 2)
+                    elif i >= 4 and way(i - 3, 1) == V_PRODUCT_HALF_SUM:
+                        add_sum("V", pair_key(i - 3, 1), 2, 1)
+                    add_quantize(i - 1)
+                if g == 1:
+                    if way(i - 2, 0) == V_PRODUCT:
+                        add_product("V", pair_key(i - 2, 0))
+                    add_product("V", pair_key(i - 2, 1))
+        last = PAIRS - 1
+        add_product("V", (last - 1, 0, 2))
+        if way(last - 2, 1) == V_ALL:
+            add_sum("V", pair_key(last - 2, 1), 2, 2)
+        add_quantize(last, 0, 2)
+        add_quantize(last, 2, 4)
+        add_product("V", pair_key(last - 1, 1))
+        for b in range(B):
+            add_product("V", (last, b, 1))
+        add_sum("V", (last, 2, 1), 2, 1)
+        add_sum("V", (last, 3, 1), 3, 1)
 
-        def next_is(what):
-            return pieces_left() > 0 and pieces[pieces_done[0]][0] == what
-
-        def vector_piece():
-            what, pair, half = pieces[pieces_done[0]]
-            pieces_done[0] += 1
-            if what == PRODUCT:
-                rope_product(nc.vector, pair, half)
-                if rope_way(pair, half) == SUM_ON_GPSIMD:
-                    rope_sum(nc.gpsimd, pair, half)
-            else:
-                rope_sum(nc.vector, pair, half)
-
-        groups = {}
-        for pair in range(PAIRS):
-            for b in range(B):
-                if pair > 0 or b < 2:
-                    groups.setdefault(PASSES * (pair + 1) + b, []).append((pair, b))
-        for b in (2, 3):
-            groups[2 * PASSES + b - 2].append((0, b))
-
-        cast_first(0, nc.vector.tensor_copy)
-        cast_first(1, nc.scalar.copy)
-        cast_first(3, nc.scalar.copy)
-        cast_pair(1)
-        transpose_weights_upto(0)
-        transpose_x(0)
-        transpose_weights_upto(1)
-        transpose_x(1)
-
-        fresh = []
-        for k in range(BANKS + PASSES):
-            i, g = divmod(k, PASSES)
-            draining = k >= BANKS
-
-            if by_scalar(k + SCALAR_AHEAD):
-                scalar_scale(k + SCALAR_AHEAD)
-
-            if not draining and not by_scalar(k):
-                vector_scale(k)
-            if g == 0:
-                if next_is(SUM):
-                    vector_piece()
-                if i >= 1:
-                    quantize(i - 1, work, "w")
-            if k == 0:
-                cast_first(2, nc.vector.tensor_copy)
-                transpose_weights_upto(2)
-                cast_pair(2)
-            if k == 2:
-                make_table()
-            if g == 0 and 1 <= i <= 2:
-                quantize("x%d" % (i - 1), const, "x%d" % (i - 1))
-            if g == 0 and for_gpsimd:
-                gpsimd_burst("x1" if i == 2 else i - 1)
-            if k < X_BANKS:
-                copy_x(k)
-
-            for unit, its_pieces in fresh:
-                if unit + PRODUCT_LAG <= k or draining:
-                    pieces.extend(its_pieces)
-            fresh = [item for item in fresh if not (item[0] + PRODUCT_LAG <= k or draining)]
-            if draining:
-                for n in range(pieces_left()):
-                    vector_piece()
-            elif (g != 0 or by_scalar(k)) and next_is(PRODUCT):
-                vector_piece()
-                if pieces_left() > 1 and next_is(PRODUCT):
-                    vector_piece()
-
-            if k + 2 < X_BANKS:
-                transpose_x(k + 2)
-                transpose_weights_upto(k + 3)
-            elif k + 2 == X_BANKS:
-                transpose_weights_upto(k + TRANSPOSE_BANKS - 1)
-            else:
-                transpose_weights_upto(k + TRANSPOSE_BANKS)
-            for pair, b in groups.get(k, []):
-                matmuls(pair, b)
-                if b % 2 == 1:
-                    half = b // 2
-                    way = rope_way(pair, half)
-                    if way == BY_GPSIMD:
-                        copy_sums(pair, half)
-                        for_gpsimd.append((pair, half))
-                    elif way == SUM_ON_GPSIMD:
-                        fresh.append((k, [(PRODUCT, pair, half)]))
+        item("G", ("table_b",), [("table_a",)], make_table_gpsimd)
+        for p in GC:
+            for it in add_widen("G", p, True):
+                item(*it)
+        for key, work_ in [("x1", [(0, 0)]), (2, [(1, 0), (0, 1)]), (3, [(2, 0), (1, 1), (2, 1)])] + [(i - 1, [(i - 2, 0), (i - 2, 1)]) for i in range(5, PAIRS)]:
+            add_fence(key)
+            for pair, half in work_:
+                if MERGE and way(pair, 0) == G_ALL and way(pair, 1) == V_PRODUCT and pair >= 2:
+                    if half == 0:
+                        add_product("G", pair_key(pair, 0))
                     else:
-                        fresh.append((k, [(PRODUCT, pair, half), (SUM, pair, half)]))
+                        add_sum("G", (pair, 0, B), 0, B)
+                    continue
+                w_ = way(pair, half)
+                pk = pair_key(pair, half)
+                if w_ == G_ALL:
+                    add_product("G", pk)
+                    add_sum("G", pk, 2 * half, 2)
+                elif w_ == V_PRODUCT:
+                    add_sum("G", pk, 2 * half, 2)
+                elif w_ == V_PRODUCT_HALF_SUM:
+                    add_sum("G", pk, 2 * half + 1, 1)
+        for half in range(2):
+            pk = pair_key(last - 1, half)
+            if way(last - 1, half) == G_ALL:
+                add_product("G", pk)
+            if way(last - 1, half) != V_ALL:
+                add_sum("G", pk, 2 * half, 2)
+        add_sum("G", (last, 0, 1), 0, 1)
+        add_sum("G", (last, 1, 1), 1, 1)
 
-            if g == 2 and CAST_AHEAD <= i + CAST_AHEAD < PAIRS:
-                cast_pair(i + CAST_AHEAD)
+        for what, k in HEAD_T:
+            if what == "w":
+                add_transpose_w(k)
+            elif what == "x":
+                add_transpose_x(k)
+            else:
+                add_matmuls((0, 0, 2), k)
+        groups = {8: [(1, 0), (0, 2)], 9: [(1, 1), (0, 3)], 10: [(1, 2)], 11: [(1, 3)]}
+        for pair in range(2, last):
+            for b in range(B):
+                groups.setdefault(PASSES * (pair + 1) + b, []).append((pair, b))
+        next_w = HEAD_W
+        for k in range(7, BANKS + PASSES):
+            for w in range(next_w, min(k + ahead(k), BANKS - 1) + 1):
+                add_transpose_w(w)
+                next_w = w + 1
+            for pair, b in groups.get(k, []):
+                add_matmuls((pair, 2 * (b // 2), 2), b)
+        for g0 in (0, 2):
+            for b in range(B):
+                add_matmuls((last, b, 1), b, g0, g0 + 2)
 
-        for unit, its_pieces in fresh:
-            pieces.extend(its_pieces)
-        for n in range(pieces_left()):
-            vector_piece()
+        sq = []
+        def s_first(g):
+            item("S", ("first_wide", g), [], lambda: cast_first(g, nc.scalar.copy))
+        def s_items(l):
+            for p in l:
+                item(*p)
+        s_first(2)
+        s_first(3)
+        pieces_of = {p: add_widen("S", p, p in HALF_CAST) for p in range(1, PAIRS) if p not in GC}
+        for what in HEAD_S:
+            if what == "sin":
+                item("S", ("table",), [("table_b",)], make_sin)
+            elif what[0] == "x":
+                add_copy_x(what[1])
+            elif what[0] == "c":
+                item(*pieces_of[what[1]][what[2]])
+            elif what[0] == "s":
+                add_copy_sums(pair_key(what[1], 0))
+        for p in range(S_FROM, PAIRS):
+            ps = pieces_of[p]
+            for n in range(len(ps)):
+                sq.append((PASSES * p - cast_lead(p) + 2 * n, 2, lambda p_=ps[n]: item(*p_)))
+        for k in SCALED_BY_SCALAR:
+            sq.append((k - 2, 0, lambda k=k: add_empty_w("S", k)))
+        for pair in range(1, last):
+            for half in range(2):
+                if way(pair, half) == G_ALL:
+                    u = PASSES * (pair + 1) + 2 + 2 * half
+                    sq.append((u, 1, lambda pair=pair, half=half: add_copy_sums(pair_key(pair, half))))
+        for u, o, f in sorted(sq, key=lambda e: e[0:2]):
+            f()
+
+        emit_all()

@@ -38,15 +38,15 @@ BY_GPSIMD = 2
 BYTES_BUFS = 12
 HALF_CAST = (1, 2, 3)
 SCALE_FIRST = ()
-SCALED_BY_SCALAR = (24, 32, 40, 48, 56, 60, 62, 63)
+SCALED_BY_SCALAR = (16, 24, 32, 40, 48, 56, 60, 61, 62, 63)
 G_ALL, V_PRODUCT, V_PRODUCT_HALF_SUM, V_ALL = range(4)
 XS = (4, 5, 6, 7)
 WHOLE_CAST = 99
 MERGE = False
 S_FROM = 4
 HEAD_W = 9
-HEAD_T = [("w", 0), ("x", 0), ("w", 1), ("x", 1), ("w", 2), ("x", 2), ("w", 3), ("x", 3), ("w", 4), ("x", 4), ("w", 5), ("x", 5), ("w", 6), ("m", 0), ("w", 7), ("x", 6), ("m", 1), ("w", 8), ("x", 7)]
-HEAD_S = [("c", 1, 0), ("c", 1, 1), ("c", 1, 2), ("c", 1, 3), ("x", 4), ("c", 2, 0), ("c", 2, 1), ("x", 5), ("c", 2, 2), ("c", 2, 3), ("x", 6), ("x", 7), "sin", ("s", 0)]
+HEAD_T = [("w", 0), ("x", 0), ("w", 1), ("x", 1), ("w", 2), ("x", 2), ("w", 3), ("x", 3), ("w", 4), ("x", 4), ("w", 5), ("x", 5), ("w", 6), ("w", 7), ("x", 6), ("m", 0), ("w", 8), ("m", 1), ("x", 7)]
+HEAD_S = [("c", 1, 0), ("c", 1, 1), ("c", 1, 2), ("c", 1, 3), ("x", 4), ("x", 5), ("c", 3, 0), ("c", 3, 1), ("x", 6), ("c", 3, 2), ("c", 3, 3), ("x", 7), "sin", ("s", 0)]
 
 
 def ahead(k):
@@ -63,7 +63,8 @@ def way(pair, half):
     if any(k in SCALED_BY_SCALAR for k in range(PASSES * (pair + 2) + 1, PASSES * (pair + 3) + 1)):
         return V_ALL
     return V_PRODUCT
-GC = (3,)
+GC = (2,)
+G_TABLE = 4
 
 def tile_multiheadselfattention_pa_kernel(tc, x, w_qk_bytes, w_qk_scale, out_0, out_1):
     nc = tc.nc
@@ -166,8 +167,9 @@ def tile_multiheadselfattention_pa_kernel(tc, x, w_qk_bytes, w_qk_scale, out_0, 
             item("load", ("bytes", i), [], lambda: load_pair(i), [("bytes", BYTES_BUFS, ("widened", i))])
 
         add_load_pair(1)
+        add_load_pair(2)
         item("load", ("second_x",), [], load_second_x)
-        for i in range(2, PAIRS):
+        for i in range(3, PAIRS):
             add_load_pair(i)
 
 
@@ -255,11 +257,12 @@ def tile_multiheadselfattention_pa_kernel(tc, x, w_qk_bytes, w_qk_scale, out_0, 
         widened_left = {}
 
         def add_widen(engine, i, halves):
-            parts = [(h, r) for h in range(2) for r in range(2)] if halves else [(None, r) for r in ((0, 1) if i < WHOLE_CAST else (2,))]
+            cuts = 4 if engine == "G" else 2
+            parts = [(h, r) for h in range(cuts) for r in range(2)] if halves else [(None, r) for r in ((0, 1) if i < WHOLE_CAST else (2,))]
             widened_left[i] = len(parts)
             out = []
             for h, r in parts:
-                k0, k1 = (0, D) if h is None else (D // 2 * h, D // 2 * (h + 1))
+                k0, k1 = (0, D) if h is None else (D // cuts * h, D // cuts * (h + 1))
                 first = (h in (None, 0)) and r in (0, 2)
                 out.append((engine, ("wide", i, h, r), [("bytes", i)] + ([("scale_rows", h)] if engine == "V" else []),
                             lambda r=r, k0=k0, k1=k1: widen_piece(i, r, k0, k1, engine),
@@ -291,6 +294,8 @@ def tile_multiheadselfattention_pa_kernel(tc, x, w_qk_bytes, w_qk_scale, out_0, 
             i, g = divmod(k, PASSES)
             if i == 0:
                 needs = [("first_wide", g)]
+            elif i in GC:
+                needs = [("wide", i, g, r) for r in range(2)]
             elif i in HALF_CAST:
                 needs = [("wide", i, g // 2, r) for r in range(2)]
             else:
@@ -487,9 +492,9 @@ def tile_multiheadselfattention_pa_kernel(tc, x, w_qk_bytes, w_qk_scale, out_0, 
         add_quantize("x1")
         for k in (9, 10, 11):
             add_empty_w("V", k)
-        add_product("V", pair_key(0, 1))
         add_empty_w("V", 12)
         add_quantize(2)
+        add_product("V", pair_key(0, 1))
         add_empty_w("V", 13)
         add_product("V", pair_key(1, 1))
         add_empty_w("V", 14)
@@ -521,9 +526,10 @@ def tile_multiheadselfattention_pa_kernel(tc, x, w_qk_bytes, w_qk_scale, out_0, 
         add_sum("V", (last, 2, 1), 2, 1)
         add_sum("V", (last, 3, 1), 3, 1)
 
-        item("G", ("table_b",), [("table_a",)], make_table_gpsimd)
         for p in GC:
-            for it in add_widen("G", p, True):
+            for n, it in enumerate(add_widen("G", p, True)):
+                if p == GC[0] and n == G_TABLE:
+                    item("G", ("table_b",), [("table_a",)], make_table_gpsimd)
                 item(*it)
         for key, work_ in [("x1", [(0, 0)]), (2, [(1, 0), (0, 1)]), (3, [(2, 0), (1, 1), (2, 1)])] + [(i - 1, [(i - 2, 0), (i - 2, 1)]) for i in range(5, PAIRS)]:
             add_fence(key)

@@ -36,21 +36,21 @@ BY_GPSIMD = 2
 
 
 BYTES_BUFS = 12
-HALF_CAST = (1, 2, 3)
+PIECES = {1: [("S", 0, 2), ("S", 2, 4)], 2: [("G", 0, 1), ("G", 1, 2), ("G", 2, 3), ("G", 3, 4)], 3: [("S", 0, 2), ("S", 2, 4)]}
 SCALE_FIRST = ()
 SCALED_BY_SCALAR = (16, 24, 32, 40, 48, 56, 60, 61, 62, 63)
 G_ALL, V_PRODUCT, V_PRODUCT_HALF_SUM, V_ALL = range(4)
-XS = (4, 5, 6, 7)
-WHOLE_CAST = 99
+XS = (2, 3, 4, 5, 6, 7)
 MERGE = False
 S_FROM = 4
 HEAD_W = 9
 HEAD_T = [("w", 0), ("x", 0), ("w", 1), ("x", 1), ("w", 2), ("x", 2), ("w", 3), ("x", 3), ("w", 4), ("x", 4), ("w", 5), ("x", 5), ("w", 6), ("w", 7), ("x", 6), ("m", 0), ("w", 8), ("m", 1), ("x", 7)]
-HEAD_S = [("c", 1, 0), ("c", 1, 1), ("c", 1, 2), ("c", 1, 3), ("x", 4), ("x", 5), ("c", 3, 0), ("c", 3, 1), ("x", 6), ("c", 3, 2), ("c", 3, 3), ("x", 7), "sin", ("s", 0)]
+HEAD_S = [("c", 1, 0), ("c", 1, 1), ("x", 2), ("x", 3), ("x", 4), ("x", 5), ("c", 3, 0), ("x", 6), ("c", 3, 1), ("x", 7), "sin", ("s", 0)]
+HEAD_G = ["table", (2, 0), (2, 1), (2, 2), (2, 3)]
 
 
 def ahead(k):
-    return 5
+    return 4
 
 
 def cast_lead(p):
@@ -63,8 +63,8 @@ def way(pair, half):
     if any(k in SCALED_BY_SCALAR for k in range(PASSES * (pair + 2) + 1, PASSES * (pair + 3) + 1)):
         return V_ALL
     return V_PRODUCT
-GC = (2,)
-G_TABLE = 4
+WHOLE_CAST = 6
+TABLE_AT = 0
 
 def tile_multiheadselfattention_pa_kernel(tc, x, w_qk_bytes, w_qk_scale, out_0, out_1):
     nc = tc.nc
@@ -138,12 +138,8 @@ def tile_multiheadselfattention_pa_kernel(tc, x, w_qk_bytes, w_qk_scale, out_0, 
         load_first_bytes(0)
         load_first_bytes(1)
         nc.sync.dma_start(out=scale[:], in_=w_qk_scale.rearrange("o (g p t) -> p (o g) t", p=P, t=PACK))
-        load_first_x(0)
         load_first_bytes(2)
-        load_first_x(1)
         load_first_bytes(3)
-        load_first_x(2)
-        load_first_x(3)
 
         pair_bytes = {}
         second_x = const.tile([P, 2, D], BF16, name="second_x")
@@ -166,10 +162,15 @@ def tile_multiheadselfattention_pa_kernel(tc, x, w_qk_bytes, w_qk_scale, out_0, 
         def add_load_pair(i):
             item("load", ("bytes", i), [], lambda: load_pair(i), [("bytes", BYTES_BUFS, ("widened", i))])
 
+        item("load", ("first_x", 0), [], lambda: load_first_x(0))
         add_load_pair(1)
+        item("load", ("first_x", 1), [], lambda: load_first_x(1))
         add_load_pair(2)
+        item("load", ("first_x", 2), [], lambda: load_first_x(2))
+        item("load", ("first_x", 3), [], lambda: load_first_x(3))
         item("load", ("second_x",), [], load_second_x)
-        for i in range(3, PAIRS):
+        add_load_pair(3)
+        for i in range(4, PAIRS):
             add_load_pair(i)
 
 
@@ -194,7 +195,7 @@ def tile_multiheadselfattention_pa_kernel(tc, x, w_qk_bytes, w_qk_scale, out_0, 
                                 op0=ALU.mult, op1=ALU.mult)
         arg = const.tile([P, 2, HD // 2, 2], F32, name="arg")
         for e in range(2):
-            nc.gpsimd.tensor_scalar(out=arg[:, 0, :, e], in0=turns[:], scalar1=0.25, scalar2=None, op0=ALU.add)
+            nc.gpsimd.tensor_scalar(out=arg[:, 0, :, e], in0=turns[:], scalar1=1.0, scalar2=0.25, op0=ALU.mult, op1=ALU.add)
             nc.gpsimd.tensor_copy(out=arg[:, 1, :, e], in_=turns[:])
         arg_flat = arg[:].rearrange("p a j e -> p (a j e)")
         whole = const.tile([P, 2 * HD], I32, name="whole")
@@ -208,11 +209,11 @@ def tile_multiheadselfattention_pa_kernel(tc, x, w_qk_bytes, w_qk_scale, out_0, 
             nc.vector.tensor_tensor(out=frac[:], in0=arg_flat, in1=whole[:], op=ALU.subtract)
 
         def make_table_gpsimd():
-            nc.gpsimd.tensor_scalar(out=over[:], in0=frac[:], scalar1=0.5, scalar2=None, op0=ALU.is_gt)
+            nc.gpsimd.tensor_scalar(out=over[:], in0=frac[:], scalar1=0.5, scalar2=1.0, op0=ALU.is_gt, op1=ALU.mult)
             nc.gpsimd.tensor_tensor(out=near[:].rearrange("p a j e -> p (a j e)"), in0=frac[:], in1=over[:],
                                     op=ALU.subtract)
-            nc.gpsimd.tensor_scalar(out=near[:, 1, :, 1], in0=near[:, 1, :, 1], scalar1=-1.0, scalar2=None,
-                                    op0=ALU.mult)
+            nc.gpsimd.tensor_scalar(out=near[:, 1, :, 1], in0=near[:, 1, :, 1], scalar1=-1.0, scalar2=0.0,
+                                    op0=ALU.mult, op1=ALU.add)
 
         def make_sin():
             for a in range(2):
@@ -256,18 +257,16 @@ def tile_multiheadselfattention_pa_kernel(tc, x, w_qk_bytes, w_qk_scale, out_0, 
 
         widened_left = {}
 
-        def add_widen(engine, i, halves):
-            cuts = 4 if engine == "G" else 2
-            parts = [(h, r) for h in range(cuts) for r in range(2)] if halves else [(None, r) for r in ((0, 1) if i < WHOLE_CAST else (2,))]
-            widened_left[i] = len(parts)
-            out = []
-            for h, r in parts:
-                k0, k1 = (0, D) if h is None else (D // cuts * h, D // cuts * (h + 1))
-                first = (h in (None, 0)) and r in (0, 2)
-                out.append((engine, ("wide", i, h, r), [("bytes", i)] + ([("scale_rows", h)] if engine == "V" else []),
-                            lambda r=r, k0=k0, k1=k1: widen_piece(i, r, k0, k1, engine),
-                            [("wide", 4, ("transposed", i))] if first else None))
-            return out
+        def pieces_of(i):
+            return PIECES.get(i, [("S", 0, PASSES)])
+
+        def add_widen(i, n):
+            engine, g0, g1 = pieces_of(i)[n]
+            rows = (2,) if i >= WHOLE_CAST else (0, 1)
+            widened_left[i] = len(rows) * len(pieces_of(i))
+            for r in rows:
+                item(engine, ("wide", i, g0, r), [("bytes", i)],
+                     lambda r=r: widen_piece(i, r, K_PASS * g0, K_PASS * g1, engine), [("wide", 4, ("transposed", i))])
 
         def transposes(src, g):
             bank = psum_t.tile([P, 2, PAIR_ROWS], F32, name="bank", tag="bank")
@@ -294,12 +293,8 @@ def tile_multiheadselfattention_pa_kernel(tc, x, w_qk_bytes, w_qk_scale, out_0, 
             i, g = divmod(k, PASSES)
             if i == 0:
                 needs = [("first_wide", g)]
-            elif i in GC:
-                needs = [("wide", i, g, r) for r in range(2)]
-            elif i in HALF_CAST:
-                needs = [("wide", i, g // 2, r) for r in range(2)]
             else:
-                needs = [("wide", i, None, r) for r in ((0, 1) if i < WHOLE_CAST else (2,))]
+                needs = [("wide", i, g0, r) for e_, g0, g1 in pieces_of(i) if g0 <= g < g1 for r in ((2,) if i >= WHOLE_CAST else (0, 1))]
             item("T", ("w", k), needs, lambda: transpose_weights(k), [("bank", TRANSPOSE_BANKS, ("emptied_w", k))])
 
         def transpose_x(k):
@@ -466,9 +461,9 @@ def tile_multiheadselfattention_pa_kernel(tc, x, w_qk_bytes, w_qk_scale, out_0, 
 
         fence_word = const.tile([P, 1], U32, name="fence_word")
 
-        def add_fence(key):
-            item("G", ("fence", key), [("codes", key, 0)],
-                 lambda: nc.gpsimd.tensor_copy(out=fence_word[:], in_=codes[key][0][:, 0, 0:1]))
+        def add_fence(key, g0=0):
+            item("G", ("fence", key), [("codes", key, g0)],
+                 lambda: nc.gpsimd.tensor_copy(out=fence_word[:], in_=codes[key][0][:, g0, 0:1]))
 
         def pair_key(pair, half):
             return (pair, 2 * half, 2)
@@ -480,7 +475,7 @@ def tile_multiheadselfattention_pa_kernel(tc, x, w_qk_bytes, w_qk_scale, out_0, 
             if k not in XS:
                 add_copy_x(k, "V")
             add_empty_w("V", k + 1)
-            if k == 1:
+            if k == TABLE_AT:
                 item("V", ("table_a",), [], make_table)
         add_quantize("x0")
         add_quantize(0)
@@ -494,10 +489,10 @@ def tile_multiheadselfattention_pa_kernel(tc, x, w_qk_bytes, w_qk_scale, out_0, 
             add_empty_w("V", k)
         add_empty_w("V", 12)
         add_quantize(2)
-        add_product("V", pair_key(0, 1))
         add_empty_w("V", 13)
-        add_product("V", pair_key(1, 1))
+        add_product("V", pair_key(0, 1))
         add_empty_w("V", 14)
+        add_product("V", pair_key(1, 1))
         add_empty_w("V", 15)
         for i in range(4, PAIRS):
             for g in range(PASSES):
@@ -526,11 +521,11 @@ def tile_multiheadselfattention_pa_kernel(tc, x, w_qk_bytes, w_qk_scale, out_0, 
         add_sum("V", (last, 2, 1), 2, 1)
         add_sum("V", (last, 3, 1), 3, 1)
 
-        for p in GC:
-            for n, it in enumerate(add_widen("G", p, True)):
-                if p == GC[0] and n == G_TABLE:
-                    item("G", ("table_b",), [("table_a",)], make_table_gpsimd)
-                item(*it)
+        for what in HEAD_G:
+            if what == "table":
+                item("G", ("table_b",), [("table_a",)], make_table_gpsimd)
+            else:
+                add_widen(what[0], what[1])
         for key, work_ in [("x1", [(0, 0)]), (2, [(1, 0), (0, 1)]), (3, [(2, 0), (1, 1), (2, 1)])] + [(i - 1, [(i - 2, 0), (i - 2, 1)]) for i in range(5, PAIRS)]:
             add_fence(key)
             for pair, half in work_:
@@ -549,6 +544,7 @@ def tile_multiheadselfattention_pa_kernel(tc, x, w_qk_bytes, w_qk_scale, out_0, 
                     add_sum("G", pk, 2 * half, 2)
                 elif w_ == V_PRODUCT_HALF_SUM:
                     add_sum("G", pk, 2 * half + 1, 1)
+        add_fence(last, 2)
         for half in range(2):
             pk = pair_key(last - 1, half)
             if way(last - 1, half) == G_ALL:
@@ -588,20 +584,17 @@ def tile_multiheadselfattention_pa_kernel(tc, x, w_qk_bytes, w_qk_scale, out_0, 
                 item(*p)
         s_first(2)
         s_first(3)
-        pieces_of = {p: add_widen("S", p, p in HALF_CAST) for p in range(1, PAIRS) if p not in GC}
         for what in HEAD_S:
             if what == "sin":
                 item("S", ("table",), [("table_b",)], make_sin)
             elif what[0] == "x":
                 add_copy_x(what[1])
             elif what[0] == "c":
-                item(*pieces_of[what[1]][what[2]])
+                add_widen(what[1], what[2])
             elif what[0] == "s":
                 add_copy_sums(pair_key(what[1], 0))
         for p in range(S_FROM, PAIRS):
-            ps = pieces_of[p]
-            for n in range(len(ps)):
-                sq.append((PASSES * p - cast_lead(p) + 2 * n, 2, lambda p_=ps[n]: item(*p_)))
+            sq.append((PASSES * p - cast_lead(p), 2, lambda p=p: add_widen(p, 0)))
         for k in SCALED_BY_SCALAR:
             sq.append((k - 2, 0, lambda k=k: add_empty_w("S", k)))
         for pair in range(1, last):

@@ -24,103 +24,92 @@ K_PASS = P * PACK
 PASSES = D // K_PASS
 PAIR_ROWS = 2 * HD
 PAIRS = 2 * D // PAIR_ROWS
+LAST = PAIRS - 1
 BANKS = PAIRS * PASSES
 X_BANKS = 2 * PASSES
 
+BYTES_SLOTS = 12
+WIDE_SLOTS = 4
 TRANSPOSE_BANKS = 5
 SUM_BANKS = 3
+SUM_COPIES = 4
+PRODUCT_SLOTS = 3
+
+TENSOR_AHEAD = 4
+SCALAR_AHEAD = 2
+CAST_AHEAD = 3
+VECTOR_X_BANKS = 2
 
 BY_VECTOR = 0
 SUM_ON_GPSIMD = 1
 BY_GPSIMD = 2
 
 
-BYTES_BUFS = 12
-PIECES = {1: [("S", 0, 2), ("S", 2, 4)], 2: [("G", 0, 1), ("G", 1, 2), ("G", 2, 3), ("G", 3, 4)], 3: [("S", 0, 2), ("S", 2, 4)]}
-SCALE_FIRST = ()
-SCALED_BY_SCALAR = (16, 24, 32, 40, 48, 56, 60, 61, 62, 63)
-G_ALL, V_PRODUCT, V_PRODUCT_HALF_SUM, V_ALL = range(4)
-XS = (2, 3, 4, 5, 6, 7)
-MERGE = False
-S_FROM = 4
-HEAD_W = 9
-HEAD_T = [("w", 0), ("x", 0), ("w", 1), ("x", 1), ("w", 2), ("x", 2), ("w", 3), ("x", 3), ("w", 4), ("x", 4), ("w", 5), ("x", 5), ("w", 6), ("w", 7), ("x", 6), ("m", 0), ("w", 8), ("m", 1), ("x", 7)]
-HEAD_S = [("c", 1, 0), ("c", 1, 1), ("x", 2), ("x", 3), ("x", 4), ("x", 5), ("c", 3, 0), ("x", 6), ("c", 3, 1), ("x", 7), "sin", ("s", 0)]
-HEAD_G = ["table", (2, 0), (2, 1), (2, 2), (2, 3)]
+def by_scalar(k):
+    pair, g = divmod(k, PASSES)
+    return pair == LAST or (pair >= 4 and pair % 2 == 0 and g == 0)
 
 
-def ahead(k):
-    return 4
+def rope_way(pair, half):
+    if half == 1 and any(by_scalar(k) for k in range(PASSES * (pair + 2) + 1, PASSES * (pair + 3) + 1) if k < BANKS):
+        return BY_VECTOR
+    if half == 0 and pair < PAIRS - 3:
+        return BY_GPSIMD
+    return SUM_ON_GPSIMD
 
 
-def cast_lead(p):
-    return 10
+def cast_pieces(i):
+    if i in (1, 3):
+        return [("scalar", 0, 2), ("scalar", 2, 4)]
+    if i == 2:
+        return [("gpsimd", g, g + 1) for g in range(PASSES)]
+    return [("scalar", 0, PASSES)]
 
 
-def way(pair, half):
-    if half == 0:
-        return G_ALL if pair < 13 else V_PRODUCT
-    if any(k in SCALED_BY_SCALAR for k in range(PASSES * (pair + 2) + 1, PASSES * (pair + 3) + 1)):
-        return V_ALL
-    return V_PRODUCT
-WHOLE_CAST = 6
-TABLE_AT = 0
+def cast_row_tiles(i):
+    return ("both",) if i > 3 else (0, 1)
+
 
 def tile_multiheadselfattention_pa_kernel(tc, x, w_qk_bytes, w_qk_scale, out_0, out_1):
     nc = tc.nc
     with ExitStack() as ctx:
         const = ctx.enter_context(tc.tile_pool(name="const", bufs=1))
-        bytes_pool = ctx.enter_context(tc.tile_pool(name="bytes", bufs=12))
-        wide = ctx.enter_context(tc.tile_pool(name="wide", bufs=4))
+        bytes_pool = ctx.enter_context(tc.tile_pool(name="bytes", bufs=BYTES_SLOTS))
+        wide = ctx.enter_context(tc.tile_pool(name="wide", bufs=WIDE_SLOTS))
         work = ctx.enter_context(tc.tile_pool(name="work", bufs=4))
         psum_t = ctx.enter_context(tc.psum_pool(name="psum_t", bufs=TRANSPOSE_BANKS))
         psum_o = ctx.enter_context(tc.psum_pool(name="psum_o", bufs=SUM_BANKS))
         ctx.enter_context(tc.manual_schedule())
 
-        programs = {"load": [], "S": [], "V": [], "T": [], "G": []}
-        done = set()
-        rings = {}
+        lists = {"loads": [], "scalar": [], "vector": [], "tensor": [], "gpsimd": []}
+        written = set()
+        taken = {}
 
-        def ring_free(name, bufs, key):
-            r = rings.setdefault(name, [])
-            return key in r or len(r) < bufs or r[len(r) - bufs] in done
+        def job(engine, name, needs, write, slot=None):
+            lists[engine].append((name, needs, write, slot))
 
-        def ring_take(name, key):
-            if key not in rings[name]:
-                rings[name].append(key)
+        def slot_is_free(slot):
+            pool, slots, frees = slot
+            users = taken.setdefault(pool, [])
+            return frees in users or len(users) < slots or users[len(users) - slots] in written
 
-        def item(engine, name, needs, run, ring=None):
-            programs[engine].append((name, needs, run, ring))
-
-        def emit_all():
-            at = {e: 0 for e in programs}
-            moved = True
-            while_guard = 0
-            for round_ in range(100000):
-                moved = False
-                for e in programs:
-                    for n in range(len(programs[e])):
-                        if at[e] >= len(programs[e]):
+        def merge():
+            at = {engine: 0 for engine in lists}
+            for turn in range(sum(len(lists[engine]) for engine in lists)):
+                for engine in lists:
+                    for name, needs, write, slot in lists[engine][at[engine]:]:
+                        if not all(n in written for n in needs) or (slot is not None and not slot_is_free(slot)):
                             break
-                        name, needs, run, ring = programs[e][at[e]]
-                        if not all(x in done for x in needs):
-                            break
-                        if ring is not None and not all(ring_free(rn, rb, rk) for rn, rb, rk in ring):
-                            break
-                        if ring is not None:
-                            for rn, rb, rk in ring:
-                                ring_take(rn, rk)
-                        run()
-                        done.add(name)
-                        at[e] += 1
-                        moved = True
-                if not moved:
-                    break
-            stuck = [(e, programs[e][at[e]][0], programs[e][at[e]][3], [x for x in programs[e][at[e]][1] if x not in done]) for e in programs if at[e] < len(programs[e])]
-            assert not stuck, stuck
+                        if slot is not None and slot[2] not in taken[slot[0]]:
+                            taken[slot[0]].append(slot[2])
+                        write()
+                        written.add(name)
+                        at[engine] += 1
+            assert all(at[engine] == len(lists[engine]) for engine in lists), "the lists wait for each other"
 
         first_bytes = []
         first_x = []
+        pair_bytes = {}
         scale = const.tile([P, PASSES, PACK], F32, name="scale")
 
         def load_first_bytes(g):
@@ -141,9 +130,7 @@ def tile_multiheadselfattention_pa_kernel(tc, x, w_qk_bytes, w_qk_scale, out_0, 
         load_first_bytes(2)
         load_first_bytes(3)
 
-        pair_bytes = {}
         second_x = const.tile([P, 2, D], BF16, name="second_x")
-        scale_rows = const.tile([P, D], F32, name="scale_rows") if SCALE_FIRST else None
 
         def load_pair(i):
             t = bytes_pool.tile([P, 2, D], U8, name="pair_bytes%d" % i, tag="pair_bytes")
@@ -151,28 +138,14 @@ def tile_multiheadselfattention_pa_kernel(tc, x, w_qk_bytes, w_qk_scale, out_0, 
                               in_=w_qk_bytes[PAIR_ROWS * i:PAIR_ROWS * (i + 1), :].rearrange("(r p) k -> p r k", p=P))
             pair_bytes[i] = t
 
-        def load_scale_rows(h):
-            k_cols = slice(D // 2 * h, D // 2 * (h + 1))
-            nc.sync.dma_start(out=scale_rows[:, k_cols],
-                              in_=w_qk_scale[:, k_cols].rearrange("o k -> (o k)").partition_broadcast(P))
-
         def load_second_x():
             nc.sync.dma_start(out=second_x[:], in_=x[2:4].rearrange("b s k -> s b k"))
 
-        def add_load_pair(i):
-            item("load", ("bytes", i), [], lambda: load_pair(i), [("bytes", BYTES_BUFS, ("widened", i))])
+        def job_load_pair(i):
+            job("loads", ("bytes", i), [], lambda: load_pair(i), ("bytes", BYTES_SLOTS, ("pair is cast", i)))
 
-        item("load", ("first_x", 0), [], lambda: load_first_x(0))
-        add_load_pair(1)
-        item("load", ("first_x", 1), [], lambda: load_first_x(1))
-        add_load_pair(2)
-        item("load", ("first_x", 2), [], lambda: load_first_x(2))
-        item("load", ("first_x", 3), [], lambda: load_first_x(3))
-        item("load", ("second_x",), [], load_second_x)
-        add_load_pair(3)
-        for i in range(4, PAIRS):
-            add_load_pair(i)
-
+        def job_load_first_x(g):
+            job("loads", ("first_x", g), [], lambda: load_first_x(g))
 
         warm = const.tile([P, 2], F32, name="warm")
         nc.gpsimd.memset(warm[:, 0:1], 0.0)
@@ -195,7 +168,8 @@ def tile_multiheadselfattention_pa_kernel(tc, x, w_qk_bytes, w_qk_scale, out_0, 
                                 op0=ALU.mult, op1=ALU.mult)
         arg = const.tile([P, 2, HD // 2, 2], F32, name="arg")
         for e in range(2):
-            nc.gpsimd.tensor_scalar(out=arg[:, 0, :, e], in0=turns[:], scalar1=1.0, scalar2=0.25, op0=ALU.mult, op1=ALU.add)
+            nc.gpsimd.tensor_scalar(out=arg[:, 0, :, e], in0=turns[:], scalar1=1.0, scalar2=0.25, op0=ALU.mult,
+                                    op1=ALU.add)
             nc.gpsimd.tensor_copy(out=arg[:, 1, :, e], in_=turns[:])
         arg_flat = arg[:].rearrange("p a j e -> p (a j e)")
         whole = const.tile([P, 2 * HD], I32, name="whole")
@@ -204,18 +178,18 @@ def tile_multiheadselfattention_pa_kernel(tc, x, w_qk_bytes, w_qk_scale, out_0, 
         near = const.tile([P, 2, HD // 2, 2], F32, name="near")
         table = const.tile([P, 2, 4, HD], F32, name="table")
 
-        def make_table():
+        def take_off_turns():
             nc.vector.tensor_copy(out=whole[:], in_=arg_flat)
             nc.vector.tensor_tensor(out=frac[:], in0=arg_flat, in1=whole[:], op=ALU.subtract)
 
-        def make_table_gpsimd():
+        def bring_near_zero():
             nc.gpsimd.tensor_scalar(out=over[:], in0=frac[:], scalar1=0.5, scalar2=1.0, op0=ALU.is_gt, op1=ALU.mult)
             nc.gpsimd.tensor_tensor(out=near[:].rearrange("p a j e -> p (a j e)"), in0=frac[:], in1=over[:],
                                     op=ALU.subtract)
             nc.gpsimd.tensor_scalar(out=near[:, 1, :, 1], in0=near[:, 1, :, 1], scalar1=-1.0, scalar2=0.0,
                                     op0=ALU.mult, op1=ALU.add)
 
-        def make_sin():
+        def make_table():
             for a in range(2):
                 nc.scalar.activation(out=table[:, a],
                                      in_=near[:, a].rearrange("p j e -> p (j e)").unsqueeze(1).to_broadcast([P, 4, HD]),
@@ -223,6 +197,7 @@ def tile_multiheadselfattention_pa_kernel(tc, x, w_qk_bytes, w_qk_scale, out_0, 
 
         first_wide = {}
         pair_wide = {}
+        pieces_left = {}
         w_bank = {}
         x_bank = {}
         grouped = {}
@@ -234,39 +209,31 @@ def tile_multiheadselfattention_pa_kernel(tc, x, w_qk_bytes, w_qk_scale, out_0, 
                  in_=first_bytes[g][:].rearrange("p r k -> p (r k)").bitcast(FP8))
             first_wide[g] = t
 
-        def need_wide(i):
+        def job_cast_first(engine, g):
+            copy = nc.vector.tensor_copy if engine == "vector" else nc.scalar.copy
+            job(engine, ("first_wide", g), [], lambda: cast_first(g, copy))
+
+        def cast_piece(engine, i, row_tile, k_cols):
             if i not in pair_wide:
                 pair_wide[i] = wide.tile([P, 2, D], BF16, name="pair_wide%d" % i, tag="pair_wide")
-
-        def widen_piece(i, r, k0, k1, engine):
-            need_wide(i)
-            if r == 2:
+            if row_tile == "both":
                 out = pair_wide[i][:].rearrange("p r k -> p (r k)")
                 in_ = pair_bytes[i][:].rearrange("p r k -> p (r k)").bitcast(FP8)
             else:
-                out, in_ = pair_wide[i][:, r, k0:k1], pair_bytes[i][:, r, k0:k1].bitcast(FP8)
-            if engine == "G":
-                nc.gpsimd.tensor_copy(out=out, in_=in_)
-            elif engine == "V":
-                nc.vector.tensor_tensor(out=out, in0=in_, in1=scale_rows[:, k0:k1], op=ALU.mult)
-            else:
-                nc.scalar.copy(out=out, in_=in_)
-            widened_left[i] -= 1
-            if widened_left[i] == 0:
-                done.add(("widened", i))
+                out, in_ = pair_wide[i][:, row_tile, k_cols], pair_bytes[i][:, row_tile, k_cols].bitcast(FP8)
+            copy = nc.gpsimd.tensor_copy if engine == "gpsimd" else nc.scalar.copy
+            copy(out=out, in_=in_)
+            pieces_left[i] -= 1
+            if pieces_left[i] == 0:
+                written.add(("pair is cast", i))
 
-        widened_left = {}
-
-        def pieces_of(i):
-            return PIECES.get(i, [("S", 0, PASSES)])
-
-        def add_widen(i, n):
-            engine, g0, g1 = pieces_of(i)[n]
-            rows = (2,) if i >= WHOLE_CAST else (0, 1)
-            widened_left[i] = len(rows) * len(pieces_of(i))
-            for r in rows:
-                item(engine, ("wide", i, g0, r), [("bytes", i)],
-                     lambda r=r: widen_piece(i, r, K_PASS * g0, K_PASS * g1, engine), [("wide", 4, ("transposed", i))])
+        def job_cast(i, piece):
+            engine, g0, g1 = cast_pieces(i)[piece]
+            pieces_left[i] = len(cast_row_tiles(i)) * len(cast_pieces(i))
+            for r in cast_row_tiles(i):
+                job(engine, ("wide", i, g0, r), [("bytes", i)],
+                    lambda r=r: cast_piece(engine, i, r, slice(K_PASS * g0, K_PASS * g1)),
+                    ("wide", WIDE_SLOTS, ("w", PASSES * i + PASSES - 1)))
 
         def transposes(src, g):
             bank = psum_t.tile([P, 2, PAIR_ROWS], F32, name="bank", tag="bank")
@@ -277,332 +244,297 @@ def tile_multiheadselfattention_pa_kernel(tc, x, w_qk_bytes, w_qk_scale, out_0, 
                                         words[:, r, K_PASS // 2 * g + u:K_PASS // 2 * (g + 1):2], ident[:])
             return bank
 
-        transposed_left = {}
-
         def transpose_weights(k):
-            i = k // PASSES
-            if i == 0:
-                w_bank[k] = transposes(first_wide[k], 0)
-            else:
-                w_bank[k] = transposes(pair_wide[i], k % PASSES)
-            transposed_left[i] = transposed_left.get(i, PASSES) - 1
-            if transposed_left[i] == 0:
-                done.add(("transposed", i))
+            i, g = divmod(k, PASSES)
+            w_bank[k] = transposes(first_wide[g], 0) if i == 0 else transposes(pair_wide[i], g)
 
-        def add_transpose_w(k):
+        def transpose_x(k):
+            x_bank[k] = transposes(first_x[k], 0) if k < PASSES else transposes(second_x, k % PASSES)
+
+        def job_transpose_w(k):
             i, g = divmod(k, PASSES)
             if i == 0:
                 needs = [("first_wide", g)]
             else:
-                needs = [("wide", i, g0, r) for e_, g0, g1 in pieces_of(i) if g0 <= g < g1 for r in ((2,) if i >= WHOLE_CAST else (0, 1))]
-            item("T", ("w", k), needs, lambda: transpose_weights(k), [("bank", TRANSPOSE_BANKS, ("emptied_w", k))])
+                needs = [("wide", i, g0, r) for engine, g0, g1 in cast_pieces(i) if g0 <= g < g1
+                         for r in cast_row_tiles(i)]
+            job("tensor", ("w", k), needs, lambda: transpose_weights(k),
+                ("transposes", TRANSPOSE_BANKS, ("w is emptied", k)))
 
-        def transpose_x(k):
-            if k < PASSES:
-                x_bank[k] = transposes(first_x[k], 0)
-            else:
-                x_bank[k] = transposes(second_x, k % PASSES)
+        def job_transpose_x(k):
+            job("tensor", ("x", k), [("first_x", k) if k < PASSES else ("second_x",)], lambda: transpose_x(k),
+                ("transposes", TRANSPOSE_BANKS, ("x is emptied", k)))
 
-        def add_transpose_x(k):
-            item("T", ("x", k), [("second_x",)] if k >= PASSES else [], lambda: transpose_x(k),
-                 [("bank", TRANSPOSE_BANKS, ("emptied_x", k))])
-
-        def need_grouped(key):
+        def grouped_tile(key):
             if key not in grouped:
-                grouped[key] = work.tile([P, PASSES, PAIR_ROWS, PACK], BF16, name="grouped", tag="grouped", align_bytes=64)
+                grouped[key] = work.tile([P, PASSES, PAIR_ROWS, PACK], BF16, name="grouped", tag="grouped",
+                                         align_bytes=64)
+            return grouped[key]
 
         def vector_scale(k):
             i, g = divmod(k, PASSES)
-            need_grouped(i)
             nc.vector.tensor_tensor(
-                out=grouped[i][:, g].rearrange("p n (u e) -> p n u e", e=2),
+                out=grouped_tile(i)[:, g].rearrange("p n (u e) -> p n u e", e=2),
                 in0=w_bank[k][:].bitcast(BF16).rearrange("p u (n e) -> p n u e", e=2),
                 in1=scale[:, g, :].rearrange("p (u e) -> p u e", e=2).unsqueeze(1).to_broadcast([P, PAIR_ROWS, 2, 2]),
                 op=ALU.mult)
 
         def scalar_scale(k):
             i, g = divmod(k, PASSES)
-            need_grouped(i)
+            out = grouped_tile(i)[:, g]
             planes = work.tile([P, PACK, PAIR_ROWS], BF16, name="planes", tag="planes", bufs=2)
             src = w_bank[k][:].bitcast(BF16).rearrange("p u (n e) -> p u n e", e=2)
             for t in range(PACK):
                 nc.scalar.activation(out=planes[:, t, :], in_=src[:, t // 2, :, t % 2], func=ACT.Copy,
                                      scale=scale[:, g, t:t + 1])
-            nc.scalar.copy(out=grouped[i][:, g].rearrange("p (c i) t -> p c t i", i=4),
+            nc.scalar.copy(out=out.rearrange("p (c i) t -> p c t i", i=4),
                            in_=planes[:].rearrange("p t (c i) -> p c t i", i=4))
 
-        def copy_bank(copy, key, g, bank):
-            need_grouped(key)
-            copy(
-                out=grouped[key][:, g].rearrange("p n t -> p (n t)").bitcast(F32).rearrange("p (n u) -> p n u", u=2),
-                in_=bank[:].rearrange("p u n -> p n u"))
-
-        def add_empty_w(engine, k):
-            i, g = divmod(k, PASSES)
-            if engine == "V":
-                run = lambda: vector_scale(k)
-            elif i in SCALE_FIRST:
-                run = lambda: copy_bank(nc.scalar.copy, i, g, w_bank[k])
+        def job_scale(k):
+            if by_scalar(k):
+                job("scalar", ("w is emptied", k), [("w", k)], lambda: scalar_scale(k))
             else:
-                run = lambda: scalar_scale(k)
-            item(engine, ("emptied_w", k), [("w", k)], run)
+                job("vector", ("w is emptied", k), [("w", k)], lambda: vector_scale(k))
 
-        def add_copy_x(k, engine="S"):
-            copy = nc.scalar.copy if engine == "S" else nc.vector.tensor_copy
-            item(engine, ("emptied_x", k), [("x", k)], lambda: copy_bank(copy, "x%d" % (k // PASSES), k % PASSES, x_bank[k]))
+        def empty_x(k, copy):
+            copy(out=grouped_tile("x%d" % (k // PASSES))[:, k % PASSES].rearrange("p n t -> p (n t)").bitcast(F32)
+                 .rearrange("p (n u) -> p n u", u=2),
+                 in_=x_bank[k][:].rearrange("p u n -> p n u"))
+
+        def job_empty_x(engine, k):
+            copy = nc.vector.tensor_copy if engine == "vector" else nc.scalar.copy
+            job(engine, ("x is emptied", k), [("x", k)], lambda: empty_x(k, copy))
 
         def quantize(key, pool, name, g0, g1):
             if key not in codes:
-                codes[key] = (pool.tile([P, PASSES, PAIR_ROWS], U32, name=name + "_codes", tag=name + "_codes", align_bytes=64),
-                              pool.tile([P, PASSES, PAIR_ROWS], U8, name=name + "_scales", tag=name + "_scales", align_bytes=64))
+                codes[key] = (pool.tile([P, PASSES, PAIR_ROWS], U32, name=name + "_codes", tag=name + "_codes",
+                                        align_bytes=64),
+                              pool.tile([P, PASSES, PAIR_ROWS], U8, name=name + "_scales", tag=name + "_scales",
+                                        align_bytes=64))
             c, s = codes[key]
             nc.vector.quantize_mx(out=c[:, g0:g1].rearrange("p g n -> p (g n)").bitcast(FP8X4),
                                   scales=s[:, g0:g1].rearrange("p g n -> p (g n)"),
                                   in_=grouped[key][:, g0:g1].rearrange("p g n t -> p (g n t)"))
 
-        def add_quantize(key, g0=0, g1=PASSES):
-            if isinstance(key, str):
-                needs = [("emptied_x", PASSES * int(key[1]) + g) for g in range(g0, g1)]
-                item("V", ("codes", key, g0), needs, lambda: quantize(key, const, key, g0, g1))
-            else:
-                needs = [("emptied_w", PASSES * key + g) for g in range(g0, g1)]
-                item("V", ("codes", key, g0), needs, lambda: quantize(key, work, "w", g0, g1))
+        def job_quantize_w(i, g0=0, g1=PASSES):
+            job("vector", ("codes", i, g0), [("w is emptied", PASSES * i + g) for g in range(g0, g1)],
+                lambda: quantize(i, work, "w", g0, g1))
 
-        sum_tile = {}
+        def job_quantize_x(half):
+            key = "x%d" % half
+            job("vector", ("codes", key, 0), [("x is emptied", PASSES * half + g) for g in range(PASSES)],
+                lambda: quantize(key, const, key, 0, PASSES))
+
         sums = {}
+        sum_tile = {}
         products = {}
         rotated = {}
+        batches_added = {}
 
-        def matmuls(key, b, g0, g1):
-            pair, b0, nb = key
-            if key not in sum_tile:
-                pool = psum_t if pair == PAIRS - 1 else psum_o
-                sum_tile[key] = pool.tile([P, 2, PAIR_ROWS], F32, name="bank" if pair == PAIRS - 1 else "sum_bank",
-                                          tag="bank" if pair == PAIRS - 1 else "sum_bank")
-                sums[key] = sum_tile[key][:, 0:nb].rearrange("p b n -> p (b n)")
+        def sum_bank(pair, half):
+            return (pair, 2 * half, 2)
+
+        def last_sum_bank(b):
+            return (LAST, b, 1)
+
+        def matmuls(bank, b, g0, g1):
+            pair, b0, n_batches = bank
+            if bank not in sum_tile:
+                if pair == LAST:
+                    sum_tile[bank] = psum_t.tile([P, 2, PAIR_ROWS], F32, name="bank", tag="bank")
+                else:
+                    sum_tile[bank] = psum_o.tile([P, 2, PAIR_ROWS], F32, name="sum_bank", tag="sum_bank")
+                sums[bank] = sum_tile[bank][:, 0:n_batches].rearrange("p b n -> p (b n)")
             w_codes, w_scales = codes[pair]
             x_codes, x_scales = codes["x%d" % (b // 2)]
-            bb = b % 2
+            positions = slice(P * (b % 2), P * (b % 2 + 1))
             for g in range(g0, g1):
-                nc.tensor.matmul_mx(out=sum_tile[key][:, b - b0, :],
-                                    lhsT=x_codes[:, g, P * bb:P * (bb + 1)].bitcast(FP8X4),
-                                    lhsT_scale=x_scales[:, g, P * bb:P * (bb + 1)],
+                nc.tensor.matmul_mx(out=sum_tile[bank][:, b - b0, :],
+                                    lhsT=x_codes[:, g, positions].bitcast(FP8X4),
+                                    lhsT_scale=x_scales[:, g, positions],
                                     rhs=w_codes[:, g, :].bitcast(FP8X4),
                                     rhs_scale=w_scales[:, g, :],
                                     start=(g == 0), stop=(g == PASSES - 1))
 
-        def add_matmuls(key, b, g0=0, g1=PASSES):
-            pair, b0, nb = key
-            ring = None
-            if b == b0 and g0 == 0:
-                ring = [("bank", TRANSPOSE_BANKS, ("read", key))] if pair == PAIRS - 1 else [("sums", SUM_BANKS, ("read", key))]
-            needs = [("codes", "x%d" % (b // 2), 0), ("codes", pair, g0 if pair == PAIRS - 1 else 0)]
-            item("T", ("mx", key, b, g1), needs, lambda: matmuls(key, b, g0, g1), ring)
+        def job_matmuls(bank, b, g0=0, g1=PASSES):
+            slot = None
+            if b == bank[1] and g0 == 0:
+                slot = (("transposes", TRANSPOSE_BANKS) if bank[0] == LAST else ("sums", SUM_BANKS)) + (("is read", bank),)
+            job("tensor", ("sums", bank, b, g1), [("codes", "x%d" % (b // 2), 0), ("codes", bank[0], g0)],
+                lambda: matmuls(bank, b, g0, g1), slot)
 
-        def summed(key):
-            return [("mx", key, b, PASSES) for b in range(key[1], key[1] + key[2])]
+        def is_summed(bank):
+            return [("sums", bank, b, PASSES) for b in range(bank[1], bank[1] + bank[2])]
 
-        def copy_sums(key):
+        def copy_sums(bank):
             t = work.tile([P, 2 * PAIR_ROWS], F32, name="sums_copy", tag="sums_copy")
-            nc.scalar.copy(out=t[:], in_=sums[key])
-            sums[key] = t[:]
+            nc.scalar.copy(out=t[:], in_=sums[bank])
+            sums[bank] = t[:]
 
-        def add_copy_sums(key):
-            item("S", ("read", key), summed(key), lambda: copy_sums(key), [("sums_copy", 4, ("product", key))])
+        def job_copy_sums(bank):
+            job("scalar", ("is read", bank), is_summed(bank), lambda: copy_sums(bank),
+                ("sums_copy", SUM_COPIES, ("product", bank)))
 
-        def rope_product(eng, key):
-            pair, b0, nb = key
-            cols = nb * PAIR_ROWS
+        def rope_product(eng, bank):
+            pair, b0, n_batches = bank
             if pair not in products:
-                products[pair] = work.tile([P, 2, 2, 2 * PAIR_ROWS], F32, name="products", tag="products", bufs=3)
-            at = PAIR_ROWS * (b0 % 2)
-            eng.tensor_tensor(out=products[pair][:, b0 // 2, :, at:at + cols], in0=sums[key].unsqueeze(1).to_broadcast([P, 2, cols]),
-                              in1=table[:, :, 0:2 * key[2]].rearrange("p a c d -> p a (c d)"), op=ALU.mult)
+                products[pair] = work.tile([P, 2, 2, 2 * PAIR_ROWS], F32, name="products", tag="products",
+                                           bufs=PRODUCT_SLOTS)
+            cols = n_batches * PAIR_ROWS
+            first = PAIR_ROWS * (b0 % 2)
+            eng.tensor_tensor(out=products[pair][:, b0 // 2, :, first:first + cols],
+                              in0=sums[bank].unsqueeze(1).to_broadcast([P, 2, cols]),
+                              in1=table[:, :, 0:2 * n_batches].rearrange("p a c d -> p a (c d)"), op=ALU.mult)
+            written.add(("is read", bank))
 
-        def add_product(engine, key):
-            def run():
-                rope_product(nc.vector if engine == "V" else nc.gpsimd, key)
-                done.add(("product", key))
-                done.add(("read", key))
-            item(engine, ("product", key), summed(key) + [("table",)] + ([("read", key)] if engine == "G" else []), run,
-                 [("products", 3, ("added", key[0]))])
+        def job_product(engine, bank):
+            eng = nc.vector if engine == "vector" else nc.gpsimd
+            needs = is_summed(bank) + [("table",)] + ([("is read", bank)] if engine == "gpsimd" else [])
+            job(engine, ("product", bank), needs, lambda: rope_product(eng, bank),
+                ("products", PRODUCT_SLOTS, ("pair is rotated", bank[0])))
 
-        added = {}
-
-        def rope_sum(eng, key, b, nb):
-            pair, b0, n_ = key
+        def rope_sum(eng, bank):
+            pair, b0, n_batches = bank
             if pair not in rotated:
                 rotated[pair] = work.tile([P, B, 2, HD], F32, name="rotated", tag="rotated")
-            if nb == B:
-                eng.tensor_tensor(out=rotated[pair][:].rearrange("p (q b) h (j e) -> p q (b h j) e", q=2, e=2),
-                                  in0=products[pair][:, :, 0].rearrange("p q (m e) -> p q m e", e=2),
-                                  in1=products[pair][:, :, 1].rearrange("p q (m e) -> p q m e", e=2)[:, :, :, ::-1],
-                                  op=ALU.add)
-            else:
-                cols = slice(PAIR_ROWS * (b % 2), PAIR_ROWS * (b % 2 + nb))
-                eng.tensor_tensor(out=rotated[pair][:, b:b + nb].rearrange("p b h (j e) -> p (b h j) e", e=2),
-                                  in0=products[pair][:, b // 2, 0, cols].rearrange("p (m e) -> p m e", e=2),
-                                  in1=products[pair][:, b // 2, 1, cols].rearrange("p (m e) -> p m e", e=2)[:, :, ::-1],
-                                  op=ALU.add)
-            added[pair] = added.get(pair, 0) + nb
-            if added[pair] == B:
-                done.add(("added", pair))
+            cols = slice(PAIR_ROWS * (b0 % 2), PAIR_ROWS * (b0 % 2 + n_batches))
+            eng.tensor_tensor(out=rotated[pair][:, b0:b0 + n_batches].rearrange("p b h (j e) -> p (b h j) e", e=2),
+                              in0=products[pair][:, b0 // 2, 0, cols].rearrange("p (m e) -> p m e", e=2),
+                              in1=products[pair][:, b0 // 2, 1, cols].rearrange("p (m e) -> p m e", e=2)[:, :, ::-1],
+                              op=ALU.add)
+            batches_added[pair] = batches_added.get(pair, 0) + n_batches
+            if batches_added[pair] == B:
+                written.add(("pair is rotated", pair))
             dst = out_0 if pair < PAIRS // 2 else out_1
             head = 2 * (pair % (PAIRS // 2))
-            if pair == PAIRS - 1:
-                for q in range(b, b + nb):
-                    nc.sync.dma_start(out=dst[head:head + 2, q].rearrange("h s d -> s h d"), in_=rotated[pair][:, q])
-            elif added[pair] == B:
+            if pair == LAST:
+                nc.sync.dma_start(out=dst[head:head + 2, b0].rearrange("h s d -> s h d"), in_=rotated[pair][:, b0])
+            elif batches_added[pair] == B:
                 for hh in range(2):
                     nc.sync.dma_start(out=dst[head + hh].rearrange("b s d -> s b d"), in_=rotated[pair][:, :, hh, :])
 
-        def add_sum(engine, key, b, nb):
-            item(engine, ("sum", key, b), [("product", key)] if nb < B else [("product", (key[0], 0, 2)), ("product", (key[0], 2, 2))], lambda: rope_sum(nc.vector if engine == "V" else nc.gpsimd, key, b, nb))
+        def job_sum(engine, bank):
+            eng = nc.vector if engine == "vector" else nc.gpsimd
+            job(engine, ("rotated", bank), [("product", bank)], lambda: rope_sum(eng, bank))
 
         fence_word = const.tile([P, 1], U32, name="fence_word")
 
-        def add_fence(key, g0=0):
-            item("G", ("fence", key), [("codes", key, g0)],
-                 lambda: nc.gpsimd.tensor_copy(out=fence_word[:], in_=codes[key][0][:, g0, 0:1]))
+        def job_fence(key, g0=0):
+            job("gpsimd", ("fence", key), [("codes", key, g0)],
+                lambda: nc.gpsimd.tensor_copy(out=fence_word[:], in_=codes[key][0][:, g0, 0:1]))
 
-        def pair_key(pair, half):
-            return (pair, 2 * half, 2)
+        job_load_first_x(0)
+        job_load_pair(1)
+        job_load_first_x(1)
+        job_load_pair(2)
+        job_load_first_x(2)
+        job_load_first_x(3)
+        job("loads", ("second_x",), [], load_second_x)
+        for i in range(3, PAIRS):
+            job_load_pair(i)
 
-        item("V", ("first_wide", 0), [], lambda: cast_first(0, nc.vector.tensor_copy))
-        item("V", ("first_wide", 1), [], lambda: cast_first(1, nc.vector.tensor_copy))
-        add_empty_w("V", 0)
-        for k in range(4):
-            if k not in XS:
-                add_copy_x(k, "V")
-            add_empty_w("V", k + 1)
-            if k == TABLE_AT:
-                item("V", ("table_a",), [], make_table)
-        add_quantize("x0")
-        add_quantize(0)
-        for k in range(4, 8):
-            if k not in XS:
-                add_copy_x(k, "V")
-            add_empty_w("V", k + 1)
-        add_quantize(1)
-        add_quantize("x1")
-        for k in (9, 10, 11):
-            add_empty_w("V", k)
-        add_empty_w("V", 12)
-        add_quantize(2)
-        add_empty_w("V", 13)
-        add_product("V", pair_key(0, 1))
-        add_empty_w("V", 14)
-        add_product("V", pair_key(1, 1))
-        add_empty_w("V", 15)
-        for i in range(4, PAIRS):
-            for g in range(PASSES):
-                k = PASSES * i + g
-                if k not in SCALED_BY_SCALAR:
-                    add_empty_w("V", k)
-                if g == 0:
-                    if i >= 4 and way(i - 3, 1) == V_ALL:
-                        add_sum("V", pair_key(i - 3, 1), 2, 2)
-                    elif i >= 4 and way(i - 3, 1) == V_PRODUCT_HALF_SUM:
-                        add_sum("V", pair_key(i - 3, 1), 2, 1)
-                    add_quantize(i - 1)
-                if g == 1:
-                    if way(i - 2, 0) == V_PRODUCT:
-                        add_product("V", pair_key(i - 2, 0))
-                    add_product("V", pair_key(i - 2, 1))
-        last = PAIRS - 1
-        add_product("V", (last - 1, 0, 2))
-        if way(last - 2, 1) == V_ALL:
-            add_sum("V", pair_key(last - 2, 1), 2, 2)
-        add_quantize(last, 0, 2)
-        add_quantize(last, 2, 4)
-        add_product("V", pair_key(last - 1, 1))
+        job_cast_first("vector", 0)
+        job_cast_first("vector", 1)
+        for k in range(BANKS):
+            i, g = divmod(k, PASSES)
+            if 1 <= k <= VECTOR_X_BANKS:
+                job_empty_x("vector", k - 1)
+            if not by_scalar(k):
+                job_scale(k)
+            if k == 1:
+                job("vector", ("turns are off",), [], take_off_turns)
+            if g == 0 and i >= 1:
+                if i >= 4 and rope_way(i - 3, 1) == BY_VECTOR:
+                    job_sum("vector", sum_bank(i - 3, 1))
+                if i == 1:
+                    job_quantize_x(0)
+                job_quantize_w(i - 1)
+                if i == 2:
+                    job_quantize_x(1)
+            if i == 3 and g in (1, 2):
+                job_product("vector", sum_bank(g - 1, 1))
+            if i >= 4 and g == 1:
+                if rope_way(i - 2, 0) == SUM_ON_GPSIMD:
+                    job_product("vector", sum_bank(i - 2, 0))
+                job_product("vector", sum_bank(i - 2, 1))
+        job_product("vector", sum_bank(LAST - 1, 0))
+        job_quantize_w(LAST, 0, 2)
+        job_sum("vector", sum_bank(LAST - 2, 1))
+        job_quantize_w(LAST, 2, 4)
+        job_product("vector", sum_bank(LAST - 1, 1))
         for b in range(B):
-            add_product("V", (last, b, 1))
-        add_sum("V", (last, 2, 1), 2, 1)
-        add_sum("V", (last, 3, 1), 3, 1)
+            job_product("vector", last_sum_bank(b))
+        job_sum("vector", last_sum_bank(2))
+        job_sum("vector", last_sum_bank(3))
 
-        for what in HEAD_G:
-            if what == "table":
-                item("G", ("table_b",), [("table_a",)], make_table_gpsimd)
-            else:
-                add_widen(what[0], what[1])
-        for key, work_ in [("x1", [(0, 0)]), (2, [(1, 0), (0, 1)]), (3, [(2, 0), (1, 1), (2, 1)])] + [(i - 1, [(i - 2, 0), (i - 2, 1)]) for i in range(5, PAIRS)]:
-            add_fence(key)
-            for pair, half in work_:
-                if MERGE and way(pair, 0) == G_ALL and way(pair, 1) == V_PRODUCT and pair >= 2:
-                    if half == 0:
-                        add_product("G", pair_key(pair, 0))
-                    else:
-                        add_sum("G", (pair, 0, B), 0, B)
-                    continue
-                w_ = way(pair, half)
-                pk = pair_key(pair, half)
-                if w_ == G_ALL:
-                    add_product("G", pk)
-                    add_sum("G", pk, 2 * half, 2)
-                elif w_ == V_PRODUCT:
-                    add_sum("G", pk, 2 * half, 2)
-                elif w_ == V_PRODUCT_HALF_SUM:
-                    add_sum("G", pk, 2 * half + 1, 1)
-        add_fence(last, 2)
+        job("gpsimd", ("angles are near zero",), [("turns are off",)], bring_near_zero)
+        for piece in range(len(cast_pieces(2))):
+            job_cast(2, piece)
+
+        def rotate_on_gpsimd(bank, way):
+            if way == BY_GPSIMD:
+                job_product("gpsimd", bank)
+            if way != BY_VECTOR:
+                job_sum("gpsimd", bank)
+
+        for key, banks in [("x1", [(0, 0)]), (2, [(1, 0), (0, 1)]), (3, [(2, 0), (1, 1), (2, 1)])] + \
+                [(i + 1, [(i, 0), (i, 1)]) for i in range(3, LAST - 1)]:
+            job_fence(key)
+            for pair, half in banks:
+                rotate_on_gpsimd(sum_bank(pair, half), rope_way(pair, half))
+        job_fence(LAST, 2)
         for half in range(2):
-            pk = pair_key(last - 1, half)
-            if way(last - 1, half) == G_ALL:
-                add_product("G", pk)
-            if way(last - 1, half) != V_ALL:
-                add_sum("G", pk, 2 * half, 2)
-        add_sum("G", (last, 0, 1), 0, 1)
-        add_sum("G", (last, 1, 1), 1, 1)
+            job_sum("gpsimd", sum_bank(LAST - 1, half))
+        job_sum("gpsimd", last_sum_bank(0))
+        job_sum("gpsimd", last_sum_bank(1))
 
-        for what, k in HEAD_T:
-            if what == "w":
-                add_transpose_w(k)
-            elif what == "x":
-                add_transpose_x(k)
-            else:
-                add_matmuls((0, 0, 2), k)
-        groups = {8: [(1, 0), (0, 2)], 9: [(1, 1), (0, 3)], 10: [(1, 2)], 11: [(1, 3)]}
-        for pair in range(2, last):
-            for b in range(B):
-                groups.setdefault(PASSES * (pair + 1) + b, []).append((pair, b))
-        next_w = HEAD_W
+        for k in range(PASSES):
+            job_transpose_w(k)
+            job_transpose_x(k)
+        job_transpose_w(4)
+        job_transpose_x(4)
+        job_transpose_w(5)
+        job_transpose_x(5)
+        job_transpose_w(6)
+        job_transpose_w(7)
+        job_transpose_x(6)
+        job_matmuls(sum_bank(0, 0), 0)
+        job_transpose_w(8)
+        job_matmuls(sum_bank(0, 0), 1)
+        job_transpose_x(7)
+        next_bank = 9
         for k in range(7, BANKS + PASSES):
-            for w in range(next_w, min(k + ahead(k), BANKS - 1) + 1):
-                add_transpose_w(w)
-                next_w = w + 1
-            for pair, b in groups.get(k, []):
-                add_matmuls((pair, 2 * (b // 2), 2), b)
+            for bank in range(next_bank, min(k + TENSOR_AHEAD, BANKS - 1) + 1):
+                job_transpose_w(bank)
+                next_bank = bank + 1
+            i, b = divmod(k, PASSES)
+            if 2 <= i <= LAST:
+                job_matmuls(sum_bank(i - 1, b // 2), b)
+            if i == 2 and b < 2:
+                job_matmuls(sum_bank(0, 1), 2 + b)
         for g0 in (0, 2):
             for b in range(B):
-                add_matmuls((last, b, 1), b, g0, g0 + 2)
+                job_matmuls(last_sum_bank(b), b, g0, g0 + 2)
 
-        sq = []
-        def s_first(g):
-            item("S", ("first_wide", g), [], lambda: cast_first(g, nc.scalar.copy))
-        def s_items(l):
-            for p in l:
-                item(*p)
-        s_first(2)
-        s_first(3)
-        for what in HEAD_S:
-            if what == "sin":
-                item("S", ("table",), [("table_b",)], make_sin)
-            elif what[0] == "x":
-                add_copy_x(what[1])
-            elif what[0] == "c":
-                add_widen(what[1], what[2])
-            elif what[0] == "s":
-                add_copy_sums(pair_key(what[1], 0))
-        for p in range(S_FROM, PAIRS):
-            sq.append((PASSES * p - cast_lead(p), 2, lambda p=p: add_widen(p, 0)))
-        for k in SCALED_BY_SCALAR:
-            sq.append((k - 2, 0, lambda k=k: add_empty_w("S", k)))
-        for pair in range(1, last):
-            for half in range(2):
-                if way(pair, half) == G_ALL:
-                    u = PASSES * (pair + 1) + 2 + 2 * half
-                    sq.append((u, 1, lambda pair=pair, half=half: add_copy_sums(pair_key(pair, half))))
-        for u, o, f in sorted(sq, key=lambda e: e[0:2]):
-            f()
+        job_cast_first("scalar", 2)
+        job_cast_first("scalar", 3)
+        job_cast(1, 0)
+        job_cast(1, 1)
+        for k in range(VECTOR_X_BANKS, 6):
+            job_empty_x("scalar", k)
+        job_cast(3, 0)
+        job_empty_x("scalar", 6)
+        job_cast(3, 1)
+        job_empty_x("scalar", 7)
+        job("scalar", ("table",), [("angles are near zero",)], make_table)
+        for k in range(PASSES + 2, BANKS):
+            i, g = divmod(k, PASSES)
+            if k + SCALAR_AHEAD < BANKS and by_scalar(k + SCALAR_AHEAD):
+                job_scale(k + SCALAR_AHEAD)
+            if g == 2:
+                if rope_way(i - 1, 0) == BY_GPSIMD:
+                    job_copy_sums(sum_bank(i - 1, 0))
+                if i + CAST_AHEAD < PAIRS:
+                    job_cast(i + CAST_AHEAD, 0)
 
-        emit_all()
+        merge()

@@ -50,16 +50,21 @@ def by_scalar(k):
     return pair == LAST or (pair >= 4 and pair % 2 == 0 and g == 0)
 
 
+def in_halves(k):
+    pair, g = divmod(k, PASSES)
+    return pair >= 5 and pair % 2 == 1 and g == 0 and not by_scalar(k)
+
+
 def rope_way(pair, half):
-    if half == 1 and any(by_scalar(k) for k in range(PASSES * (pair + 2) + 1, PASSES * (pair + 3) + 1) if k < BANKS):
-        return BY_VECTOR
     if half == 0 and pair < PAIRS - 3:
         return BY_GPSIMD
+    if half == 1 and pair == PAIRS - 3:
+        return BY_VECTOR
     return SUM_ON_GPSIMD
 
 
 def cast_pieces(i):
-    if i in (1, 3):
+    if i == 1:
         return [("scalar", 0, 2), ("scalar", 2, 4)]
     if i == 2:
         return [("gpsimd", g, g + 1) for g in range(PASSES)]
@@ -67,7 +72,7 @@ def cast_pieces(i):
 
 
 def cast_row_tiles(i):
-    return ("both",) if i > 3 else (0, 1)
+    return (0, 1) if i in (1, 2) else ("both",)
 
 
 def tile_multiheadselfattention_pa_kernel(tc, x, w_qk_bytes, w_qk_scale, out_0, out_1):
@@ -271,12 +276,13 @@ def tile_multiheadselfattention_pa_kernel(tc, x, w_qk_bytes, w_qk_scale, out_0, 
                                          align_bytes=64)
             return grouped[key]
 
-        def vector_scale(k):
+        def vector_scale(k, first_row, n_rows):
             i, g = divmod(k, PASSES)
+            rows = slice(first_row, first_row + n_rows)
             nc.vector.tensor_tensor(
-                out=grouped_tile(i)[:, g].rearrange("p n (u e) -> p n u e", e=2),
-                in0=w_bank[k][:].bitcast(BF16).rearrange("p u (n e) -> p n u e", e=2),
-                in1=scale[:, g, :].rearrange("p (u e) -> p u e", e=2).unsqueeze(1).to_broadcast([P, PAIR_ROWS, 2, 2]),
+                out=grouped_tile(i)[:, g, rows].rearrange("p n (u e) -> p n u e", e=2),
+                in0=w_bank[k][:, :, rows].bitcast(BF16).rearrange("p u (n e) -> p n u e", e=2),
+                in1=scale[:, g, :].rearrange("p (u e) -> p u e", e=2).unsqueeze(1).to_broadcast([P, n_rows, 2, 2]),
                 op=ALU.mult)
 
         def scalar_scale(k):
@@ -290,11 +296,15 @@ def tile_multiheadselfattention_pa_kernel(tc, x, w_qk_bytes, w_qk_scale, out_0, 
             nc.scalar.copy(out=out.rearrange("p (c i) t -> p c t i", i=4),
                            in_=planes[:].rearrange("p t (c i) -> p c t i", i=4))
 
-        def job_scale(k):
-            if by_scalar(k):
-                job("scalar", ("w is emptied", k), [("w", k)], lambda: scalar_scale(k))
-            else:
-                job("vector", ("w is emptied", k), [("w", k)], lambda: vector_scale(k))
+        def job_scalar_scale(k):
+            job("scalar", ("w is emptied", k), [("w", k)], lambda: scalar_scale(k))
+
+        def job_vector_scale(k):
+            job("vector", ("w is emptied", k), [("w", k)], lambda: vector_scale(k, 0, PAIR_ROWS))
+
+        def job_vector_scale_half(k, half):
+            name = "half of w is emptied" if half == 0 else "w is emptied"
+            job("vector", (name, k), [("w", k)], lambda: vector_scale(k, PAIR_ROWS // 2 * half, PAIR_ROWS // 2))
 
         def empty_x(k, copy):
             copy(out=grouped_tile("x%d" % (k // PASSES))[:, k % PASSES].rearrange("p n t -> p (n t)").bitcast(F32)
@@ -439,18 +449,20 @@ def tile_multiheadselfattention_pa_kernel(tc, x, w_qk_bytes, w_qk_scale, out_0, 
             i, g = divmod(k, PASSES)
             if 1 <= k <= VECTOR_X_BANKS:
                 job_empty_x("vector", k - 1)
-            if not by_scalar(k):
-                job_scale(k)
+            if in_halves(k):
+                job_vector_scale_half(k, 0)
+            elif not by_scalar(k):
+                job_vector_scale(k)
             if k == 1:
                 job("vector", ("turns are off",), [], take_off_turns)
             if g == 0 and i >= 1:
-                if i >= 4 and rope_way(i - 3, 1) == BY_VECTOR:
-                    job_sum("vector", sum_bank(i - 3, 1))
                 if i == 1:
                     job_quantize_x(0)
                 job_quantize_w(i - 1)
                 if i == 2:
                     job_quantize_x(1)
+            if in_halves(k):
+                job_vector_scale_half(k, 1)
             if i == 3 and g in (1, 2):
                 job_product("vector", sum_bank(g - 1, 1))
             if i >= 4 and g == 1:
@@ -524,13 +536,12 @@ def tile_multiheadselfattention_pa_kernel(tc, x, w_qk_bytes, w_qk_scale, out_0, 
             job_empty_x("scalar", k)
         job_cast(3, 0)
         job_empty_x("scalar", 6)
-        job_cast(3, 1)
         job_empty_x("scalar", 7)
         job("scalar", ("table",), [("angles are near zero",)], make_table)
         for k in range(PASSES + 2, BANKS):
             i, g = divmod(k, PASSES)
             if k + SCALAR_AHEAD < BANKS and by_scalar(k + SCALAR_AHEAD):
-                job_scale(k + SCALAR_AHEAD)
+                job_scalar_scale(k + SCALAR_AHEAD)
             if g == 2:
                 if rope_way(i - 1, 0) == BY_GPSIMD:
                     job_copy_sums(sum_bank(i - 1, 0))

@@ -40,10 +40,6 @@ SCALAR_AHEAD = 2
 CAST_AHEAD = 3
 VECTOR_X_BANKS = 2
 
-BY_VECTOR = 0
-SUM_ON_GPSIMD = 1
-BY_GPSIMD = 2
-
 
 def by_scalar(k):
     pair, g = divmod(k, PASSES)
@@ -55,12 +51,12 @@ def in_halves(k):
     return pair >= 5 and pair % 2 == 1 and g == 0 and not by_scalar(k)
 
 
-def rope_way(pair, half):
-    if half == 0 and pair < PAIRS - 3:
-        return BY_GPSIMD
-    if half == 1 and pair == PAIRS - 3:
-        return BY_VECTOR
-    return SUM_ON_GPSIMD
+def product_on_gpsimd(pair, half):
+    return half == 0 and pair < PAIRS - 3
+
+
+def vector_heads(pair, half):
+    return 1 if half == 1 and 1 <= pair < LAST - 1 else 0
 
 
 def cast_pieces(i):
@@ -339,7 +335,7 @@ def tile_multiheadselfattention_pa_kernel(tc, x, w_qk_bytes, w_qk_scale, out_0, 
         sum_tile = {}
         products = {}
         rotated = {}
-        batches_added = {}
+        heads_added = {}
 
         def sum_bank(pair, half):
             return (pair, 2 * half, 2)
@@ -403,29 +399,36 @@ def tile_multiheadselfattention_pa_kernel(tc, x, w_qk_bytes, w_qk_scale, out_0, 
             job(engine, ("product", bank), needs, lambda: rope_product(eng, bank),
                 ("products", PRODUCT_SLOTS, ("pair is rotated", bank[0])))
 
-        def rope_sum(eng, bank):
+        def rope_sum(eng, bank, h0, h1):
             pair, b0, n_batches = bank
             if pair not in rotated:
-                rotated[pair] = work.tile([P, B, 2, HD], F32, name="rotated", tag="rotated")
-            cols = slice(PAIR_ROWS * (b0 % 2), PAIR_ROWS * (b0 % 2 + n_batches))
-            eng.tensor_tensor(out=rotated[pair][:, b0:b0 + n_batches].rearrange("p b h (j e) -> p (b h j) e", e=2),
+                rotated[pair] = work.tile([P, 2 * B, HD], F32, name="rotated", tag="rotated")
+            cols = slice(PAIR_ROWS * (b0 % 2) + HD * h0, PAIR_ROWS * (b0 % 2) + HD * h1)
+            eng.tensor_tensor(out=rotated[pair][:, 2 * b0 + h0:2 * b0 + h1].rearrange("p h (j e) -> p (h j) e", e=2),
                               in0=products[pair][:, b0 // 2, 0, cols].rearrange("p (m e) -> p m e", e=2),
                               in1=products[pair][:, b0 // 2, 1, cols].rearrange("p (m e) -> p m e", e=2)[:, :, ::-1],
                               op=ALU.add)
-            batches_added[pair] = batches_added.get(pair, 0) + n_batches
-            if batches_added[pair] == B:
+            heads_added[pair] = heads_added.get(pair, 0) + h1 - h0
+            if heads_added[pair] == 2 * B:
                 written.add(("pair is rotated", pair))
             dst = out_0 if pair < PAIRS // 2 else out_1
             head = 2 * (pair % (PAIRS // 2))
             if pair == LAST:
-                nc.sync.dma_start(out=dst[head:head + 2, b0].rearrange("h s d -> s h d"), in_=rotated[pair][:, b0])
-            elif batches_added[pair] == B:
+                nc.sync.dma_start(out=dst[head:head + 2, b0].rearrange("h s d -> s h d"),
+                                  in_=rotated[pair][:, 2 * b0:2 * b0 + 2])
+            elif heads_added[pair] == 2 * B:
                 for hh in range(2):
-                    nc.sync.dma_start(out=dst[head + hh].rearrange("b s d -> s b d"), in_=rotated[pair][:, :, hh, :])
+                    nc.sync.dma_start(out=dst[head + hh].rearrange("b s d -> s b d"),
+                                      in_=rotated[pair][:, hh:2 * B:2, :])
 
-        def job_sum(engine, bank):
+        def job_sum(engine, bank, h0, h1):
             eng = nc.vector if engine == "vector" else nc.gpsimd
-            job(engine, ("rotated", bank), [("product", bank)], lambda: rope_sum(eng, bank))
+            job(engine, ("rotated", bank, h0), [("product", bank)], lambda: rope_sum(eng, bank, h0, h1))
+
+        def job_vector_heads(pair):
+            n = vector_heads(pair, 1)
+            if n > 0:
+                job_sum("vector", sum_bank(pair, 1), 4 - n, 4)
 
         fence_word = const.tile([P, 1], U32, name="fence_word")
 
@@ -456,6 +459,8 @@ def tile_multiheadselfattention_pa_kernel(tc, x, w_qk_bytes, w_qk_scale, out_0, 
             if k == 1:
                 job("vector", ("turns are off",), [], take_off_turns)
             if g == 0 and i >= 1:
+                if i >= 4:
+                    job_vector_heads(i - 3)
                 if i == 1:
                     job_quantize_x(0)
                 job_quantize_w(i - 1)
@@ -466,39 +471,38 @@ def tile_multiheadselfattention_pa_kernel(tc, x, w_qk_bytes, w_qk_scale, out_0, 
             if i == 3 and g in (1, 2):
                 job_product("vector", sum_bank(g - 1, 1))
             if i >= 4 and g == 1:
-                if rope_way(i - 2, 0) == SUM_ON_GPSIMD:
+                if not product_on_gpsimd(i - 2, 0):
                     job_product("vector", sum_bank(i - 2, 0))
                 job_product("vector", sum_bank(i - 2, 1))
         job_product("vector", sum_bank(LAST - 1, 0))
         job_quantize_w(LAST, 0, 2)
-        job_sum("vector", sum_bank(LAST - 2, 1))
+        job_vector_heads(LAST - 2)
         job_quantize_w(LAST, 2, 4)
         job_product("vector", sum_bank(LAST - 1, 1))
         for b in range(B):
             job_product("vector", last_sum_bank(b))
-        job_sum("vector", last_sum_bank(2))
-        job_sum("vector", last_sum_bank(3))
+        job_sum("vector", last_sum_bank(2), 0, 2)
+        job_sum("vector", last_sum_bank(3), 0, 2)
 
         job("gpsimd", ("angles are near zero",), [("turns are off",)], bring_near_zero)
         for piece in range(len(cast_pieces(2))):
             job_cast(2, piece)
 
-        def rotate_on_gpsimd(bank, way):
-            if way == BY_GPSIMD:
-                job_product("gpsimd", bank)
-            if way != BY_VECTOR:
-                job_sum("gpsimd", bank)
+        def rotate_on_gpsimd(pair, half):
+            if product_on_gpsimd(pair, half):
+                job_product("gpsimd", sum_bank(pair, half))
+            job_sum("gpsimd", sum_bank(pair, half), 0, 4 - vector_heads(pair, half))
 
         for key, banks in [("x1", [(0, 0)]), (2, [(1, 0), (0, 1)]), (3, [(2, 0), (1, 1), (2, 1)])] + \
                 [(i + 1, [(i, 0), (i, 1)]) for i in range(3, LAST - 1)]:
             job_fence(key)
             for pair, half in banks:
-                rotate_on_gpsimd(sum_bank(pair, half), rope_way(pair, half))
+                rotate_on_gpsimd(pair, half)
         job_fence(LAST, 2)
         for half in range(2):
-            job_sum("gpsimd", sum_bank(LAST - 1, half))
-        job_sum("gpsimd", last_sum_bank(0))
-        job_sum("gpsimd", last_sum_bank(1))
+            rotate_on_gpsimd(LAST - 1, half)
+        job_sum("gpsimd", last_sum_bank(0), 0, 2)
+        job_sum("gpsimd", last_sum_bank(1), 0, 2)
 
         for k in range(PASSES):
             job_transpose_w(k)
@@ -543,7 +547,7 @@ def tile_multiheadselfattention_pa_kernel(tc, x, w_qk_bytes, w_qk_scale, out_0, 
             if k + SCALAR_AHEAD < BANKS and by_scalar(k + SCALAR_AHEAD):
                 job_scalar_scale(k + SCALAR_AHEAD)
             if g == 2:
-                if rope_way(i - 1, 0) == BY_GPSIMD:
+                if product_on_gpsimd(i - 1, 0):
                     job_copy_sums(sum_bank(i - 1, 0))
                 if i + CAST_AHEAD < PAIRS:
                     job_cast(i + CAST_AHEAD, 0)

import math
from contextlib import ExitStack

import concourse.mybir as mybir
from concourse.masks import make_identity

F32 = mybir.dt.float32
BF16 = mybir.dt.bfloat16
U32 = mybir.dt.uint32
U8 = mybir.dt.uint8
I32 = mybir.dt.int32
FP8 = mybir.dt.float8_e4m3fn
FP8X4 = mybir.dt.float8_e4m3fn_x4
ALU = mybir.AluOpType
ACT = mybir.ActivationFunctionType

B, S, D, H = 4, 128, 2048, 16
HD = D // H
FLOPS = 2 * B * S * D * 2 * D

P = 128
PACK = 4
K_PASS = P * PACK
PASSES = D // K_PASS
PAIR_ROWS = 2 * HD
PAIRS = 2 * D // PAIR_ROWS
LAST = PAIRS - 1
BANKS = PAIRS * PASSES
X_BANKS = 2 * PASSES

BYTES_SLOTS = 12
WIDE_SLOTS = 4
TRANSPOSE_BANKS = 5
SUM_BANKS = 3
SUM_COPIES = 4
PRODUCT_SLOTS = 3

TENSOR_AHEAD = 4
SCALAR_AHEAD = 2
CAST_AHEAD = 3
VECTOR_X_BANKS = 2


def by_scalar(k):
    pair, g = divmod(k, PASSES)
    return pair == LAST or (pair >= 4 and pair % 2 == 0 and g == 0)


def in_halves(k):
    pair, g = divmod(k, PASSES)
    return pair >= 5 and pair % 2 == 1 and g == 0 and not by_scalar(k)


def product_on_gpsimd(pair, half):
    return half == 0 and pair < PAIRS - 3


def vector_heads(pair, half):
    return 1 if half == 1 and 1 <= pair < LAST - 1 else 0


def cast_pieces(i):
    if i == 1:
        return [("scalar", 0, 2), ("scalar", 2, 4)]
    if i == 2:
        return [("gpsimd", g, g + 1) for g in range(PASSES)]
    return [("scalar", 0, PASSES)]


def cast_row_tiles(i):
    return (0, 1) if i in (1, 2) else ("both",)


def tile_multiheadselfattention_pa_kernel(tc, x, w_qk_bytes, w_qk_scale, out_0, out_1):
    nc = tc.nc
    with ExitStack() as ctx:
        const = ctx.enter_context(tc.tile_pool(name="const", bufs=1))
        bytes_pool = ctx.enter_context(tc.tile_pool(name="bytes", bufs=BYTES_SLOTS))
        wide = ctx.enter_context(tc.tile_pool(name="wide", bufs=WIDE_SLOTS))
        work = ctx.enter_context(tc.tile_pool(name="work", bufs=4))
        psum_t = ctx.enter_context(tc.psum_pool(name="psum_t", bufs=TRANSPOSE_BANKS))
        psum_o = ctx.enter_context(tc.psum_pool(name="psum_o", bufs=SUM_BANKS))
        ctx.enter_context(tc.manual_schedule())

        lists = {"loads": [], "scalar": [], "vector": [], "tensor": [], "gpsimd": []}
        written = set()
        taken = {}

        def job(engine, name, needs, write, slot=None):
            lists[engine].append((name, needs, write, slot))

        def slot_is_free(slot):
            pool, slots, frees = slot
            users = taken.setdefault(pool, [])
            return frees in users or len(users) < slots or users[len(users) - slots] in written

        def merge():
            at = {engine: 0 for engine in lists}
            for turn in range(sum(len(lists[engine]) for engine in lists)):
                for engine in lists:
                    for name, needs, write, slot in lists[engine][at[engine]:]:
                        if not all(n in written for n in needs) or (slot is not None and not slot_is_free(slot)):
                            break
                        if slot is not None and slot[2] not in taken[slot[0]]:
                            taken[slot[0]].append(slot[2])
                        write()
                        written.add(name)
                        at[engine] += 1
            assert all(at[engine] == len(lists[engine]) for engine in lists), "the lists wait for each other"

        first_bytes = []
        first_x = []
        pair_bytes = {}
        scale = const.tile([P, PASSES, PACK], F32, name="scale")

        def load_first_bytes(g):
            k_cols = slice(K_PASS * g, K_PASS * (g + 1))
            t = const.tile([P, 2, K_PASS], U8, name="first_bytes%d" % g)
            nc.sync.dma_start(out=t[:], in_=w_qk_bytes[0:PAIR_ROWS, k_cols].rearrange("(r p) k -> p r k", p=P))
            first_bytes.append(t)

        def load_first_x(g):
            k_cols = slice(K_PASS * g, K_PASS * (g + 1))
            t = const.tile([P, 2, K_PASS], BF16, name="first_x%d" % g)
            nc.sync.dma_start(out=t[:], in_=x[0:2, :, k_cols].rearrange("b s k -> s b k"))
            first_x.append(t)

        load_first_bytes(0)
        load_first_bytes(1)
        nc.sync.dma_start(out=scale[:], in_=w_qk_scale.rearrange("o (g p t) -> p (o g) t", p=P, t=PACK))
        load_first_bytes(2)
        load_first_bytes(3)

        second_x = const.tile([P, 2, D], BF16, name="second_x")

        def load_pair(i):
            t = bytes_pool.tile([P, 2, D], U8, name="pair_bytes%d" % i, tag="pair_bytes")
            nc.sync.dma_start(out=t[:],
                              in_=w_qk_bytes[PAIR_ROWS * i:PAIR_ROWS * (i + 1), :].rearrange("(r p) k -> p r k", p=P))
            pair_bytes[i] = t

        def load_second_x():
            nc.sync.dma_start(out=second_x[:], in_=x[2:4].rearrange("b s k -> s b k"))

        def job_load_pair(i):
            job("loads", ("bytes", i), [], lambda: load_pair(i), ("bytes", BYTES_SLOTS, ("pair is cast", i)))

        def job_load_first_x(g):
            job("loads", ("first_x", g), [], lambda: load_first_x(g))

        warm = const.tile([P, 2], F32, name="warm")
        nc.gpsimd.memset(warm[:, 0:1], 0.0)
        nc.scalar.activation(out=warm[:, 1:2], in_=warm[:, 0:1], func=ACT.Sin)
        ident = const.tile([P, P], F32, name="ident")
        make_identity(nc, ident[:])

        pos_i = const.tile([P, 1], I32, name="pos_i")
        nc.gpsimd.iota(out=pos_i[:], pattern=[[0, 1]], base=0, channel_multiplier=1)
        pos_f = const.tile([P, 1], F32, name="pos_f")
        nc.vector.tensor_copy(out=pos_f[:], in_=pos_i[:])
        power = const.tile([P, HD // 2], F32, name="power")
        nc.gpsimd.memset(power[:, 0:1], 1.0)
        ratio = 10000.0 ** (-2.0 / HD)
        for w in (1, 2, 4, 8, 16, 32):
            nc.gpsimd.tensor_scalar(out=power[:, w:2 * w], in0=power[:, 0:w], scalar1=ratio ** w, scalar2=None,
                                    op0=ALU.mult)
        turns = const.tile([P, HD // 2], F32, name="turns")
        nc.gpsimd.tensor_scalar(out=turns[:], in0=power[:], scalar1=pos_f[:, 0:1], scalar2=1.0 / (2.0 * math.pi),
                                op0=ALU.mult, op1=ALU.mult)
        arg = const.tile([P, 2, HD // 2, 2], F32, name="arg")
        for e in range(2):
            nc.gpsimd.tensor_scalar(out=arg[:, 0, :, e], in0=turns[:], scalar1=1.0, scalar2=0.25, op0=ALU.mult,
                                    op1=ALU.add)
            nc.gpsimd.tensor_copy(out=arg[:, 1, :, e], in_=turns[:])
        arg_flat = arg[:].rearrange("p a j e -> p (a j e)")
        whole = const.tile([P, 2 * HD], I32, name="whole")
        frac = const.tile([P, 2 * HD], F32, name="frac")
        over = const.tile([P, 2 * HD], F32, name="over")
        near = const.tile([P, 2, HD // 2, 2], F32, name="near")
        table = const.tile([P, 2, 4, HD], F32, name="table")

        def take_off_turns():
            nc.vector.tensor_copy(out=whole[:], in_=arg_flat)
            nc.vector.tensor_tensor(out=frac[:], in0=arg_flat, in1=whole[:], op=ALU.subtract)

        def bring_near_zero():
            nc.gpsimd.tensor_scalar(out=over[:], in0=frac[:], scalar1=0.5, scalar2=1.0, op0=ALU.is_gt, op1=ALU.mult)
            nc.gpsimd.tensor_tensor(out=near[:].rearrange("p a j e -> p (a j e)"), in0=frac[:], in1=over[:],
                                    op=ALU.subtract)
            nc.gpsimd.tensor_scalar(out=near[:, 1, :, 1], in0=near[:, 1, :, 1], scalar1=-1.0, scalar2=0.0,
                                    op0=ALU.mult, op1=ALU.add)

        def make_table():
            for a in range(2):
                nc.scalar.activation(out=table[:, a],
                                     in_=near[:, a].rearrange("p j e -> p (j e)").unsqueeze(1).to_broadcast([P, 4, HD]),
                                     func=ACT.Sin, scale=2.0 * math.pi)

        first_wide = {}
        pair_wide = {}
        pieces_left = {}
        w_bank = {}
        x_bank = {}
        grouped = {}
        codes = {}

        def cast_first(g, copy):
            t = const.tile([P, 2, K_PASS], BF16, name="first_wide%d" % g)
            copy(out=t[:].rearrange("p r k -> p (r k)"),
                 in_=first_bytes[g][:].rearrange("p r k -> p (r k)").bitcast(FP8))
            first_wide[g] = t

        def job_cast_first(engine, g):
            copy = nc.vector.tensor_copy if engine == "vector" else nc.scalar.copy
            job(engine, ("first_wide", g), [], lambda: cast_first(g, copy))

        def cast_piece(engine, i, row_tile, k_cols):
            if i not in pair_wide:
                pair_wide[i] = wide.tile([P, 2, D], BF16, name="pair_wide%d" % i, tag="pair_wide")
            if row_tile == "both":
                out = pair_wide[i][:].rearrange("p r k -> p (r k)")
                in_ = pair_bytes[i][:].rearrange("p r k -> p (r k)").bitcast(FP8)
            else:
                out, in_ = pair_wide[i][:, row_tile, k_cols], pair_bytes[i][:, row_tile, k_cols].bitcast(FP8)
            copy = nc.gpsimd.tensor_copy if engine == "gpsimd" else nc.scalar.copy
            copy(out=out, in_=in_)
            pieces_left[i] -= 1
            if pieces_left[i] == 0:
                written.add(("pair is cast", i))

        def job_cast(i, piece):
            engine, g0, g1 = cast_pieces(i)[piece]
            pieces_left[i] = len(cast_row_tiles(i)) * len(cast_pieces(i))
            for r in cast_row_tiles(i):
                job(engine, ("wide", i, g0, r), [("bytes", i)],
                    lambda r=r: cast_piece(engine, i, r, slice(K_PASS * g0, K_PASS * g1)),
                    ("wide", WIDE_SLOTS, ("w", PASSES * i + PASSES - 1)))

        def transposes(src, g):
            bank = psum_t.tile([P, 2, PAIR_ROWS], F32, name="bank", tag="bank")
            words = src[:].bitcast(F32)
            for r in range(2):
                for u in range(2):
                    nc.tensor.transpose(bank[:, u, P * r:P * (r + 1)],
                                        words[:, r, K_PASS // 2 * g + u:K_PASS // 2 * (g + 1):2], ident[:])
            return bank

        def transpose_weights(k):
            i, g = divmod(k, PASSES)
            w_bank[k] = transposes(first_wide[g], 0) if i == 0 else transposes(pair_wide[i], g)

        def transpose_x(k):
            x_bank[k] = transposes(first_x[k], 0) if k < PASSES else transposes(second_x, k % PASSES)

        def job_transpose_w(k):
            i, g = divmod(k, PASSES)
            if i == 0:
                needs = [("first_wide", g)]
            else:
                needs = [("wide", i, g0, r) for engine, g0, g1 in cast_pieces(i) if g0 <= g < g1
                         for r in cast_row_tiles(i)]
            job("tensor", ("w", k), needs, lambda: transpose_weights(k),
                ("transposes", TRANSPOSE_BANKS, ("w is emptied", k)))

        def job_transpose_x(k):
            job("tensor", ("x", k), [("first_x", k) if k < PASSES else ("second_x",)], lambda: transpose_x(k),
                ("transposes", TRANSPOSE_BANKS, ("x is emptied", k)))

        def grouped_tile(key):
            if key not in grouped:
                grouped[key] = work.tile([P, PASSES, PAIR_ROWS, PACK], BF16, name="grouped", tag="grouped",
                                         align_bytes=64)
            return grouped[key]

        def vector_scale(k, first_row, n_rows):
            i, g = divmod(k, PASSES)
            rows = slice(first_row, first_row + n_rows)
            nc.vector.tensor_tensor(
                out=grouped_tile(i)[:, g, rows].rearrange("p n (u e) -> p n u e", e=2),
                in0=w_bank[k][:, :, rows].bitcast(BF16).rearrange("p u (n e) -> p n u e", e=2),
                in1=scale[:, g, :].rearrange("p (u e) -> p u e", e=2).unsqueeze(1).to_broadcast([P, n_rows, 2, 2]),
                op=ALU.mult)

        def scalar_scale(k):
            i, g = divmod(k, PASSES)
            out = grouped_tile(i)[:, g]
            planes = work.tile([P, PACK, PAIR_ROWS], BF16, name="planes", tag="planes", bufs=2)
            src = w_bank[k][:].bitcast(BF16).rearrange("p u (n e) -> p u n e", e=2)
            for t in range(PACK):
                nc.scalar.activation(out=planes[:, t, :], in_=src[:, t // 2, :, t % 2], func=ACT.Copy,
                                     scale=scale[:, g, t:t + 1])
            nc.scalar.copy(out=out.rearrange("p (c i) t -> p c t i", i=4),
                           in_=planes[:].rearrange("p t (c i) -> p c t i", i=4))

        def job_scalar_scale(k):
            job("scalar", ("w is emptied", k), [("w", k)], lambda: scalar_scale(k))

        def job_vector_scale(k):
            job("vector", ("w is emptied", k), [("w", k)], lambda: vector_scale(k, 0, PAIR_ROWS))

        def job_vector_scale_half(k, half):
            name = "half of w is emptied" if half == 0 else "w is emptied"
            job("vector", (name, k), [("w", k)], lambda: vector_scale(k, PAIR_ROWS // 2 * half, PAIR_ROWS // 2))

        def empty_x(k, copy):
            copy(out=grouped_tile("x%d" % (k // PASSES))[:, k % PASSES].rearrange("p n t -> p (n t)").bitcast(F32)
                 .rearrange("p (n u) -> p n u", u=2),
                 in_=x_bank[k][:].rearrange("p u n -> p n u"))

        def job_empty_x(engine, k):
            copy = nc.vector.tensor_copy if engine == "vector" else nc.scalar.copy
            job(engine, ("x is emptied", k), [("x", k)], lambda: empty_x(k, copy))

        def quantize(key, pool, name, g0, g1):
            if key not in codes:
                codes[key] = (pool.tile([P, PASSES, PAIR_ROWS], U32, name=name + "_codes", tag=name + "_codes",
                                        align_bytes=64),
                              pool.tile([P, PASSES, PAIR_ROWS], U8, name=name + "_scales", tag=name + "_scales",
                                        align_bytes=64))
            c, s = codes[key]
            nc.vector.quantize_mx(out=c[:, g0:g1].rearrange("p g n -> p (g n)").bitcast(FP8X4),
                                  scales=s[:, g0:g1].rearrange("p g n -> p (g n)"),
                                  in_=grouped[key][:, g0:g1].rearrange("p g n t -> p (g n t)"))

        def job_quantize_w(i, g0=0, g1=PASSES):
            job("vector", ("codes", i, g0), [("w is emptied", PASSES * i + g) for g in range(g0, g1)],
                lambda: quantize(i, work, "w", g0, g1))

        def job_quantize_x(half):
            key = "x%d" % half
            job("vector", ("codes", key, 0), [("x is emptied", PASSES * half + g) for g in range(PASSES)],
                lambda: quantize(key, const, key, 0, PASSES))

        sums = {}
        sum_tile = {}
        products = {}
        rotated = {}
        heads_added = {}

        def sum_bank(pair, half):
            return (pair, 2 * half, 2)

        def last_sum_bank(b):
            return (LAST, b, 1)

        def matmuls(bank, b, g0, g1):
            pair, b0, n_batches = bank
            if bank not in sum_tile:
                if pair == LAST:
                    sum_tile[bank] = psum_t.tile([P, 2, PAIR_ROWS], F32, name="bank", tag="bank")
                else:
                    sum_tile[bank] = psum_o.tile([P, 2, PAIR_ROWS], F32, name="sum_bank", tag="sum_bank")
                sums[bank] = sum_tile[bank][:, 0:n_batches].rearrange("p b n -> p (b n)")
            w_codes, w_scales = codes[pair]
            x_codes, x_scales = codes["x%d" % (b // 2)]
            positions = slice(P * (b % 2), P * (b % 2 + 1))
            for g in range(g0, g1):
                nc.tensor.matmul_mx(out=sum_tile[bank][:, b - b0, :],
                                    lhsT=x_codes[:, g, positions].bitcast(FP8X4),
                                    lhsT_scale=x_scales[:, g, positions],
                                    rhs=w_codes[:, g, :].bitcast(FP8X4),
                                    rhs_scale=w_scales[:, g, :],
                                    start=(g == 0), stop=(g == PASSES - 1))

        def job_matmuls(bank, b, g0=0, g1=PASSES):
            slot = None
            if b == bank[1] and g0 == 0:
                slot = (("transposes", TRANSPOSE_BANKS) if bank[0] == LAST else ("sums", SUM_BANKS)) + (("is read", bank),)
            job("tensor", ("sums", bank, b, g1), [("codes", "x%d" % (b // 2), 0), ("codes", bank[0], g0)],
                lambda: matmuls(bank, b, g0, g1), slot)

        def is_summed(bank):
            return [("sums", bank, b, PASSES) for b in range(bank[1], bank[1] + bank[2])]

        def copy_sums(bank):
            t = work.tile([P, 2 * PAIR_ROWS], F32, name="sums_copy", tag="sums_copy")
            nc.scalar.copy(out=t[:], in_=sums[bank])
            sums[bank] = t[:]

        def job_copy_sums(bank):
            job("scalar", ("is read", bank), is_summed(bank), lambda: copy_sums(bank),
                ("sums_copy", SUM_COPIES, ("product", bank)))

        def rope_product(eng, bank):
            pair, b0, n_batches = bank
            if pair not in products:
                products[pair] = work.tile([P, 2, 2, 2 * PAIR_ROWS], F32, name="products", tag="products",
                                           bufs=PRODUCT_SLOTS)
            cols = n_batches * PAIR_ROWS
            first = PAIR_ROWS * (b0 % 2)
            eng.tensor_tensor(out=products[pair][:, b0 // 2, :, first:first + cols],
                              in0=sums[bank].unsqueeze(1).to_broadcast([P, 2, cols]),
                              in1=table[:, :, 0:2 * n_batches].rearrange("p a c d -> p a (c d)"), op=ALU.mult)
            written.add(("is read", bank))

        def job_product(engine, bank):
            eng = nc.vector if engine == "vector" else nc.gpsimd
            needs = is_summed(bank) + [("table",)] + ([("is read", bank)] if engine == "gpsimd" else [])
            job(engine, ("product", bank), needs, lambda: rope_product(eng, bank),
                ("products", PRODUCT_SLOTS, ("pair is rotated", bank[0])))

        def rope_sum(eng, bank, h0, h1):
            pair, b0, n_batches = bank
            if pair not in rotated:
                rotated[pair] = work.tile([P, 2 * B, HD], F32, name="rotated", tag="rotated")
            cols = slice(PAIR_ROWS * (b0 % 2) + HD * h0, PAIR_ROWS * (b0 % 2) + HD * h1)
            eng.tensor_tensor(out=rotated[pair][:, 2 * b0 + h0:2 * b0 + h1].rearrange("p h (j e) -> p (h j) e", e=2),
                              in0=products[pair][:, b0 // 2, 0, cols].rearrange("p (m e) -> p m e", e=2),
                              in1=products[pair][:, b0 // 2, 1, cols].rearrange("p (m e) -> p m e", e=2)[:, :, ::-1],
                              op=ALU.add)
            heads_added[pair] = heads_added.get(pair, 0) + h1 - h0
            if heads_added[pair] == 2 * B:
                written.add(("pair is rotated", pair))
            dst = out_0 if pair < PAIRS // 2 else out_1
            head = 2 * (pair % (PAIRS // 2))
            if pair == LAST:
                nc.sync.dma_start(out=dst[head:head + 2, b0].rearrange("h s d -> s h d"),
                                  in_=rotated[pair][:, 2 * b0:2 * b0 + 2])
            elif heads_added[pair] == 2 * B:
                for hh in range(2):
                    nc.sync.dma_start(out=dst[head + hh].rearrange("b s d -> s b d"),
                                      in_=rotated[pair][:, hh:2 * B:2, :])

        def job_sum(engine, bank, h0, h1):
            eng = nc.vector if engine == "vector" else nc.gpsimd
            job(engine, ("rotated", bank, h0), [("product", bank)], lambda: rope_sum(eng, bank, h0, h1))

        def job_vector_heads(pair):
            n = vector_heads(pair, 1)
            if n > 0:
                job_sum("vector", sum_bank(pair, 1), 4 - n, 4)

        fence_word = const.tile([P, 1], U32, name="fence_word")

        def job_fence(key, g0=0):
            job("gpsimd", ("fence", key), [("codes", key, g0)],
                lambda: nc.gpsimd.tensor_copy(out=fence_word[:], in_=codes[key][0][:, g0, 0:1]))

        job_load_first_x(0)
        job_load_pair(1)
        job_load_first_x(1)
        job_load_pair(2)
        job_load_first_x(2)
        job_load_first_x(3)
        job("loads", ("second_x",), [], load_second_x)
        for i in range(3, PAIRS):
            job_load_pair(i)

        job_cast_first("vector", 0)
        job_cast_first("vector", 1)
        for k in range(BANKS):
            i, g = divmod(k, PASSES)
            if 1 <= k <= VECTOR_X_BANKS:
                job_empty_x("vector", k - 1)
            if in_halves(k):
                job_vector_scale_half(k, 0)
            elif not by_scalar(k):
                job_vector_scale(k)
            if k == 1:
                job("vector", ("turns are off",), [], take_off_turns)
            if g == 0 and i >= 1:
                if i >= 4:
                    job_vector_heads(i - 3)
                if i == 1:
                    job_quantize_x(0)
                job_quantize_w(i - 1)
                if i == 2:
                    job_quantize_x(1)
            if in_halves(k):
                job_vector_scale_half(k, 1)
            if i == 3 and g in (1, 2):
                job_product("vector", sum_bank(g - 1, 1))
            if i >= 4 and g == 1:
                if not product_on_gpsimd(i - 2, 0):
                    job_product("vector", sum_bank(i - 2, 0))
                job_product("vector", sum_bank(i - 2, 1))
        job_product("vector", sum_bank(LAST - 1, 0))
        job_quantize_w(LAST, 0, 2)
        job_vector_heads(LAST - 2)
        job_quantize_w(LAST, 2, 4)
        job_product("vector", sum_bank(LAST - 1, 1))
        for b in range(B):
            job_product("vector", last_sum_bank(b))
        job_sum("vector", last_sum_bank(2), 0, 2)
        job_sum("vector", last_sum_bank(3), 0, 2)

        job("gpsimd", ("angles are near zero",), [("turns are off",)], bring_near_zero)
        for piece in range(len(cast_pieces(2))):
            job_cast(2, piece)

        def rotate_on_gpsimd(pair, half):
            if product_on_gpsimd(pair, half):
                job_product("gpsimd", sum_bank(pair, half))
            job_sum("gpsimd", sum_bank(pair, half), 0, 4 - vector_heads(pair, half))

        for key, banks in [("x1", [(0, 0)]), (2, [(1, 0), (0, 1)]), (3, [(2, 0), (1, 1), (2, 1)])] + \
                [(i + 1, [(i, 0), (i, 1)]) for i in range(3, LAST - 1)]:
            job_fence(key)
            for pair, half in banks:
                rotate_on_gpsimd(pair, half)
        job_fence(LAST, 2)
        for half in range(2):
            rotate_on_gpsimd(LAST - 1, half)
        job_sum("gpsimd", last_sum_bank(0), 0, 2)
        job_sum("gpsimd", last_sum_bank(1), 0, 2)

        for k in range(PASSES):
            job_transpose_w(k)
            job_transpose_x(k)
        job_transpose_w(4)
        job_transpose_x(4)
        job_transpose_w(5)
        job_transpose_x(5)
        job_transpose_w(6)
        job_transpose_w(7)
        job_transpose_x(6)
        job_matmuls(sum_bank(0, 0), 0)
        job_transpose_w(8)
        job_matmuls(sum_bank(0, 0), 1)
        job_transpose_x(7)
        next_bank = 9
        for k in range(7, BANKS + PASSES):
            for bank in range(next_bank, min(k + TENSOR_AHEAD, BANKS - 1) + 1):
                job_transpose_w(bank)
                next_bank = bank + 1
            i, b = divmod(k, PASSES)
            if 2 <= i <= LAST:
                job_matmuls(sum_bank(i - 1, b // 2), b)
            if i == 2 and b < 2:
                job_matmuls(sum_bank(0, 1), 2 + b)
        for g0 in (0, 2):
            for b in range(B):
                job_matmuls(last_sum_bank(b), b, g0, g0 + 2)

        job_cast_first("scalar", 2)
        job_cast_first("scalar", 3)
        job_cast(1, 0)
        job_cast(1, 1)
        for k in range(VECTOR_X_BANKS, 6):
            job_empty_x("scalar", k)
        job_cast(3, 0)
        job_empty_x("scalar", 6)
        job_empty_x("scalar", 7)
        job("scalar", ("table",), [("angles are near zero",)], make_table)
        for k in range(PASSES + 2, BANKS):
            i, g = divmod(k, PASSES)
            if k + SCALAR_AHEAD < BANKS and by_scalar(k + SCALAR_AHEAD):
                job_scalar_scale(k + SCALAR_AHEAD)
            if g == 2:
                if product_on_gpsimd(i - 1, 0):
                    job_copy_sums(sum_bank(i - 1, 0))
                if i + CAST_AHEAD < PAIRS:
                    job_cast(i + CAST_AHEAD, 0)

        merge()
